import numpy as np
import ml_dtypes


def mxq(x, axis, fmt="e4m3"):
    dtype, down = {"e4m3": (ml_dtypes.float8_e4m3fn, 7), "e5m2": (ml_dtypes.float8_e5m2, 14)}[fmt]
    v = np.moveaxis(np.asarray(x, np.float32).astype(ml_dtypes.bfloat16).astype(np.float64), axis, -1)
    blocks = v.reshape(v.shape[:-1] + (-1, 32))
    amax = np.abs(blocks).max(-1, keepdims=True)
    byte = np.maximum(np.where(amax > 0, np.frexp(amax)[1] - 1 + 127, 0) - down, 1)
    scale = np.exp2(byte - 127.0)
    codes = (blocks / scale).astype(np.float32).astype(dtype).astype(np.float64)
    return np.moveaxis((codes * scale).reshape(v.shape), -1, axis)


WIDE = False


def mx_kscale(k):
    if not WIDE:
        return np.ones(k)
    levels = np.array([10, -10, 5, -5, 0])
    a = np.random.permutation(np.resize(levels, k // 512 * 4)).reshape(k // 512, 4)
    idx = np.arange(k)
    return np.exp2(a[idx // 512, idx % 128 // 32])


BF16 = ml_dtypes.bfloat16


def bf(x):
    return np.asarray(x, np.float32).astype(BF16)


def f64(x):
    return np.asarray(x).astype(np.float64)


E2M1 = np.array([0.0, 0.5, 1.0, 1.5, 2.0, 3.0, 4.0, 6.0, -0.0, -0.5, -1.0, -1.5, -2.0, -3.0, -4.0, -6.0])


def pack_weight(w, fmt):
    k, n = w.shape
    w = f64(bf(w)).reshape(k // 32, 32, n)
    amax = np.abs(w).max(1)
    if fmt == "e4m3":
        byte = np.frexp(amax)[1] - 1 + 127 - 7
    else:
        mant, ex = np.frexp(amax / 6.0)
        byte = np.where(mant > 0.5, ex, ex - 1) + 127
    byte = np.clip(np.where(amax > 0, byte, 1), 1, 254)
    scaled = (w * np.exp2(127.0 - byte)[:, None, :]).reshape(k, n).astype(np.float32)
    by_word = np.ascontiguousarray(scaled.reshape(k // 512, 128, 4, n).transpose(0, 1, 3, 2))
    if fmt == "e4m3":
        words = by_word.astype(ml_dtypes.float8_e4m3fn).view(np.uint8)
    else:
        c = by_word.astype(ml_dtypes.float4_e2m1fn).view(np.uint8) & 0xF
        words = c[..., 0::2] | (c[..., 1::2] << 4)
    return np.ascontiguousarray(words), np.ascontiguousarray(byte.astype(np.uint8).reshape(k // 512, 16, n))


def unpack_weight(words, scales, fmt):
    g, p, n, _ = words.shape
    if fmt == "e4m3":
        vals = np.ascontiguousarray(words).view(ml_dtypes.float8_e4m3fn).astype(np.float64)
    else:
        nib = np.empty((g, p, n, 4), np.uint8)
        nib[..., 0::2] = words & 0xF
        nib[..., 1::2] = words >> 4
        vals = E2M1[nib]
    vals = vals * np.repeat(np.exp2(scales.astype(np.float64) - 127.0), 8, axis=1)[..., None]
    return vals.transpose(0, 1, 3, 2).reshape(g * 512, n)


B, IN, OUT, G, P = 512, 1024, 1024, 5, 3
NB = G + P
LO, HI = -1.0, 1.0


def silu(v):
    return v / (1.0 + np.exp(-v))


def b_splines(x, grid):
    xe = x[..., None]
    bases = np.logical_and(xe >= grid[:, :-1], xe < grid[:, 1:]).astype(np.float64)
    for k in range(1, P + 1):
        left = (xe - grid[:, :-(k + 1)]) / (grid[:, k:-1] - grid[:, :-(k + 1)])
        right = (grid[:, k + 1:] - xe) / (grid[:, k + 1:] - grid[:, 1:-k])
        bases = left * bases[..., :-1] + right * bases[..., 1:]
    return bases


def setup_inputs():
    s = mx_kscale(IN)
    s = s / s.max()
    h = (HI - LO) / G
    g = np.arange(-P, G + P + 1) * h + LO
    x = bf(np.random.uniform(LO, HI, (B, IN)) * s)
    base = np.random.standard_normal((OUT, IN)) * 2.5 / np.sqrt(IN) / s[None, :]
    words, scales = pack_weight(np.ascontiguousarray(base.T), "e4m3")
    return {"x": x,
            "base_weight_words": words,
            "base_weight_scales": scales,
            "spline_weight": bf(np.random.standard_normal((OUT, IN, NB))),
            "spline_scaler": bf(np.random.standard_normal((OUT, IN)) * 1.5 / np.sqrt(IN)),
            "grid": bf(np.tile(g[None, :], (IN, 1)))}


def reference(x, base_weight_words, base_weight_scales, spline_weight, spline_scaler, grid):
    x, grid = f64(x), f64(grid)
    base_out = mxq(silu(x), 1, "e4m3") @ unpack_weight(base_weight_words, base_weight_scales, "e4m3")
    ssw = f64(spline_weight) * f64(spline_scaler)[..., None]
    bs = b_splines(x, grid).reshape(x.shape[0], -1)
    spline_out = mxq(bs, 1, "e4m3") @ mxq(ssw.reshape(OUT, -1), 1, "e4m3").T
    return base_out + spline_out

@@ -1,0 +1,332 @@
+import concourse.mybir as mybir
+from concourse.masks import make_identity
+
+F32 = mybir.dt.float32
+BF16 = mybir.dt.bfloat16
+U32 = mybir.dt.uint32
+U8 = mybir.dt.uint8
+I32 = mybir.dt.int32
+FP8X4 = mybir.dt.float8_e4m3fn_x4
+ALU = mybir.AluOpType
+ACT = mybir.ActivationFunctionType
+
+P = 128
+PACK = 4
+BATCH = 512
+N_IN = 1024
+N_OUT = 1024
+N_BASIS = 8
+N_KNOTS = 12
+HALVES = N_BASIS // PACK
+B_TILES = BATCH // P
+F_TILES = N_IN // P
+O_TILES = N_OUT // P
+BASE_PASSES = N_IN // (P * PACK)
+SPLINE_PASSES = F_TILES * HALVES
+N_TILE = 512
+N_TILES = N_OUT // N_TILE
+
+FLOPS = 2 * BATCH * N_OUT * (N_IN + N_IN * N_BASIS)
+
+
+def spline_constants(nc, consts, grid):
+    knot_bf = consts.tile([P, F_TILES, N_KNOTS], BF16)
+    nc.sync.dma_start(out=knot_bf[:], in_=grid.rearrange("(c p) m -> p c m", p=P))
+    knot = consts.tile([P, F_TILES, N_KNOTS], F32)
+    nc.vector.tensor_copy(out=knot[:], in_=knot_bf[:])
+    neg_knot = consts.tile([P, F_TILES, N_KNOTS], F32)
+    nc.vector.tensor_scalar_mul(out=neg_knot[:], in0=knot[:], scalar1=-1.0)
+
+    def span(width):
+        count = N_KNOTS - width
+        h = consts.tile([P, F_TILES, count], F32, name="span%d" % width)
+        nc.vector.tensor_sub(out=h[:], in0=knot[:, :, width:], in1=knot[:, :, :count])
+        return h
+
+    h1, h2, h3, h4 = span(1), span(2), span(3), span(4)
+
+    def inverse_product(name, factors):
+        prod = consts.tile([P, F_TILES, N_BASIS], F32, name=name)
+        nc.vector.tensor_mul(out=prod[:], in0=factors[0], in1=factors[1])
+        for factor in factors[2:]:
+            nc.vector.tensor_mul(out=prod[:], in0=prod[:], in1=factor)
+        nc.vector.reciprocal(out=prod[:], in_=prod[:])
+        return prod
+
+    first_left = inverse_product("first_left", [h1[:, :, 0:8], h2[:, :, 0:8], h3[:, :, 0:8]])
+    first_right = inverse_product("first_right", [h1[:, :, 3:11], h2[:, :, 2:10], h3[:, :, 1:9]])
+    second_left = inverse_product(
+        "second_left", [h1[:, :, 0:8], h1[:, :, 1:9], h2[:, :, 1:9], h3[:, :, 1:9]]
+    )
+    second_right = inverse_product(
+        "second_right", [h3[:, :, 0:8], h2[:, :, 1:9], h1[:, :, 2:10], h1[:, :, 3:11]]
+    )
+
+    up_scale = consts.tile([P, F_TILES, N_BASIS + 1], F32)
+    nc.vector.tensor_copy(out=up_scale[:, :, 0:1], in_=first_left[:, :, 0:1])
+    nc.vector.tensor_mul(out=up_scale[:, :, 1:9], in0=second_left[:], in1=h4[:])
+    down_scale = consts.tile([P, F_TILES, N_BASIS + 1], F32)
+    nc.vector.tensor_mul(out=down_scale[:, :, 0:8], in0=second_right[:], in1=h4[:])
+    nc.vector.tensor_copy(out=down_scale[:, :, 8:9], in_=first_right[:, :, 7:8])
+
+    left_mix = consts.tile([P, F_TILES, N_BASIS], F32)
+    nc.vector.reciprocal(out=left_mix[:], in_=up_scale[:, :, 0:8])
+    nc.vector.tensor_mul(out=left_mix[:], in0=left_mix[:], in1=first_left[:])
+    right_mix = consts.tile([P, F_TILES, N_BASIS], F32)
+    nc.vector.reciprocal(out=right_mix[:], in_=down_scale[:, :, 1:9])
+    nc.vector.tensor_mul(out=right_mix[:], in0=right_mix[:], in1=first_right[:])
+
+    neg_down_scale = consts.tile([P, F_TILES, N_BASIS + 1], F32)
+    nc.vector.tensor_scalar_mul(out=neg_down_scale[:], in0=down_scale[:], scalar1=-1.0)
+    return knot, neg_knot, up_scale, neg_down_scale, left_mix, right_mix
+
+
+def tile_bsplinekanlayer_kernel(
+    tc, x, base_weight_words, base_weight_scales, spline_weight, spline_scaler, grid, out
+):
+    nc = tc.nc
+    with (
+        tc.tile_pool(name="consts", bufs=1) as consts,
+        tc.tile_pool(name="keep", bufs=1) as keep,
+    ):
+        knot, neg_knot, up_scale, neg_down_scale, left_mix, right_mix = spline_constants(
+            nc, consts, grid
+        )
+        ident_bf = consts.tile([P, P], BF16)
+        make_identity(nc, ident_bf[:])
+        ident_f32 = consts.tile([P, P], F32)
+        make_identity(nc, ident_f32[:])
+
+        x_by_feature = keep.tile([P, F_TILES, BATCH], BF16)
+        silu_codes = keep.tile([P, BASE_PASSES, BATCH], U32, align_bytes=64)
+        silu_scales = keep.tile([P, BASE_PASSES, BATCH], U8, align_bytes=64)
+        w_codes = keep.tile([P, BASE_PASSES, N_OUT], U32, align_bytes=64)
+        w_scales = keep.tile([P, BASE_PASSES, N_OUT], U8, align_bytes=64)
+        ssw_codes = keep.tile([P, SPLINE_PASSES, N_OUT], U32, align_bytes=64)
+        ssw_scales = keep.tile([P, SPLINE_PASSES, N_OUT], U8, align_bytes=64)
+
+        with (
+            tc.tile_pool(name="early", bufs=1) as early,
+            tc.tile_pool(name="slabs", bufs=2) as slabs,
+            tc.tile_pool(name="prep", bufs=2) as prep,
+            tc.psum_pool(name="psum_flip", bufs=8) as psum_flip,
+        ):
+            x_rows = early.tile([P, B_TILES, N_IN], BF16)
+            nc.sync.dma_start(out=x_rows[:], in_=x.rearrange("(s p) i -> p s i", p=P))
+            scaler_rows = early.tile([P, O_TILES, N_IN], BF16)
+            nc.sync.dma_start(
+                out=scaler_rows[:], in_=spline_scaler.rearrange("(s p) i -> p s i", p=P)
+            )
+
+            for pair in range(F_TILES // 2):
+                flipped = psum_flip.tile([P, 2, BATCH], BF16, tag="flip")
+                for c in range(2):
+                    for s in range(B_TILES):
+                        nc.tensor.transpose(
+                            flipped[:, c, s * P : (s + 1) * P],
+                            x_rows[:, s, (2 * pair + c) * P : (2 * pair + c + 1) * P],
+                            ident_bf[:],
+                        )
+                nc.scalar.copy(out=x_by_feature[:, 2 * pair : 2 * pair + 2, :], in_=flipped[:])
+
+            silu_grouped = early.tile([P, BASE_PASSES, BATCH, PACK], BF16, align_bytes=64)
+            for g in range(BASE_PASSES):
+                for pair in range(B_TILES // 2):
+                    words = psum_flip.tile([P, 2, 2, P], F32, tag="flip")
+                    for u in range(2):
+                        for s in range(2):
+                            nc.tensor.transpose(
+                                words[:, u, s, :],
+                                x_rows[:, 2 * pair + s, :].bitcast(F32)[
+                                    :, 256 * g + u : 256 * (g + 1) : 2
+                                ],
+                                ident_f32[:],
+                            )
+                    nc.scalar.activation(
+                        out=silu_grouped[:, g, 2 * pair * P : 2 * (pair + 1) * P, :].rearrange(
+                            "p b (u e) -> p b u e", e=2
+                        ),
+                        in_=words[:].bitcast(BF16).rearrange("p u s (b e) -> p (s b) u e", e=2),
+                        func=ACT.Silu,
+                    )
+            nc.vector.quantize_mx(
+                out=silu_codes[:].rearrange("p g b -> p (g b)").bitcast(FP8X4),
+                scales=silu_scales[:].rearrange("p g b -> p (g b)"),
+                in_=silu_grouped[:].rearrange("p g b t -> p (g b t)"),
+            )
+
+            for c in range(F_TILES):
+                f_cols = slice(c * P, (c + 1) * P)
+                slab = slabs.tile([P, O_TILES, P * N_BASIS], BF16)
+                nc.sync.dma_start(
+                    out=slab[:],
+                    in_=spline_weight[:, f_cols, :].rearrange("(s p) i j -> p s (i j)", p=P),
+                )
+                scaler_flipped = psum_flip.tile([P, N_OUT], BF16, tag="flip")
+                for s in range(O_TILES):
+                    nc.tensor.transpose(
+                        scaler_flipped[:, s * P : (s + 1) * P], scaler_rows[:, s, f_cols], ident_bf[:]
+                    )
+                scaler_pairs = prep.tile([P, N_OUT, 2], BF16)
+                nc.scalar.copy(
+                    out=scaler_pairs[:],
+                    in_=scaler_flipped[:].unsqueeze(2).to_broadcast([P, N_OUT, 2]),
+                )
+                ssw_grouped = prep.tile([P, HALVES, N_OUT, PACK], BF16, align_bytes=64)
+                for s in range(O_TILES):
+                    o_cols = slice(s * P, (s + 1) * P)
+                    slab_words = slab[:, s, :].bitcast(F32)
+                    words = psum_flip.tile([P, PACK, P], F32, tag="flip")
+                    for w in range(PACK):
+                        nc.tensor.transpose(
+                            words[:, w, :], slab_words[:, w : PACK * P : PACK], ident_f32[:]
+                        )
+                    by_half = words[:].bitcast(BF16).rearrange(
+                        "p (h u) (o e) -> p h o u e", u=2, e=2
+                    )
+                    for half in range(HALVES):
+                        nc.vector.tensor_tensor(
+                            out=ssw_grouped[:, half, o_cols, :].rearrange(
+                                "p o (u e) -> p o u e", e=2
+                            ),
+                            in0=by_half[:, half],
+                            in1=scaler_pairs[:, o_cols, :].unsqueeze(2).to_broadcast([P, P, 2, 2]),
+                            op=ALU.mult,
+                        )
+                for half in range(HALVES):
+                    nc.vector.quantize_mx(
+                        out=ssw_codes[:, c * HALVES + half, :].bitcast(FP8X4),
+                        scales=ssw_scales[:, c * HALVES + half, :],
+                        in_=ssw_grouped[:, half].rearrange("p o t -> p (o t)"),
+                    )
+
+            nc.vector.memset(w_scales[:].bitcast(I32), 0)
+            for quadrant in range(4):
+                nc.sync.dma_start(
+                    out=w_scales[32 * quadrant : 32 * quadrant + 4, :, :].bitcast(I32),
+                    in_=base_weight_scales[:, 4 * quadrant : 4 * quadrant + 4, :]
+                    .rearrange("g r n -> r g n")
+                    .bitcast(I32),
+                )
+            for g in range(BASE_PASSES):
+                nc.sync.dma_start(
+                    out=w_codes[:, g, :].bitcast(I32),
+                    in_=base_weight_words[g].rearrange("p n t -> p (n t)").bitcast(I32),
+                )
+
+        with (
+            tc.tile_pool(name="cubes", bufs=3) as cubes,
+            tc.tile_pool(name="sided", bufs=4) as sided,
+            tc.tile_pool(name="forms", bufs=2) as forms,
+            tc.tile_pool(name="results", bufs=4) as results,
+            tc.psum_pool(name="psum_acc", bufs=1) as psum_acc,
+        ):
+            groups = [(s, n) for s in range(B_TILES) for n in range(N_TILES)]
+            acc = {}
+            for s, n in groups:
+                acc[(s, n)] = psum_acc.tile([P, N_TILE], F32, name="acc_%d_%d" % (s, n))
+                for g in range(BASE_PASSES):
+                    nc.tensor.matmul_mx(
+                        out=acc[(s, n)][:],
+                        lhsT=silu_codes[:, g, s * P : (s + 1) * P].bitcast(FP8X4),
+                        lhsT_scale=silu_scales[:, g, s * P : (s + 1) * P],
+                        rhs=w_codes[:, g, n * N_TILE : (n + 1) * N_TILE].bitcast(FP8X4),
+                        rhs_scale=w_scales[:, g, n * N_TILE : (n + 1) * N_TILE],
+                        start=(g == 0),
+                        stop=False,
+                    )
+
+            for c in range(F_TILES):
+                v = x_by_feature[:, c, :]
+                left = forms.tile([P, N_BASIS, BATCH], BF16)
+                right = forms.tile([P, N_BASIS, BATCH], BF16)
+                up = {}
+                down = {}
+                for m in range(N_KNOTS):
+                    square = cubes.tile([P, BATCH], F32)
+                    nc.scalar.activation(
+                        out=square[:], in_=v, func=ACT.Square, bias=neg_knot[:, c, m : m + 1]
+                    )
+                    cube = cubes.tile([P, BATCH], F32)
+                    nc.vector.scalar_tensor_tensor(
+                        out=cube[:],
+                        in0=v,
+                        scalar=knot[:, c, m : m + 1],
+                        in1=square[:],
+                        op0=ALU.subtract,
+                        op1=ALU.mult,
+                    )
+                    if m <= N_BASIS:
+                        up_m = sided.tile([P, BATCH], F32)
+                        nc.scalar.activation(
+                            out=up_m[:], in_=cube[:], func=ACT.Relu, scale=up_scale[:, c, m : m + 1]
+                        )
+                        up[m] = up_m
+                    if m >= 3:
+                        down_m = sided.tile([P, BATCH], F32)
+                        nc.scalar.activation(
+                            out=down_m[:],
+                            in_=cube[:],
+                            func=ACT.Relu,
+                            scale=neg_down_scale[:, c, m - 3 : m - 2],
+                        )
+                        down[m] = down_m
+                    if 1 <= m <= N_BASIS:
+                        j = m - 1
+                        nc.vector.scalar_tensor_tensor(
+                            out=left[:, j, :],
+                            in0=up[j][:],
+                            scalar=left_mix[:, c, j : j + 1],
+                            in1=up[j + 1][:],
+                            op0=ALU.mult,
+                            op1=ALU.subtract,
+                        )
+                    if m >= 4:
+                        j = m - 4
+                        nc.vector.scalar_tensor_tensor(
+                            out=right[:, j, :],
+                            in0=down[j + 4][:],
+                            scalar=right_mix[:, c, j : j + 1],
+                            in1=down[j + 3][:],
+                            op0=ALU.mult,
+                            op1=ALU.subtract,
+                        )
+                grouped = forms.tile([P, HALVES, BATCH, PACK], BF16, align_bytes=64)
+                for half in range(HALVES):
+                    planes = slice(half * PACK, (half + 1) * PACK)
+                    nc.vector.tensor_tensor(
+                        out=grouped[:, half, :, :],
+                        in0=left[:, planes, :].rearrange("p t b -> p b t"),
+                        in1=right[:, planes, :].rearrange("p t b -> p b t"),
+                        op=ALU.max,
+                    )
+                basis_codes = forms.tile([P, HALVES, BATCH], U32, align_bytes=64)
+                basis_scales = forms.tile([P, HALVES, BATCH], U8, align_bytes=64)
+                nc.vector.quantize_mx(
+                    out=basis_codes[:].rearrange("p h b -> p (h b)").bitcast(FP8X4),
+                    scales=basis_scales[:].rearrange("p h b -> p (h b)"),
+                    in_=grouped[:].rearrange("p h b t -> p (h b t)"),
+                )
+                for s, n in groups:
+                    for half in range(HALVES):
+                        nc.tensor.matmul_mx(
+                            out=acc[(s, n)][:],
+                            lhsT=basis_codes[:, half, s * P : (s + 1) * P].bitcast(FP8X4),
+                            lhsT_scale=basis_scales[:, half, s * P : (s + 1) * P],
+                            rhs=ssw_codes[
+                                :, c * HALVES + half, n * N_TILE : (n + 1) * N_TILE
+                            ].bitcast(FP8X4),
+                            rhs_scale=ssw_scales[:, c * HALVES + half, n * N_TILE : (n + 1) * N_TILE],
+                            start=False,
+                            stop=(c == F_TILES - 1 and half == HALVES - 1),
+                        )
+
+            for index, (s, n) in enumerate(groups):
+                result = results.tile([P, N_TILE], F32)
+                if index % 2 == 0:
+                    nc.scalar.copy(out=result[:], in_=acc[(s, n)][:])
+                else:
+                    nc.vector.tensor_copy(out=result[:], in_=acc[(s, n)][:])
+                nc.sync.dma_start(
+                    out=out[s * P : (s + 1) * P, n * N_TILE : (n + 1) * N_TILE], in_=result[:]
+                )

@@ -88,6 +88,8 @@ def tile_bsplinekanlayer_kernel(
     with (
         tc.tile_pool(name="consts", bufs=1) as consts,
         tc.tile_pool(name="keep", bufs=1) as keep,
+        tc.tile_pool(name="cubes", bufs=4) as cubes,
+        tc.tile_pool(name="sided", bufs=6) as sided,
     ):
         knot, neg_knot, up_scale, neg_down_scale, left_mix, right_mix = spline_constants(
             nc, consts, grid
@@ -111,68 +113,71 @@ def tile_bsplinekanlayer_kernel(
             tc.tile_pool(name="prep", bufs=2) as prep,
             tc.psum_pool(name="psum_flip", bufs=8) as psum_flip,
         ):
-            x_rows = early.tile([P, B_TILES, N_IN], BF16)
-            nc.sync.dma_start(out=x_rows[:], in_=x.rearrange("(s p) i -> p s i", p=P))
-            scaler_rows = early.tile([P, O_TILES, N_IN], BF16)
-            nc.sync.dma_start(
-                out=scaler_rows[:], in_=spline_scaler.rearrange("(s p) i -> p s i", p=P)
-            )
 
-            for pair in range(F_TILES // 2):
-                flipped = psum_flip.tile([P, 2, BATCH], BF16, tag="flip")
-                for c in range(2):
-                    for s in range(B_TILES):
-                        nc.tensor.transpose(
-                            flipped[:, c, s * P : (s + 1) * P],
-                            x_rows[:, s, (2 * pair + c) * P : (2 * pair + c + 1) * P],
-                            ident_bf[:],
-                        )
-                nc.scalar.copy(out=x_by_feature[:, 2 * pair : 2 * pair + 2, :], in_=flipped[:])
-
-            silu_grouped = early.tile([P, BASE_PASSES, BATCH, PACK], BF16, align_bytes=64)
-            for g in range(BASE_PASSES):
-                for pair in range(B_TILES // 2):
-                    words = psum_flip.tile([P, 2, 2, P], F32, tag="flip")
-                    for u in range(2):
-                        for s in range(2):
-                            nc.tensor.transpose(
-                                words[:, u, s, :],
-                                x_rows[:, 2 * pair + s, :].bitcast(F32)[
-                                    :, 256 * g + u : 256 * (g + 1) : 2
-                                ],
-                                ident_f32[:],
-                            )
-                    nc.scalar.activation(
-                        out=silu_grouped[:, g, 2 * pair * P : 2 * (pair + 1) * P, :].rearrange(
-                            "p b (u e) -> p b u e", e=2
-                        ),
-                        in_=words[:].bitcast(BF16).rearrange("p u s (b e) -> p (s b) u e", e=2),
-                        func=ACT.Silu,
-                    )
-            nc.vector.quantize_mx(
-                out=silu_codes[:].rearrange("p g b -> p (g b)").bitcast(FP8X4),
-                scales=silu_scales[:].rearrange("p g b -> p (g b)"),
-                in_=silu_grouped[:].rearrange("p g b t -> p (g b t)"),
-            )
-
-            for c in range(F_TILES):
+            def load_feature_tile(c):
                 f_cols = slice(c * P, (c + 1) * P)
-                slab = slabs.tile([P, O_TILES, P * N_BASIS], BF16)
+                scaler_rows = slabs.tile([P, O_TILES, P], BF16)
                 nc.sync.dma_start(
-                    out=slab[:],
-                    in_=spline_weight[:, f_cols, :].rearrange("(s p) i j -> p s (i j)", p=P),
+                    out=scaler_rows[:],
+                    in_=spline_scaler[:, f_cols].rearrange("(s p) i -> p s i", p=P),
                 )
+                slab = slabs.tile([P, O_TILES, P * N_BASIS], BF16)
+                rows = spline_weight[:, f_cols, :].rearrange("(s p) i j -> p s (i j)", p=P)
+                for part in (slice(0, O_TILES // 2), slice(O_TILES // 2, O_TILES)):
+                    nc.sync.dma_start(out=slab[:, part, :], in_=rows[:, part, :])
+                return scaler_rows, slab
+
+
+            def prepare_x():
+                for pair in range(F_TILES // 2):
+                    flipped = psum_flip.tile([P, 2, BATCH], BF16, tag="flip")
+                    for c in range(2):
+                        for s in range(B_TILES):
+                            nc.tensor.transpose(
+                                flipped[:, c, s * P : (s + 1) * P],
+                                x_rows[:, s, (2 * pair + c) * P : (2 * pair + c + 1) * P],
+                                ident_bf[:],
+                            )
+                    nc.scalar.copy(out=x_by_feature[:, 2 * pair : 2 * pair + 2, :], in_=flipped[:])
+
+                silu_grouped = early.tile([P, BASE_PASSES, BATCH, PACK], BF16, align_bytes=64)
+                for g in range(BASE_PASSES):
+                    for pair in range(B_TILES // 2):
+                        words = psum_flip.tile([P, 2, 2, P], F32, tag="flip")
+                        for u in range(2):
+                            for s in range(2):
+                                nc.tensor.transpose(
+                                    words[:, u, s, :],
+                                    x_rows[:, 2 * pair + s, :].bitcast(F32)[
+                                        :, 256 * g + u : 256 * (g + 1) : 2
+                                    ],
+                                    ident_f32[:],
+                                )
+                        nc.scalar.activation(
+                            out=silu_grouped[:, g, 2 * pair * P : 2 * (pair + 1) * P, :].rearrange(
+                                "p b (u e) -> p b u e", e=2
+                            ),
+                            in_=words[:].bitcast(BF16).rearrange("p u s (b e) -> p (s b) u e", e=2),
+                            func=ACT.Silu,
+                        )
+                nc.vector.quantize_mx(
+                    out=silu_codes[:].rearrange("p g b -> p (g b)").bitcast(FP8X4),
+                    scales=silu_scales[:].rearrange("p g b -> p (g b)"),
+                    in_=silu_grouped[:].rearrange("p g b t -> p (g b t)"),
+                )
+
+            def quantise_ssw_tile(c, scaler_rows, slab):
                 scaler_flipped = psum_flip.tile([P, N_OUT], BF16, tag="flip")
                 for s in range(O_TILES):
                     nc.tensor.transpose(
-                        scaler_flipped[:, s * P : (s + 1) * P], scaler_rows[:, s, f_cols], ident_bf[:]
+                        scaler_flipped[:, s * P : (s + 1) * P], scaler_rows[:, s, :], ident_bf[:]
                     )
                 scaler_pairs = prep.tile([P, N_OUT, 2], BF16)
                 nc.scalar.copy(
                     out=scaler_pairs[:],
                     in_=scaler_flipped[:].unsqueeze(2).to_broadcast([P, N_OUT, 2]),
                 )
-                ssw_grouped = prep.tile([P, HALVES, N_OUT, PACK], BF16, align_bytes=64)
+                ssw_grouped = early.tile([P, HALVES, N_OUT, PACK], BF16, align_bytes=64)
                 for s in range(O_TILES):
                     o_cols = slice(s * P, (s + 1) * P)
                     slab_words = slab[:, s, :].bitcast(F32)
@@ -200,6 +205,16 @@ def tile_bsplinekanlayer_kernel(
                         in_=ssw_grouped[:, half].rearrange("p o t -> p (o t)"),
                     )
 
+            arrived = load_feature_tile(0)
+            x_rows = early.tile([P, B_TILES, N_IN], BF16)
+            nc.sync.dma_start(out=x_rows[:], in_=x.rearrange("(s p) i -> p s i", p=P))
+            for c in range(F_TILES):
+                coming = load_feature_tile(c + 1) if c + 1 < F_TILES else None
+                quantise_ssw_tile(c, arrived[0], arrived[1])
+                if c == 0:
+                    prepare_x()
+                arrived = coming
+
             nc.vector.memset(w_scales[:].bitcast(I32), 0)
             for quadrant in range(4):
                 nc.sync.dma_start(
@@ -215,8 +230,6 @@ def tile_bsplinekanlayer_kernel(
                 )
 
         with (
-            tc.tile_pool(name="cubes", bufs=3) as cubes,
-            tc.tile_pool(name="sided", bufs=4) as sided,
             tc.tile_pool(name="forms", bufs=2) as forms,
             tc.tile_pool(name="results", bufs=4) as results,
             tc.psum_pool(name="psum_acc", bufs=1) as psum_acc,
@@ -234,6 +247,41 @@ def tile_bsplinekanlayer_kernel(
                         rhs_scale=w_scales[:, g, n * N_TILE : (n + 1) * N_TILE],
                         start=(g == 0),
                         stop=False,
+                    )
+
+            def finish_half(c, half, left, right):
+                planes = slice(half * PACK, (half + 1) * PACK)
+                grouped = forms.tile([P, BATCH, PACK], BF16, align_bytes=64)
+                if half == 0:
+                    peak = forms.tile([P, PACK, BATCH], BF16)
+                    nc.vector.tensor_tensor(
+                        out=peak[:], in0=left[:, planes, :], in1=right[:, planes, :], op=ALU.max
+                    )
+                    nc.scalar.copy(out=grouped[:], in_=peak[:].rearrange("p t b -> p b t"))
+                else:
+                    nc.vector.tensor_tensor(
+                        out=grouped[:],
+                        in0=left[:, planes, :].rearrange("p t b -> p b t"),
+                        in1=right[:, planes, :].rearrange("p t b -> p b t"),
+                        op=ALU.max,
+                    )
+                basis_codes = forms.tile([P, BATCH], U32, align_bytes=64)
+                basis_scales = forms.tile([P, BATCH], U8, align_bytes=64)
+                nc.vector.quantize_mx(
+                    out=basis_codes[:].bitcast(FP8X4),
+                    scales=basis_scales[:],
+                    in_=grouped[:].rearrange("p b t -> p (b t)"),
+                )
+                k = c * HALVES + half
+                for s, n in groups:
+                    nc.tensor.matmul_mx(
+                        out=acc[(s, n)][:],
+                        lhsT=basis_codes[:, s * P : (s + 1) * P].bitcast(FP8X4),
+                        lhsT_scale=basis_scales[:, s * P : (s + 1) * P],
+                        rhs=ssw_codes[:, k, n * N_TILE : (n + 1) * N_TILE].bitcast(FP8X4),
+                        rhs_scale=ssw_scales[:, k, n * N_TILE : (n + 1) * N_TILE],
+                        start=False,
+                        stop=(k == SPLINE_PASSES - 1),
                     )
 
             for c in range(F_TILES):
@@ -291,35 +339,9 @@ def tile_bsplinekanlayer_kernel(
                             op0=ALU.mult,
                             op1=ALU.subtract,
                         )
-                grouped = forms.tile([P, HALVES, BATCH, PACK], BF16, align_bytes=64)
-                for half in range(HALVES):
-                    planes = slice(half * PACK, (half + 1) * PACK)
-                    nc.vector.tensor_tensor(
-                        out=grouped[:, half, :, :],
-                        in0=left[:, planes, :].rearrange("p t b -> p b t"),
-                        in1=right[:, planes, :].rearrange("p t b -> p b t"),
-                        op=ALU.max,
-                    )
-                basis_codes = forms.tile([P, HALVES, BATCH], U32, align_bytes=64)
-                basis_scales = forms.tile([P, HALVES, BATCH], U8, align_bytes=64)
-                nc.vector.quantize_mx(
-                    out=basis_codes[:].rearrange("p h b -> p (h b)").bitcast(FP8X4),
-                    scales=basis_scales[:].rearrange("p h b -> p (h b)"),
-                    in_=grouped[:].rearrange("p h b t -> p (h b t)"),
-                )
-                for s, n in groups:
-                    for half in range(HALVES):
-                        nc.tensor.matmul_mx(
-                            out=acc[(s, n)][:],
-                            lhsT=basis_codes[:, half, s * P : (s + 1) * P].bitcast(FP8X4),
-                            lhsT_scale=basis_scales[:, half, s * P : (s + 1) * P],
-                            rhs=ssw_codes[
-                                :, c * HALVES + half, n * N_TILE : (n + 1) * N_TILE
-                            ].bitcast(FP8X4),
-                            rhs_scale=ssw_scales[:, c * HALVES + half, n * N_TILE : (n + 1) * N_TILE],
-                            start=False,
-                            stop=(c == F_TILES - 1 and half == HALVES - 1),
-                        )
+                    if m == N_KNOTS - 1 - PACK:
+                        finish_half(c, 0, left, right)
+                finish_half(c, 1, left, right)
 
             for index, (s, n) in enumerate(groups):
                 result = results.tile([P, N_TILE], F32)

@@ -1,3 +1,5 @@
+from contextlib import ExitStack
+
 import concourse.mybir as mybir
 from concourse.masks import make_identity
 
@@ -29,9 +31,7 @@ N_TILES = N_OUT // N_TILE
 FLOPS = 2 * BATCH * N_OUT * (N_IN + N_IN * N_BASIS)
 
 
-def spline_constants(nc, consts, grid):
-    knot_bf = consts.tile([P, F_TILES, N_KNOTS], BF16)
-    nc.sync.dma_start(out=knot_bf[:], in_=grid.rearrange("(c p) m -> p c m", p=P))
+def spline_constants(tc, nc, consts, knot_bf):
     knot = consts.tile([P, F_TILES, N_KNOTS], F32)
     nc.vector.tensor_copy(out=knot[:], in_=knot_bf[:])
     neg_knot = consts.tile([P, F_TILES, N_KNOTS], F32)
@@ -81,141 +81,236 @@ def spline_constants(nc, consts, grid):
     return knot, neg_knot, up_scale, neg_down_scale, left_mix, right_mix
 
 
+LOOKAHEAD = 2
+COMBINE_LAG = 2
+PREFETCH = 4
+HALF_O = O_TILES // 2
+CHUNKS = F_TILES * O_TILES
+FIRST_CHUNK_STEP = 3
+EARLY_TILES = 4
+SWITCH = EARLY_TILES * N_KNOTS + 2
+STEPS = F_TILES * N_KNOTS
+
+
 def tile_bsplinekanlayer_kernel(
     tc, x, base_weight_words, base_weight_scales, spline_weight, spline_scaler, grid, out
 ):
     nc = tc.nc
-    with (
-        tc.tile_pool(name="consts", bufs=1) as consts,
-        tc.tile_pool(name="keep", bufs=1) as keep,
-        tc.tile_pool(name="cubes", bufs=4) as cubes,
-        tc.tile_pool(name="sided", bufs=6) as sided,
-    ):
-        knot, neg_knot, up_scale, neg_down_scale, left_mix, right_mix = spline_constants(
-            nc, consts, grid
-        )
+    with ExitStack() as ctx:
+        ctx.enter_context(tc.manual_schedule())
+        consts = ctx.enter_context(tc.tile_pool(name="consts", bufs=1))
+        keep = ctx.enter_context(tc.tile_pool(name="keep", bufs=1))
+        pool = ctx.enter_context(tc.tile_pool(name="work", bufs=1))
+
+        x_rows = pool.tile([P, B_TILES, N_IN], BF16, tag="slab", bufs=PREFETCH, align_bytes=64)
+        x_in = x.rearrange("(s p) i -> p s i", p=P)
+        knot_bf = consts.tile([P, F_TILES, N_KNOTS], BF16)
+        nc.scalar.dma_start(out=knot_bf[:], in_=grid.rearrange("(c p) m -> p c m", p=P))
+        for s in range(B_TILES):
+            nc.sync.dma_start(out=x_rows[:, s, :], in_=x_in[:, s, :])
+
+        scaler_rows = {}
+
+        def load_scaler(c):
+            rows = pool.tile([P, O_TILES, P], BF16, tag="scaler_rows", bufs=2, align_bytes=64)
+            nc.sync.dma_start(
+                out=rows[:],
+                in_=spline_scaler[:, c * P : (c + 1) * P].rearrange("(s p) i -> p s i", p=P),
+            )
+            scaler_rows[c] = rows
+
+        slabs = {}
+
+        def load_slab(c, part):
+            slab = pool.tile([P, HALF_O, P * N_BASIS], BF16, tag="slab", bufs=PREFETCH, align_bytes=64)
+            rows = spline_weight[:, c * P : (c + 1) * P, :].rearrange("(s p) i j -> p s (i j)", p=P)
+            nc.sync.dma_start(out=slab[:], in_=rows[:, part * HALF_O : (part + 1) * HALF_O, :])
+            slabs[(c, part)] = slab
+
+        load_scaler(0)
+        load_slab(0, 0)
+        load_slab(0, 1)
+        load_slab(1, 0)
+        load_scaler(1)
+
+        warm = consts.tile([P, 1], F32)
+        nc.vector.memset(warm[:], 0.0)
+        nc.scalar.activation(out=warm[:], in_=warm[:], func=ACT.Silu)
         ident_bf = consts.tile([P, P], BF16)
         make_identity(nc, ident_bf[:])
         ident_f32 = consts.tile([P, P], F32)
         make_identity(nc, ident_f32[:])
 
+        knot, neg_knot, up_scale, neg_down_scale, left_mix, right_mix = spline_constants(
+            tc, nc, consts, knot_bf
+        )
+
         x_by_feature = keep.tile([P, F_TILES, BATCH], BF16)
         silu_codes = keep.tile([P, BASE_PASSES, BATCH], U32, align_bytes=64)
         silu_scales = keep.tile([P, BASE_PASSES, BATCH], U8, align_bytes=64)
-        w_codes = keep.tile([P, BASE_PASSES, N_OUT], U32, align_bytes=64)
-        w_scales = keep.tile([P, BASE_PASSES, N_OUT], U8, align_bytes=64)
         ssw_codes = keep.tile([P, SPLINE_PASSES, N_OUT], U32, align_bytes=64)
         ssw_scales = keep.tile([P, SPLINE_PASSES, N_OUT], U8, align_bytes=64)
 
-        with (
-            tc.tile_pool(name="early", bufs=1) as early,
-            tc.tile_pool(name="slabs", bufs=2) as slabs,
-            tc.tile_pool(name="prep", bufs=2) as prep,
-            tc.psum_pool(name="psum_flip", bufs=8) as psum_flip,
-        ):
+        square = {}
+        cube = {}
+        up = {}
+        down = {}
+        left = {}
+        right = {}
+        peak = {}
+        grouped = {}
+        codes = {}
 
-            def load_feature_tile(c):
-                f_cols = slice(c * P, (c + 1) * P)
-                scaler_rows = slabs.tile([P, O_TILES, P], BF16)
-                nc.sync.dma_start(
-                    out=scaler_rows[:],
-                    in_=spline_scaler[:, f_cols].rearrange("(s p) i -> p s i", p=P),
+        def take_square(n):
+            c, m = divmod(n, N_KNOTS)
+            square[n] = pool.tile([P, BATCH], F32, tag="square", bufs=3, name="square")
+            nc.scalar.activation(
+                out=square[n][:], in_=x_by_feature[:, c, :], func=ACT.Square,
+                bias=neg_knot[:, c, m : m + 1],
+            )
+
+        def take_cube(n):
+            c, m = divmod(n, N_KNOTS)
+            cube[n] = pool.tile([P, BATCH], F32, tag="cube", bufs=3, name="cube")
+            nc.vector.scalar_tensor_tensor(
+                out=cube[n][:], in0=x_by_feature[:, c, :], scalar=knot[:, c, m : m + 1],
+                in1=square[n][:], op0=ALU.subtract, op1=ALU.mult,
+            )
+
+        def take_sides(n):
+            c, m = divmod(n, N_KNOTS)
+            if m <= N_BASIS:
+                up[n] = pool.tile([P, BATCH], F32, tag="up", bufs=4, name="up")
+                nc.scalar.activation(
+                    out=up[n][:], in_=cube[n][:], func=ACT.Relu, scale=up_scale[:, c, m : m + 1]
                 )
-                slab = slabs.tile([P, O_TILES, P * N_BASIS], BF16)
-                rows = spline_weight[:, f_cols, :].rearrange("(s p) i j -> p s (i j)", p=P)
-                for part in (slice(0, O_TILES // 2), slice(O_TILES // 2, O_TILES)):
-                    nc.sync.dma_start(out=slab[:, part, :], in_=rows[:, part, :])
-                return scaler_rows, slab
-
-
-            def prepare_x():
-                for pair in range(F_TILES // 2):
-                    flipped = psum_flip.tile([P, 2, BATCH], BF16, tag="flip")
-                    for c in range(2):
-                        for s in range(B_TILES):
-                            nc.tensor.transpose(
-                                flipped[:, c, s * P : (s + 1) * P],
-                                x_rows[:, s, (2 * pair + c) * P : (2 * pair + c + 1) * P],
-                                ident_bf[:],
-                            )
-                    nc.scalar.copy(out=x_by_feature[:, 2 * pair : 2 * pair + 2, :], in_=flipped[:])
-
-                silu_grouped = early.tile([P, BASE_PASSES, BATCH, PACK], BF16, align_bytes=64)
-                for g in range(BASE_PASSES):
-                    for pair in range(B_TILES // 2):
-                        words = psum_flip.tile([P, 2, 2, P], F32, tag="flip")
-                        for u in range(2):
-                            for s in range(2):
-                                nc.tensor.transpose(
-                                    words[:, u, s, :],
-                                    x_rows[:, 2 * pair + s, :].bitcast(F32)[
-                                        :, 256 * g + u : 256 * (g + 1) : 2
-                                    ],
-                                    ident_f32[:],
-                                )
-                        nc.scalar.activation(
-                            out=silu_grouped[:, g, 2 * pair * P : 2 * (pair + 1) * P, :].rearrange(
-                                "p b (u e) -> p b u e", e=2
-                            ),
-                            in_=words[:].bitcast(BF16).rearrange("p u s (b e) -> p (s b) u e", e=2),
-                            func=ACT.Silu,
-                        )
-                nc.vector.quantize_mx(
-                    out=silu_codes[:].rearrange("p g b -> p (g b)").bitcast(FP8X4),
-                    scales=silu_scales[:].rearrange("p g b -> p (g b)"),
-                    in_=silu_grouped[:].rearrange("p g b t -> p (g b t)"),
+            if m >= 3:
+                down[n] = pool.tile([P, BATCH], F32, tag="down", bufs=4, name="down")
+                nc.scalar.activation(
+                    out=down[n][:], in_=cube[n][:], func=ACT.Relu,
+                    scale=neg_down_scale[:, c, m - 3 : m - 2],
                 )
 
-            def quantise_ssw_tile(c, scaler_rows, slab):
-                scaler_flipped = psum_flip.tile([P, N_OUT], BF16, tag="flip")
-                for s in range(O_TILES):
-                    nc.tensor.transpose(
-                        scaler_flipped[:, s * P : (s + 1) * P], scaler_rows[:, s, :], ident_bf[:]
-                    )
-                scaler_pairs = prep.tile([P, N_OUT, 2], BF16)
+        def half_tile(store, c, j, tag):
+            key = (c, j // PACK)
+            if key not in store:
+                store[key] = pool.tile([P, PACK, BATCH], BF16, tag=tag, bufs=2, name=tag)
+            return store[key][:, j % PACK, :]
+
+        def combine(n):
+            c, m = divmod(n, N_KNOTS)
+            if 1 <= m <= N_BASIS:
+                j = m - 1
+                nc.vector.scalar_tensor_tensor(
+                    out=half_tile(left, c, j, "left"), in0=up[n - 1][:],
+                    scalar=left_mix[:, c, j : j + 1], in1=up[n][:],
+                    op0=ALU.mult, op1=ALU.subtract,
+                )
+            if m >= 4:
+                j = m - 4
+                nc.vector.scalar_tensor_tensor(
+                    out=half_tile(right, c, j, "right"), in0=down[n][:],
+                    scalar=right_mix[:, c, j : j + 1], in1=down[n - 1][:],
+                    op0=ALU.mult, op1=ALU.subtract,
+                )
+
+        def take_peak(c, half):
+            peak[(c, half)] = pool.tile([P, PACK, BATCH], BF16, tag="peak", bufs=1, name="peak")
+            nc.vector.tensor_tensor(
+                out=peak[(c, half)][:], in0=left[(c, half)][:], in1=right[(c, half)][:], op=ALU.max
+            )
+
+        def regroup(c, half):
+            grouped[(c, half)] = pool.tile(
+                [P, BATCH, PACK], BF16, tag="grouped", bufs=2, align_bytes=64, name="grouped"
+            )
+            nc.scalar.copy(
+                out=grouped[(c, half)][:].rearrange("p (g i) t -> p g t i", i=4),
+                in_=peak[(c, half)][:].rearrange("p t (g i) -> p g t i", i=4),
+            )
+
+        def quantise_half(c, half):
+            k = c * HALVES + half
+            k_codes = pool.tile([P, BATCH], U32, tag="k_codes", bufs=8, align_bytes=64, name="k_codes")
+            k_scales = pool.tile([P, BATCH], U8, tag="k_scales", bufs=8, align_bytes=64, name="k_scales")
+            nc.vector.quantize_mx(
+                out=k_codes[:].bitcast(FP8X4), scales=k_scales[:],
+                in_=grouped[(c, half)][:].rearrange("p b t -> p (b t)"),
+            )
+            codes[k] = (k_codes, k_scales)
+
+        pairs = {}
+        chunk_words = {}
+        ssw_grouped = {}
+
+        def flip_scaler(psum_flip, c):
+            bank = psum_flip.tile([P, N_OUT], BF16, tag="flip", bufs=8, name="bank")
+            for s in range(O_TILES):
+                nc.tensor.transpose(
+                    bank[:, s * P : (s + 1) * P], scaler_rows[c][:, s, :], ident_bf[:]
+                )
+            for part in range(2):
+                cols = slice(part * N_TILE, (part + 1) * N_TILE)
+                pairs[(c, part)] = pool.tile([P, N_TILE, 2], BF16, tag="pairs", bufs=4, name="pairs")
                 nc.scalar.copy(
-                    out=scaler_pairs[:],
-                    in_=scaler_flipped[:].unsqueeze(2).to_broadcast([P, N_OUT, 2]),
+                    out=pairs[(c, part)][:],
+                    in_=bank[:, cols].unsqueeze(2).to_broadcast([P, N_TILE, 2]),
                 )
-                ssw_grouped = early.tile([P, HALVES, N_OUT, PACK], BF16, align_bytes=64)
-                for s in range(O_TILES):
-                    o_cols = slice(s * P, (s + 1) * P)
-                    slab_words = slab[:, s, :].bitcast(F32)
-                    words = psum_flip.tile([P, PACK, P], F32, tag="flip")
-                    for w in range(PACK):
-                        nc.tensor.transpose(
-                            words[:, w, :], slab_words[:, w : PACK * P : PACK], ident_f32[:]
-                        )
-                    by_half = words[:].bitcast(BF16).rearrange(
-                        "p (h u) (o e) -> p h o u e", u=2, e=2
-                    )
-                    for half in range(HALVES):
-                        nc.vector.tensor_tensor(
-                            out=ssw_grouped[:, half, o_cols, :].rearrange(
-                                "p o (u e) -> p o u e", e=2
-                            ),
-                            in0=by_half[:, half],
-                            in1=scaler_pairs[:, o_cols, :].unsqueeze(2).to_broadcast([P, P, 2, 2]),
-                            op=ALU.mult,
-                        )
-                for half in range(HALVES):
-                    nc.vector.quantize_mx(
-                        out=ssw_codes[:, c * HALVES + half, :].bitcast(FP8X4),
-                        scales=ssw_scales[:, c * HALVES + half, :],
-                        in_=ssw_grouped[:, half].rearrange("p o t -> p (o t)"),
-                    )
 
-            arrived = load_feature_tile(0)
-            x_rows = early.tile([P, B_TILES, N_IN], BF16)
-            nc.sync.dma_start(out=x_rows[:], in_=x.rearrange("(s p) i -> p s i", p=P))
-            for c in range(F_TILES):
-                coming = load_feature_tile(c + 1) if c + 1 < F_TILES else None
-                quantise_ssw_tile(c, arrived[0], arrived[1])
-                if c == 0:
-                    prepare_x()
-                arrived = coming
+        def flip_chunk(psum_flip, k):
+            c, s = divmod(k, O_TILES)
+            part, r = divmod(s, HALF_O)
+            slab_words = slabs[(c, part)][:, r, :].bitcast(F32)
+            words = psum_flip.tile([P, PACK, P], F32, tag="flip", bufs=8, name="words")
+            for w in range(PACK):
+                nc.tensor.transpose(
+                    words[:, w, :], slab_words[:, w : PACK * P : PACK], ident_f32[:]
+                )
+            chunk_words[k] = words
+            if r == HALF_O - 1:
+                following = 2 * c + part + PREFETCH
+                if following < 2 * F_TILES:
+                    load_slab(following // 2, following % 2)
+                elif following == 2 * F_TILES + 1:
+                    load_w()
 
-            nc.vector.memset(w_scales[:].bitcast(I32), 0)
+        def scale_chunk(k):
+            c, s = divmod(k, O_TILES)
+            part, r = divmod(s, HALF_O)
+            if r == 0:
+                ssw_grouped[(c, part)] = pool.tile(
+                    [P, HALVES, N_TILE, PACK], BF16, tag="ssw_grouped", bufs=2, align_bytes=64,
+                    name="ssw_grouped",
+                )
+            o_cols = slice(r * P, (r + 1) * P)
+            by_half = chunk_words[k][:].bitcast(BF16).rearrange(
+                "p (h u) (o e) -> p h o u e", u=2, e=2
+            )
+            for half in range(HALVES):
+                nc.vector.tensor_tensor(
+                    out=ssw_grouped[(c, part)][:, half, o_cols, :].rearrange(
+                        "p o (u e) -> p o u e", e=2
+                    ),
+                    in0=by_half[:, half],
+                    in1=pairs[(c, part)][:, o_cols, :].unsqueeze(2).to_broadcast([P, P, 2, 2]),
+                    op=ALU.mult,
+                )
+
+        def quantise_ssw(c, part):
+            n_cols = slice(part * N_TILE, (part + 1) * N_TILE)
+            for half in range(HALVES):
+                nc.vector.quantize_mx(
+                    out=ssw_codes[:, c * HALVES + half, n_cols].bitcast(FP8X4),
+                    scales=ssw_scales[:, c * HALVES + half, n_cols],
+                    in_=ssw_grouped[(c, part)][:, half].rearrange("p o t -> p (o t)"),
+                )
+
+        w_tiles = {}
+
+        def load_w():
+            w_codes = pool.tile([P, BASE_PASSES, N_OUT], U32, tag="slab", bufs=PREFETCH, align_bytes=64)
+            w_scales = pool.tile([P, BASE_PASSES, N_OUT], U8, tag="scaler_rows", bufs=2, align_bytes=64)
+            nc.gpsimd.memset(w_scales[:].bitcast(I32), 0)
             for quadrant in range(4):
                 nc.sync.dma_start(
                     out=w_scales[32 * quadrant : 32 * quadrant + 4, :, :].bitcast(I32),
@@ -228,12 +323,103 @@ def tile_bsplinekanlayer_kernel(
                     out=w_codes[:, g, :].bitcast(I32),
                     in_=base_weight_words[g].rearrange("p n t -> p (n t)").bitcast(I32),
                 )
+            w_tiles["codes"] = w_codes
+            w_tiles["scales"] = w_scales
 
-        with (
-            tc.tile_pool(name="forms", bufs=2) as forms,
-            tc.tile_pool(name="results", bufs=4) as results,
-            tc.psum_pool(name="psum_acc", bufs=1) as psum_acc,
-        ):
+        def chunks_done(n):
+            return max(0, min(CHUNKS, (n + 1 - FIRST_CHUNK_STEP) * CHUNKS // (SWITCH - 3 - FIRST_CHUNK_STEP)))
+
+        finish = {}
+        for c in range(F_TILES):
+            for half in range(HALVES):
+                ready = c * N_KNOTS + (7 if half == 0 else 11) + COMBINE_LAG
+                finish.setdefault(ready + 1, []).append(("peak", c, half))
+                finish.setdefault(ready + 2, []).append(("regroup", c, half))
+                finish.setdefault(ready + 4, []).append(("quantise", c, half))
+
+        def run_step(n):
+            if n >= 1 and n - 1 < STEPS:
+                take_sides(n - 1)
+            if n + LOOKAHEAD < STEPS:
+                take_square(n + LOOKAHEAD)
+            if n < STEPS:
+                take_cube(n)
+            for kind, c, half in finish.get(n, []):
+                if kind == "peak":
+                    take_peak(c, half)
+                elif kind == "regroup":
+                    regroup(c, half)
+            if 0 <= n - COMBINE_LAG < STEPS:
+                combine(n - COMBINE_LAG)
+            for kind, c, half in finish.get(n, []):
+                if kind == "quantise":
+                    quantise_half(c, half)
+
+        with tc.psum_pool(name="psum_flip", bufs=8) as psum_flip:
+            for pair in range(F_TILES // 2):
+                flipped = psum_flip.tile([P, 2, BATCH], BF16, tag="flip", bufs=8)
+                for c in range(2):
+                    for s in range(B_TILES):
+                        nc.tensor.transpose(
+                            flipped[:, c, s * P : (s + 1) * P],
+                            x_rows[:, s, (2 * pair + c) * P : (2 * pair + c + 1) * P],
+                            ident_bf[:],
+                        )
+                if pair % 2 == 0:
+                    nc.vector.tensor_copy(out=x_by_feature[:, 2 * pair : 2 * pair + 2, :], in_=flipped[:])
+                else:
+                    nc.scalar.copy(out=x_by_feature[:, 2 * pair : 2 * pair + 2, :], in_=flipped[:])
+            flip_scaler(psum_flip, 0)
+            for n in range(LOOKAHEAD):
+                take_square(n)
+
+            silu_grouped = pool.tile(
+                [P, HALVES, N_TILE, PACK], BF16, tag="ssw_grouped", bufs=2, align_bytes=64
+            )
+
+            def silu_piece(g, pair):
+                words = psum_flip.tile([P, 2, 2, P], F32, tag="flip", bufs=8)
+                for u in range(2):
+                    for s in range(2):
+                        nc.tensor.transpose(
+                            words[:, u, s, :],
+                            x_rows[:, 2 * pair + s, :].bitcast(F32)[:, 256 * g + u : 256 * (g + 1) : 2],
+                            ident_f32[:],
+                        )
+                nc.scalar.activation(
+                    out=silu_grouped[:, g, 2 * pair * P : 2 * (pair + 1) * P, :].rearrange(
+                        "p b (u e) -> p b u e", e=2
+                    ),
+                    in_=words[:].bitcast(BF16).rearrange("p u s (b e) -> p (s b) u e", e=2),
+                    func=ACT.Silu,
+                )
+
+            for n in range(SWITCH):
+                for k in range(chunks_done(n), chunks_done(n + 1)):
+                    flip_chunk(psum_flip, k)
+                    c, s = divmod(k, O_TILES)
+                    if s == HALF_O and c + 1 < F_TILES:
+                        flip_scaler(psum_flip, c + 1)
+                        if c + 2 < F_TILES:
+                            load_scaler(c + 2)
+                if n < 4:
+                    silu_piece(n // 2, n % 2)
+                    if n == 3:
+                        load_slab(1, 1)
+                if n == 6:
+                    nc.vector.quantize_mx(
+                        out=silu_codes[:].rearrange("p g b -> p (g b)").bitcast(FP8X4),
+                        scales=silu_scales[:].rearrange("p g b -> p (g b)"),
+                        in_=silu_grouped[:].rearrange("p g b t -> p (g b t)"),
+                    )
+                run_step(n)
+                for k in range(chunks_done(n - 1), chunks_done(n)):
+                    scale_chunk(k)
+                    if k % HALF_O == 0 and k > 0:
+                        quantise_ssw((k - 1) // O_TILES, (k - 1) // HALF_O % 2)
+            quantise_ssw(F_TILES - 1, 1)
+
+        with tc.psum_pool(name="psum_acc", bufs=1) as psum_acc:
             groups = [(s, n) for s in range(B_TILES) for n in range(N_TILES)]
             acc = {}
             for s, n in groups:
@@ -243,108 +429,37 @@ def tile_bsplinekanlayer_kernel(
                         out=acc[(s, n)][:],
                         lhsT=silu_codes[:, g, s * P : (s + 1) * P].bitcast(FP8X4),
                         lhsT_scale=silu_scales[:, g, s * P : (s + 1) * P],
-                        rhs=w_codes[:, g, n * N_TILE : (n + 1) * N_TILE].bitcast(FP8X4),
-                        rhs_scale=w_scales[:, g, n * N_TILE : (n + 1) * N_TILE],
+                        rhs=w_tiles["codes"][:, g, n * N_TILE : (n + 1) * N_TILE].bitcast(FP8X4),
+                        rhs_scale=w_tiles["scales"][:, g, n * N_TILE : (n + 1) * N_TILE],
                         start=(g == 0),
                         stop=False,
                     )
 
-            def finish_half(c, half, left, right):
-                planes = slice(half * PACK, (half + 1) * PACK)
-                grouped = forms.tile([P, BATCH, PACK], BF16, align_bytes=64)
-                if half == 0:
-                    peak = forms.tile([P, PACK, BATCH], BF16)
-                    nc.vector.tensor_tensor(
-                        out=peak[:], in0=left[:, planes, :], in1=right[:, planes, :], op=ALU.max
-                    )
-                    nc.scalar.copy(out=grouped[:], in_=peak[:].rearrange("p t b -> p b t"))
-                else:
-                    nc.vector.tensor_tensor(
-                        out=grouped[:],
-                        in0=left[:, planes, :].rearrange("p t b -> p b t"),
-                        in1=right[:, planes, :].rearrange("p t b -> p b t"),
-                        op=ALU.max,
-                    )
-                basis_codes = forms.tile([P, BATCH], U32, align_bytes=64)
-                basis_scales = forms.tile([P, BATCH], U8, align_bytes=64)
-                nc.vector.quantize_mx(
-                    out=basis_codes[:].bitcast(FP8X4),
-                    scales=basis_scales[:],
-                    in_=grouped[:].rearrange("p b t -> p (b t)"),
-                )
-                k = c * HALVES + half
+            def multiply(k):
+                k_codes, k_scales = codes[k]
                 for s, n in groups:
                     nc.tensor.matmul_mx(
                         out=acc[(s, n)][:],
-                        lhsT=basis_codes[:, s * P : (s + 1) * P].bitcast(FP8X4),
-                        lhsT_scale=basis_scales[:, s * P : (s + 1) * P],
+                        lhsT=k_codes[:, s * P : (s + 1) * P].bitcast(FP8X4),
+                        lhsT_scale=k_scales[:, s * P : (s + 1) * P],
                         rhs=ssw_codes[:, k, n * N_TILE : (n + 1) * N_TILE].bitcast(FP8X4),
                         rhs_scale=ssw_scales[:, k, n * N_TILE : (n + 1) * N_TILE],
                         start=False,
                         stop=(k == SPLINE_PASSES - 1),
                     )
 
-            for c in range(F_TILES):
-                v = x_by_feature[:, c, :]
-                left = forms.tile([P, N_BASIS, BATCH], BF16)
-                right = forms.tile([P, N_BASIS, BATCH], BF16)
-                up = {}
-                down = {}
-                for m in range(N_KNOTS):
-                    square = cubes.tile([P, BATCH], F32)
-                    nc.scalar.activation(
-                        out=square[:], in_=v, func=ACT.Square, bias=neg_knot[:, c, m : m + 1]
-                    )
-                    cube = cubes.tile([P, BATCH], F32)
-                    nc.vector.scalar_tensor_tensor(
-                        out=cube[:],
-                        in0=v,
-                        scalar=knot[:, c, m : m + 1],
-                        in1=square[:],
-                        op0=ALU.subtract,
-                        op1=ALU.mult,
-                    )
-                    if m <= N_BASIS:
-                        up_m = sided.tile([P, BATCH], F32)
-                        nc.scalar.activation(
-                            out=up_m[:], in_=cube[:], func=ACT.Relu, scale=up_scale[:, c, m : m + 1]
-                        )
-                        up[m] = up_m
-                    if m >= 3:
-                        down_m = sided.tile([P, BATCH], F32)
-                        nc.scalar.activation(
-                            out=down_m[:],
-                            in_=cube[:],
-                            func=ACT.Relu,
-                            scale=neg_down_scale[:, c, m - 3 : m - 2],
-                        )
-                        down[m] = down_m
-                    if 1 <= m <= N_BASIS:
-                        j = m - 1
-                        nc.vector.scalar_tensor_tensor(
-                            out=left[:, j, :],
-                            in0=up[j][:],
-                            scalar=left_mix[:, c, j : j + 1],
-                            in1=up[j + 1][:],
-                            op0=ALU.mult,
-                            op1=ALU.subtract,
-                        )
-                    if m >= 4:
-                        j = m - 4
-                        nc.vector.scalar_tensor_tensor(
-                            out=right[:, j, :],
-                            in0=down[j + 4][:],
-                            scalar=right_mix[:, c, j : j + 1],
-                            in1=down[j + 3][:],
-                            op0=ALU.mult,
-                            op1=ALU.subtract,
-                        )
-                    if m == N_KNOTS - 1 - PACK:
-                        finish_half(c, 0, left, right)
-                finish_half(c, 1, left, right)
+            multiplied = 0
+            for n in range(SWITCH, max(finish) + 1):
+                while multiplied in codes:
+                    multiply(multiplied)
+                    multiplied += 1
+                run_step(n)
+            while multiplied in codes:
+                multiply(multiplied)
+                multiplied += 1
 
             for index, (s, n) in enumerate(groups):
-                result = results.tile([P, N_TILE], F32)
+                result = pool.tile([P, N_TILE], F32, tag="slab", bufs=PREFETCH, align_bytes=64)
                 if index % 2 == 0:
                     nc.scalar.copy(out=result[:], in_=acc[(s, n)][:])
                 else:

@@ -90,6 +90,7 @@ FIRST_CHUNK_STEP = 3
 EARLY_TILES = 4
 SWITCH = EARLY_TILES * N_KNOTS + 2
 STEPS = F_TILES * N_KNOTS
+TENSOR_FORMS = 28
 
 
 def tile_bsplinekanlayer_kernel(
@@ -140,6 +141,10 @@ def tile_bsplinekanlayer_kernel(
         make_identity(nc, ident_bf[:])
         ident_f32 = consts.tile([P, P], F32)
         make_identity(nc, ident_f32[:])
+        minus_ident = consts.tile([P, P], F32)
+        nc.gpsimd.tensor_scalar(
+            out=minus_ident[:], in0=ident_f32[:], scalar1=-1.0, scalar2=1.0, op0=ALU.mult, op1=ALU.mult
+        )
 
         knot, neg_knot, up_scale, neg_down_scale, left_mix, right_mix = spline_constants(
             tc, nc, consts, knot_bf
@@ -163,14 +168,43 @@ def tile_bsplinekanlayer_kernel(
 
         def take_square(n):
             c, m = divmod(n, N_KNOTS)
-            square[n] = pool.tile([P, BATCH], F32, tag="square", bufs=3, name="square")
+            square[n] = pool.tile([P, BATCH], F32, tag="square", bufs=4, name="square")
             nc.scalar.activation(
                 out=square[n][:], in_=x_by_feature[:, c, :], func=ACT.Square,
                 bias=neg_knot[:, c, m : m + 1],
             )
 
+        def one_sided(n):
+            c, m = divmod(n, N_KNOTS)
+            return c >= EARLY_TILES and not 3 <= m <= N_BASIS
+
+        def take_one_side(n):
+            c, m = divmod(n, N_KNOTS)
+            distance = pool.tile([P, BATCH], F32, tag="cube", bufs=3, name="distance")
+            nc.vector.tensor_scalar(
+                out=distance[:], in0=x_by_feature[:, c, :], scalar1=knot[:, c, m : m + 1], scalar2=0.0,
+                op0=ALU.subtract, op1=ALU.max if m < 3 else ALU.min,
+            )
+            cube[n] = distance
+
+        def finish_one_side(n):
+            c, m = divmod(n, N_KNOTS)
+            if m < 3:
+                up[n] = pool.tile([P, BATCH], F32, tag="up", bufs=5, name="up")
+                side, scale = up[n], up_scale[:, c, m : m + 1]
+            else:
+                down[n] = pool.tile([P, BATCH], F32, tag="down", bufs=4, name="down")
+                side, scale = down[n], neg_down_scale[:, c, m - 3 : m - 2]
+            nc.vector.scalar_tensor_tensor(
+                out=side[:], in0=cube[n][:], scalar=scale, in1=square[n][:],
+                op0=ALU.mult, op1=ALU.mult,
+            )
+
         def take_cube(n):
             c, m = divmod(n, N_KNOTS)
+            if one_sided(n):
+                take_one_side(n)
+                return
             cube[n] = pool.tile([P, BATCH], F32, tag="cube", bufs=3, name="cube")
             nc.vector.scalar_tensor_tensor(
                 out=cube[n][:], in0=x_by_feature[:, c, :], scalar=knot[:, c, m : m + 1],
@@ -179,8 +213,11 @@ def tile_bsplinekanlayer_kernel(
 
         def take_sides(n):
             c, m = divmod(n, N_KNOTS)
+            if one_sided(n):
+                finish_one_side(n)
+                return
             if m <= N_BASIS:
-                up[n] = pool.tile([P, BATCH], F32, tag="up", bufs=4, name="up")
+                up[n] = pool.tile([P, BATCH], F32, tag="up", bufs=5, name="up")
                 nc.scalar.activation(
                     out=up[n][:], in_=cube[n][:], func=ACT.Relu, scale=up_scale[:, c, m : m + 1]
                 )
@@ -197,9 +234,35 @@ def tile_bsplinekanlayer_kernel(
                 store[key] = pool.tile([P, PACK, BATCH], BF16, tag=tag, bufs=2, name=tag)
             return store[key][:, j % PACK, :]
 
+        form_banks = {}
+
+        def on_tensor(c, j):
+            return c * N_BASIS + j < TENSOR_FORMS
+
+        def combine_on_tensor(psum, n):
+            c, m = divmod(n, N_KNOTS)
+            j = m - 1
+            if not (0 <= j < N_BASIS and on_tensor(c, j)):
+                return
+            diagonal = pool.tile([P, P], F32, tag="diagonal", bufs=2, name="diagonal")
+            nc.gpsimd.tensor_scalar(
+                out=diagonal[:], in0=ident_f32[:], scalar1=left_mix[:, c, j : j + 1], scalar2=1.0,
+                op0=ALU.mult, op1=ALU.mult,
+            )
+            bank = psum.tile([P, BATCH], F32, tag="flip", bufs=8, name="form")
+            nc.tensor.matmul(out=bank[:], lhsT=diagonal[:], rhs=up[n - 1][:], start=True, stop=False)
+            nc.tensor.matmul(out=bank[:], lhsT=minus_ident[:], rhs=up[n][:], start=False, stop=True)
+            form_banks[(c, j)] = bank
+
+        def collect_form(n):
+            c, m = divmod(n, N_KNOTS)
+            j = m - 1
+            if (c, j) in form_banks:
+                nc.scalar.copy(out=half_tile(left, c, j, "left"), in_=form_banks.pop((c, j))[:])
+
         def combine(n):
             c, m = divmod(n, N_KNOTS)
-            if 1 <= m <= N_BASIS:
+            if 1 <= m <= N_BASIS and not on_tensor(c, m - 1):
                 j = m - 1
                 nc.vector.scalar_tensor_tensor(
                     out=half_tile(left, c, j, "left"), in0=up[n - 1][:],
@@ -231,8 +294,8 @@ def tile_bsplinekanlayer_kernel(
 
         def quantise_half(c, half):
             k = c * HALVES + half
-            k_codes = pool.tile([P, BATCH], U32, tag="k_codes", bufs=8, align_bytes=64, name="k_codes")
-            k_scales = pool.tile([P, BATCH], U8, tag="k_scales", bufs=8, align_bytes=64, name="k_scales")
+            k_codes = pool.tile([P, BATCH], U32, tag="k_codes", bufs=7, align_bytes=64, name="k_codes")
+            k_scales = pool.tile([P, BATCH], U8, tag="k_scales", bufs=7, align_bytes=64, name="k_scales")
             nc.vector.quantize_mx(
                 out=k_codes[:].bitcast(FP8X4), scales=k_scales[:],
                 in_=grouped[(c, half)][:].rearrange("p b t -> p (b t)"),
@@ -338,6 +401,7 @@ def tile_bsplinekanlayer_kernel(
                 finish.setdefault(ready + 4, []).append(("quantise", c, half))
 
         def run_step(n):
+            collect_form(n - COMBINE_LAG - 1)
             if n >= 1 and n - 1 < STEPS:
                 take_sides(n - 1)
             if n + LOOKAHEAD < STEPS:
@@ -402,6 +466,7 @@ def tile_bsplinekanlayer_kernel(
                         flip_scaler(psum_flip, c + 1)
                         if c + 2 < F_TILES:
                             load_scaler(c + 2)
+                combine_on_tensor(psum_flip, n - COMBINE_LAG)
                 if n < 4:
                     silu_piece(n // 2, n % 2)
                     if n == 3:

@@ -31,56 +31,6 @@ N_TILES = N_OUT // N_TILE
 FLOPS = 2 * BATCH * N_OUT * (N_IN + N_IN * N_BASIS)
 
 
-def spline_constants(tc, nc, consts, knot_bf):
-    knot = consts.tile([P, F_TILES, N_KNOTS], F32)
-    nc.vector.tensor_copy(out=knot[:], in_=knot_bf[:])
-    neg_knot = consts.tile([P, F_TILES, N_KNOTS], F32)
-    nc.vector.tensor_scalar_mul(out=neg_knot[:], in0=knot[:], scalar1=-1.0)
-
-    def span(width):
-        count = N_KNOTS - width
-        h = consts.tile([P, F_TILES, count], F32, name="span%d" % width)
-        nc.vector.tensor_sub(out=h[:], in0=knot[:, :, width:], in1=knot[:, :, :count])
-        return h
-
-    h1, h2, h3, h4 = span(1), span(2), span(3), span(4)
-
-    def inverse_product(name, factors):
-        prod = consts.tile([P, F_TILES, N_BASIS], F32, name=name)
-        nc.vector.tensor_mul(out=prod[:], in0=factors[0], in1=factors[1])
-        for factor in factors[2:]:
-            nc.vector.tensor_mul(out=prod[:], in0=prod[:], in1=factor)
-        nc.vector.reciprocal(out=prod[:], in_=prod[:])
-        return prod
-
-    first_left = inverse_product("first_left", [h1[:, :, 0:8], h2[:, :, 0:8], h3[:, :, 0:8]])
-    first_right = inverse_product("first_right", [h1[:, :, 3:11], h2[:, :, 2:10], h3[:, :, 1:9]])
-    second_left = inverse_product(
-        "second_left", [h1[:, :, 0:8], h1[:, :, 1:9], h2[:, :, 1:9], h3[:, :, 1:9]]
-    )
-    second_right = inverse_product(
-        "second_right", [h3[:, :, 0:8], h2[:, :, 1:9], h1[:, :, 2:10], h1[:, :, 3:11]]
-    )
-
-    up_scale = consts.tile([P, F_TILES, N_BASIS + 1], F32)
-    nc.vector.tensor_copy(out=up_scale[:, :, 0:1], in_=first_left[:, :, 0:1])
-    nc.vector.tensor_mul(out=up_scale[:, :, 1:9], in0=second_left[:], in1=h4[:])
-    down_scale = consts.tile([P, F_TILES, N_BASIS + 1], F32)
-    nc.vector.tensor_mul(out=down_scale[:, :, 0:8], in0=second_right[:], in1=h4[:])
-    nc.vector.tensor_copy(out=down_scale[:, :, 8:9], in_=first_right[:, :, 7:8])
-
-    left_mix = consts.tile([P, F_TILES, N_BASIS], F32)
-    nc.vector.reciprocal(out=left_mix[:], in_=up_scale[:, :, 0:8])
-    nc.vector.tensor_mul(out=left_mix[:], in0=left_mix[:], in1=first_left[:])
-    right_mix = consts.tile([P, F_TILES, N_BASIS], F32)
-    nc.vector.reciprocal(out=right_mix[:], in_=down_scale[:, :, 1:9])
-    nc.vector.tensor_mul(out=right_mix[:], in0=right_mix[:], in1=first_right[:])
-
-    neg_down_scale = consts.tile([P, F_TILES, N_BASIS + 1], F32)
-    nc.vector.tensor_scalar_mul(out=neg_down_scale[:], in0=down_scale[:], scalar1=-1.0)
-    return knot, neg_knot, up_scale, neg_down_scale, left_mix, right_mix
-
-
 LOOKAHEAD = 2
 COMBINE_LAG = 2
 PREFETCH = 4
@@ -88,10 +38,76 @@ HALF_O = O_TILES // 2
 CHUNKS = F_TILES * O_TILES
 FIRST_CHUNK_STEP = 3
 EARLY_TILES = 4
-SWITCH = EARLY_TILES * N_KNOTS + 2
+SWITCH = EARLY_TILES * N_KNOTS - 2
 STEPS = F_TILES * N_KNOTS
-TENSOR_FORMS = 28
 
+
+def spline_constants(nc, consts, scratch, knot_bf):
+    used = [0]
+
+    def temporary(count):
+        first = used[0]
+        used[0] = first + F_TILES * count
+        return scratch[:, first : used[0]].rearrange("p (c m) -> p c m", c=F_TILES)
+
+    def constant(name, count):
+        return consts.tile([P, F_TILES, count], F32, name=name)
+
+    knot = constant("knot", N_KNOTS)
+    nc.vector.tensor_copy(out=knot[:], in_=knot_bf[:])
+    neg_knot = constant("neg_knot", N_KNOTS)
+    nc.vector.tensor_scalar_mul(out=neg_knot[:], in0=knot[:], scalar1=-1.0)
+
+    spans = temporary(30)
+    starts = {1: 0, 2: 11, 3: 21}
+    for w, first in starts.items():
+        count = N_KNOTS - w
+        nc.vector.tensor_sub(
+            out=spans[:, :, first : first + count], in0=knot[:, :, w:], in1=knot[:, :, :count]
+        )
+    h4 = temporary(N_BASIS)
+    nc.vector.tensor_sub(out=h4, in0=knot[:, :, 4:], in1=knot[:, :, :N_BASIS])
+    inverses = temporary(30)
+    nc.vector.reciprocal(out=inverses, in_=spans)
+    h1, h3 = spans[:, :, 0:11], spans[:, :, 21:30]
+    r1, r2, r3 = inverses[:, :, 0:11], inverses[:, :, 11:21], inverses[:, :, 21:30]
+
+    first_left = temporary(N_BASIS + 1)
+    nc.vector.tensor_mul(out=first_left, in0=r1[:, :, 0:9], in1=r2[:, :, 0:9])
+    ratio = temporary(N_BASIS)
+    nc.vector.tensor_mul(out=ratio, in0=h4, in1=r1[:, :, 0:8])
+    nc.vector.tensor_mul(out=first_left, in0=first_left, in1=r3)
+    up_scale = constant("up_scale", N_BASIS + 1)
+    nc.vector.tensor_copy(out=up_scale[:, :, 0:1], in_=first_left[:, :, 0:1])
+    nc.vector.tensor_mul(out=up_scale[:, :, 1:9], in0=first_left[:, :, 1:9], in1=ratio)
+
+    neg_down_scale = constant("neg_down_scale", N_BASIS + 1)
+    left_mix = constant("left_mix", N_BASIS)
+    right_mix = constant("right_mix", N_BASIS)
+    third_mix = constant("third_mix", PACK)
+    neg_outer = constant("neg_outer", PACK)
+
+    def rest():
+        r4 = temporary(N_BASIS)
+        nc.vector.reciprocal(out=r4, in_=h4)
+        nc.vector.memset(left_mix[:, :, 0:1], 1.0)
+        nc.vector.tensor_mul(out=left_mix[:, :, 1:8], in0=h1[:, :, 0:7], in1=r4[:, :, 0:7])
+        nc.vector.tensor_mul(out=third_mix[:], in0=h4[:, :, 0:4], in1=r2[:, :, 0:4])
+        nc.vector.tensor_mul(out=neg_outer[:], in0=h3[:, :, 2:6], in1=r4[:, :, 1:5])
+        nc.vector.tensor_mul(out=third_mix[:], in0=third_mix[:], in1=neg_outer[:])
+        first_right = temporary(N_BASIS + 1)
+        nc.vector.tensor_mul(out=first_right, in0=r3, in1=r2[:, :, 1:10])
+        down_ratio = temporary(N_BASIS)
+        nc.vector.tensor_mul(out=down_ratio, in0=h4, in1=r1[:, :, 3:11])
+        nc.vector.tensor_mul(out=first_right, in0=first_right, in1=r1[:, :, 2:11])
+        nc.vector.tensor_scalar_mul(out=first_right, in0=first_right, scalar1=-1.0)
+        nc.vector.tensor_mul(out=neg_down_scale[:, :, 0:8], in0=first_right[:, :, 0:8], in1=down_ratio)
+        nc.vector.tensor_copy(out=neg_down_scale[:, :, 8:9], in_=first_right[:, :, 8:9])
+        nc.vector.tensor_copy(out=neg_outer[:], in_=first_right[:, :, 1:5])
+        nc.vector.memset(right_mix[:, :, 7:8], 1.0)
+        nc.vector.tensor_mul(out=right_mix[:, :, 0:7], in0=h1[:, :, 4:11], in1=r4[:, :, 1:8])
+
+    return knot, neg_knot, up_scale, neg_down_scale, left_mix, right_mix, third_mix, neg_outer, rest
 
 def tile_bsplinekanlayer_kernel(
     tc, x, base_weight_words, base_weight_scales, spline_weight, spline_scaler, grid, out
@@ -141,20 +157,26 @@ def tile_bsplinekanlayer_kernel(
         make_identity(nc, ident_bf[:])
         ident_f32 = consts.tile([P, P], F32)
         make_identity(nc, ident_f32[:])
+
         minus_ident = consts.tile([P, P], F32)
         nc.gpsimd.tensor_scalar(
             out=minus_ident[:], in0=ident_f32[:], scalar1=-1.0, scalar2=1.0, op0=ALU.mult, op1=ALU.mult
         )
 
-        knot, neg_knot, up_scale, neg_down_scale, left_mix, right_mix = spline_constants(
-            tc, nc, consts, knot_bf
-        )
+        scratch = pool.tile([P, 1024], F32, tag="grouped", bufs=2, align_bytes=64)
+        (
+            knot, neg_knot, up_scale, neg_down_scale, left_mix, right_mix, third_mix, neg_outer,
+            remaining_constants,
+        ) = spline_constants(nc, consts, scratch, knot_bf)
 
         x_by_feature = keep.tile([P, F_TILES, BATCH], BF16)
         silu_codes = keep.tile([P, BASE_PASSES, BATCH], U32, align_bytes=64)
         silu_scales = keep.tile([P, BASE_PASSES, BATCH], U8, align_bytes=64)
         ssw_codes = keep.tile([P, SPLINE_PASSES, N_OUT], U32, align_bytes=64)
         ssw_scales = keep.tile([P, SPLINE_PASSES, N_OUT], U8, align_bytes=64)
+
+        def three_term(c, j):
+            return c < EARLY_TILES and j < PACK
 
         square = {}
         cube = {}
@@ -168,44 +190,15 @@ def tile_bsplinekanlayer_kernel(
 
         def take_square(n):
             c, m = divmod(n, N_KNOTS)
-            square[n] = pool.tile([P, BATCH], F32, tag="square", bufs=4, name="square")
+            square[n] = pool.tile([P, BATCH], F32, tag="square", bufs=3, name="square")
             nc.scalar.activation(
                 out=square[n][:], in_=x_by_feature[:, c, :], func=ACT.Square,
                 bias=neg_knot[:, c, m : m + 1],
             )
 
-        def one_sided(n):
-            c, m = divmod(n, N_KNOTS)
-            return c >= EARLY_TILES and not 3 <= m <= N_BASIS
-
-        def take_one_side(n):
-            c, m = divmod(n, N_KNOTS)
-            distance = pool.tile([P, BATCH], F32, tag="cube", bufs=3, name="distance")
-            nc.vector.tensor_scalar(
-                out=distance[:], in0=x_by_feature[:, c, :], scalar1=knot[:, c, m : m + 1], scalar2=0.0,
-                op0=ALU.subtract, op1=ALU.max if m < 3 else ALU.min,
-            )
-            cube[n] = distance
-
-        def finish_one_side(n):
-            c, m = divmod(n, N_KNOTS)
-            if m < 3:
-                up[n] = pool.tile([P, BATCH], F32, tag="up", bufs=5, name="up")
-                side, scale = up[n], up_scale[:, c, m : m + 1]
-            else:
-                down[n] = pool.tile([P, BATCH], F32, tag="down", bufs=4, name="down")
-                side, scale = down[n], neg_down_scale[:, c, m - 3 : m - 2]
-            nc.vector.scalar_tensor_tensor(
-                out=side[:], in0=cube[n][:], scalar=scale, in1=square[n][:],
-                op0=ALU.mult, op1=ALU.mult,
-            )
-
         def take_cube(n):
             c, m = divmod(n, N_KNOTS)
-            if one_sided(n):
-                take_one_side(n)
-                return
-            cube[n] = pool.tile([P, BATCH], F32, tag="cube", bufs=3, name="cube")
+            cube[n] = pool.tile([P, BATCH], F32, tag="cube", bufs=4, name="cube")
             nc.vector.scalar_tensor_tensor(
                 out=cube[n][:], in0=x_by_feature[:, c, :], scalar=knot[:, c, m : m + 1],
                 in1=square[n][:], op0=ALU.subtract, op1=ALU.mult,
@@ -213,15 +206,12 @@ def tile_bsplinekanlayer_kernel(
 
         def take_sides(n):
             c, m = divmod(n, N_KNOTS)
-            if one_sided(n):
-                finish_one_side(n)
-                return
             if m <= N_BASIS:
                 up[n] = pool.tile([P, BATCH], F32, tag="up", bufs=5, name="up")
                 nc.scalar.activation(
                     out=up[n][:], in_=cube[n][:], func=ACT.Relu, scale=up_scale[:, c, m : m + 1]
                 )
-            if m >= 3:
+            if m >= 3 and not three_term(c, m - 3):
                 down[n] = pool.tile([P, BATCH], F32, tag="down", bufs=4, name="down")
                 nc.scalar.activation(
                     out=down[n][:], in_=cube[n][:], func=ACT.Relu,
@@ -236,40 +226,44 @@ def tile_bsplinekanlayer_kernel(
 
         form_banks = {}
 
-        def on_tensor(c, j):
-            return c * N_BASIS + j < TENSOR_FORMS
+        def diagonal(scale):
+            tile = pool.tile([P, P], F32, tag="diagonal", bufs=3, name="diagonal")
+            nc.gpsimd.tensor_scalar(
+                out=tile[:], in0=ident_f32[:], scalar1=scale, scalar2=1.0, op0=ALU.mult, op1=ALU.mult
+            )
+            return tile
 
         def combine_on_tensor(psum, n):
             c, m = divmod(n, N_KNOTS)
-            j = m - 1
-            if not (0 <= j < N_BASIS and on_tensor(c, j)):
+            j = m - 2
+            if j < 0 or not three_term(c, j):
                 return
-            diagonal = pool.tile([P, P], F32, tag="diagonal", bufs=2, name="diagonal")
-            nc.gpsimd.tensor_scalar(
-                out=diagonal[:], in0=ident_f32[:], scalar1=left_mix[:, c, j : j + 1], scalar2=1.0,
-                op0=ALU.mult, op1=ALU.mult,
-            )
+            first = diagonal(left_mix[:, c, j : j + 1])
+            third = diagonal(third_mix[:, c, j : j + 1])
             bank = psum.tile([P, BATCH], F32, tag="flip", bufs=8, name="form")
-            nc.tensor.matmul(out=bank[:], lhsT=diagonal[:], rhs=up[n - 1][:], start=True, stop=False)
-            nc.tensor.matmul(out=bank[:], lhsT=minus_ident[:], rhs=up[n][:], start=False, stop=True)
+            nc.tensor.matmul(out=bank[:], lhsT=first[:], rhs=up[n - 2][:], start=True, stop=False)
+            nc.tensor.matmul(out=bank[:], lhsT=minus_ident[:], rhs=up[n - 1][:], start=False, stop=False)
+            nc.tensor.matmul(out=bank[:], lhsT=third[:], rhs=up[n][:], start=False, stop=True)
             form_banks[(c, j)] = bank
-
-        def collect_form(n):
-            c, m = divmod(n, N_KNOTS)
-            j = m - 1
-            if (c, j) in form_banks:
-                nc.scalar.copy(out=half_tile(left, c, j, "left"), in_=form_banks.pop((c, j))[:])
 
         def combine(n):
             c, m = divmod(n, N_KNOTS)
-            if 1 <= m <= N_BASIS and not on_tensor(c, m - 1):
+            if 1 <= m <= N_BASIS and not three_term(c, m - 1):
                 j = m - 1
                 nc.vector.scalar_tensor_tensor(
                     out=half_tile(left, c, j, "left"), in0=up[n - 1][:],
                     scalar=left_mix[:, c, j : j + 1], in1=up[n][:],
                     op0=ALU.mult, op1=ALU.subtract,
                 )
-            if m >= 4:
+            if m >= 4 and three_term(c, m - 4):
+                j = m - 4
+                if j == 0:
+                    peak[(c, 0)] = pool.tile([P, PACK, BATCH], BF16, tag="peak", bufs=2, name="peak")
+                nc.vector.scalar_tensor_tensor(
+                    out=peak[(c, 0)][:, j, :], in0=cube[n][:], scalar=neg_outer[:, c, j : j + 1],
+                    in1=form_banks[(c, j)][:], op0=ALU.mult, op1=ALU.min,
+                )
+            elif m >= 4:
                 j = m - 4
                 nc.vector.scalar_tensor_tensor(
                     out=half_tile(right, c, j, "right"), in0=down[n][:],
@@ -278,7 +272,7 @@ def tile_bsplinekanlayer_kernel(
                 )
 
         def take_peak(c, half):
-            peak[(c, half)] = pool.tile([P, PACK, BATCH], BF16, tag="peak", bufs=1, name="peak")
+            peak[(c, half)] = pool.tile([P, PACK, BATCH], BF16, tag="peak", bufs=2, name="peak")
             nc.vector.tensor_tensor(
                 out=peak[(c, half)][:], in0=left[(c, half)][:], in1=right[(c, half)][:], op=ALU.max
             )
@@ -287,20 +281,35 @@ def tile_bsplinekanlayer_kernel(
             grouped[(c, half)] = pool.tile(
                 [P, BATCH, PACK], BF16, tag="grouped", bufs=2, align_bytes=64, name="grouped"
             )
-            nc.scalar.copy(
-                out=grouped[(c, half)][:].rearrange("p (g i) t -> p g t i", i=4),
-                in_=peak[(c, half)][:].rearrange("p t (g i) -> p g t i", i=4),
+            to = grouped[(c, half)][:].rearrange("p (g i) t -> p g t i", i=4)
+            of = peak[(c, half)][:].rearrange("p t (g i) -> p g t i", i=4)
+            if half == 0 and three_term(c, 0):
+                nc.scalar.activation(out=to, in_=of, func=ACT.Relu)
+            else:
+                nc.scalar.copy(out=to, in_=of)
+
+        def take_grouped_peak(c, half, cols):
+            if (c, half) not in grouped:
+                grouped[(c, half)] = pool.tile(
+                    [P, BATCH, PACK], BF16, tag="grouped", bufs=2, align_bytes=64, name="grouped"
+                )
+            nc.vector.tensor_tensor(
+                out=grouped[(c, half)][:, cols, :],
+                in0=left[(c, half)][:, :, cols].rearrange("p t b -> p b t"),
+                in1=right[(c, half)][:, :, cols].rearrange("p t b -> p b t"),
+                op=ALU.max,
             )
 
-        def quantise_half(c, half):
+        def quantise_half(c, half, cols=slice(0, BATCH)):
             k = c * HALVES + half
-            k_codes = pool.tile([P, BATCH], U32, tag="k_codes", bufs=7, align_bytes=64, name="k_codes")
-            k_scales = pool.tile([P, BATCH], U8, tag="k_scales", bufs=7, align_bytes=64, name="k_scales")
+            if k not in codes:
+                k_codes = pool.tile([P, BATCH], U32, tag="k_codes", bufs=6, align_bytes=64, name="k_codes")
+                k_scales = pool.tile([P, BATCH], U8, tag="k_scales", bufs=6, align_bytes=64, name="k_scales")
+                codes[k] = (k_codes, k_scales)
             nc.vector.quantize_mx(
-                out=k_codes[:].bitcast(FP8X4), scales=k_scales[:],
-                in_=grouped[(c, half)][:].rearrange("p b t -> p (b t)"),
+                out=codes[k][0][:, cols].bitcast(FP8X4), scales=codes[k][1][:, cols],
+                in_=grouped[(c, half)][:, cols, :].rearrange("p b t -> p (b t)"),
             )
-            codes[k] = (k_codes, k_scales)
 
         pairs = {}
         chunk_words = {}
@@ -314,7 +323,7 @@ def tile_bsplinekanlayer_kernel(
                 )
             for part in range(2):
                 cols = slice(part * N_TILE, (part + 1) * N_TILE)
-                pairs[(c, part)] = pool.tile([P, N_TILE, 2], BF16, tag="pairs", bufs=4, name="pairs")
+                pairs[(c, part)] = pool.tile([P, N_TILE, 2], BF16, tag="pairs", bufs=3, name="pairs")
                 nc.scalar.copy(
                     out=pairs[(c, part)][:],
                     in_=bank[:, cols].unsqueeze(2).to_broadcast([P, N_TILE, 2]),
@@ -396,12 +405,18 @@ def tile_bsplinekanlayer_kernel(
         for c in range(F_TILES):
             for half in range(HALVES):
                 ready = c * N_KNOTS + (7 if half == 0 else 11) + COMBINE_LAG
-                finish.setdefault(ready + 1, []).append(("peak", c, half))
-                finish.setdefault(ready + 2, []).append(("regroup", c, half))
-                finish.setdefault(ready + 4, []).append(("quantise", c, half))
+                if half == 0 and three_term(c, 0):
+                    steps = (("regroup", 1), ("quantise", 3))
+                elif c < EARLY_TILES or (half == 0 and c < F_TILES - 1):
+                    steps = (("peak", 1), ("regroup", 2), ("quantise", 4))
+                elif half == 0 or c < F_TILES - 1:
+                    steps = (("grouped_peak", 1), ("quantise", 2))
+                else:
+                    steps = (("last", 1),)
+                for kind, delay in steps:
+                    finish.setdefault(ready + delay, []).append((kind, c, half))
 
         def run_step(n):
-            collect_form(n - COMBINE_LAG - 1)
             if n >= 1 and n - 1 < STEPS:
                 take_sides(n - 1)
             if n + LOOKAHEAD < STEPS:
@@ -411,6 +426,8 @@ def tile_bsplinekanlayer_kernel(
             for kind, c, half in finish.get(n, []):
                 if kind == "peak":
                     take_peak(c, half)
+                elif kind == "grouped_peak":
+                    take_grouped_peak(c, half, slice(0, BATCH))
                 elif kind == "regroup":
                     regroup(c, half)
             if 0 <= n - COMBINE_LAG < STEPS:
@@ -429,13 +446,14 @@ def tile_bsplinekanlayer_kernel(
                             x_rows[:, s, (2 * pair + c) * P : (2 * pair + c + 1) * P],
                             ident_bf[:],
                         )
-                if pair % 2 == 0:
+                if pair in (1, 2):
                     nc.vector.tensor_copy(out=x_by_feature[:, 2 * pair : 2 * pair + 2, :], in_=flipped[:])
                 else:
                     nc.scalar.copy(out=x_by_feature[:, 2 * pair : 2 * pair + 2, :], in_=flipped[:])
+                if pair == 0:
+                    for n in range(LOOKAHEAD):
+                        take_square(n)
             flip_scaler(psum_flip, 0)
-            for n in range(LOOKAHEAD):
-                take_square(n)
 
             silu_grouped = pool.tile(
                 [P, HALVES, N_TILE, PACK], BF16, tag="ssw_grouped", bufs=2, align_bytes=64
@@ -462,7 +480,7 @@ def tile_bsplinekanlayer_kernel(
                 for k in range(chunks_done(n), chunks_done(n + 1)):
                     flip_chunk(psum_flip, k)
                     c, s = divmod(k, O_TILES)
-                    if s == HALF_O and c + 1 < F_TILES:
+                    if s == HALF_O + 2 and c + 1 < F_TILES:
                         flip_scaler(psum_flip, c + 1)
                         if c + 2 < F_TILES:
                             load_scaler(c + 2)
@@ -478,6 +496,8 @@ def tile_bsplinekanlayer_kernel(
                         in_=silu_grouped[:].rearrange("p g b t -> p (g b t)"),
                     )
                 run_step(n)
+                if n == 0:
+                    remaining_constants()
                 for k in range(chunks_done(n - 1), chunks_done(n)):
                     scale_chunk(k)
                     if k % HALF_O == 0 and k > 0:
@@ -489,27 +509,30 @@ def tile_bsplinekanlayer_kernel(
             acc = {}
             for s, n in groups:
                 acc[(s, n)] = psum_acc.tile([P, N_TILE], F32, name="acc_%d_%d" % (s, n))
-                for g in range(BASE_PASSES):
-                    nc.tensor.matmul_mx(
-                        out=acc[(s, n)][:],
-                        lhsT=silu_codes[:, g, s * P : (s + 1) * P].bitcast(FP8X4),
-                        lhsT_scale=silu_scales[:, g, s * P : (s + 1) * P],
-                        rhs=w_tiles["codes"][:, g, n * N_TILE : (n + 1) * N_TILE].bitcast(FP8X4),
-                        rhs_scale=w_tiles["scales"][:, g, n * N_TILE : (n + 1) * N_TILE],
-                        start=(g == 0),
-                        stop=False,
-                    )
 
-            def multiply(k):
-                k_codes, k_scales = codes[k]
+            def multiply_base():
                 for s, n in groups:
+                    for g in range(BASE_PASSES):
+                        nc.tensor.matmul_mx(
+                            out=acc[(s, n)][:],
+                            lhsT=silu_codes[:, g, s * P : (s + 1) * P].bitcast(FP8X4),
+                            lhsT_scale=silu_scales[:, g, s * P : (s + 1) * P],
+                            rhs=w_tiles["codes"][:, g, n * N_TILE : (n + 1) * N_TILE].bitcast(FP8X4),
+                            rhs_scale=w_tiles["scales"][:, g, n * N_TILE : (n + 1) * N_TILE],
+                            start=False,
+                            stop=False,
+                        )
+
+            def multiply(k, of=groups):
+                k_codes, k_scales = codes[k]
+                for s, n in of:
                     nc.tensor.matmul_mx(
                         out=acc[(s, n)][:],
                         lhsT=k_codes[:, s * P : (s + 1) * P].bitcast(FP8X4),
                         lhsT_scale=k_scales[:, s * P : (s + 1) * P],
                         rhs=ssw_codes[:, k, n * N_TILE : (n + 1) * N_TILE].bitcast(FP8X4),
                         rhs_scale=ssw_scales[:, k, n * N_TILE : (n + 1) * N_TILE],
-                        start=False,
+                        start=(k == 0),
                         stop=(k == SPLINE_PASSES - 1),
                     )
 
@@ -518,17 +541,34 @@ def tile_bsplinekanlayer_kernel(
                 while multiplied in codes:
                     multiply(multiplied)
                     multiplied += 1
+                if n == SWITCH:
+                    multiply_base()
                 run_step(n)
             while multiplied in codes:
                 multiply(multiplied)
                 multiplied += 1
 
-            for index, (s, n) in enumerate(groups):
-                result = pool.tile([P, N_TILE], F32, tag="slab", bufs=PREFETCH, align_bytes=64)
-                if index % 2 == 0:
-                    nc.scalar.copy(out=result[:], in_=acc[(s, n)][:])
+            last = (F_TILES - 1, HALVES - 1)
+
+            def rows_of(s):
+                return slice(s * P, (s + 1) * P)
+
+            def leave(s, n, copy):
+                if n == 0:
+                    result = pool.tile([P, N_TILE], F32, tag="slab", bufs=PREFETCH, align_bytes=64)
                 else:
-                    nc.vector.tensor_copy(out=result[:], in_=acc[(s, n)][:])
-                nc.sync.dma_start(
-                    out=out[s * P : (s + 1) * P, n * N_TILE : (n + 1) * N_TILE], in_=result[:]
-                )
+                    result = pool.tile([P, N_TILE], F32, tag="cube", bufs=4)
+                copy(out=result[:], in_=acc[(s, n)][:])
+                nc.sync.dma_start(out=out[rows_of(s), n * N_TILE : (n + 1) * N_TILE], in_=result[:])
+
+            take_grouped_peak(last[0], last[1], rows_of(0))
+            for s in range(B_TILES):
+                if s + 1 < B_TILES:
+                    take_grouped_peak(last[0], last[1], rows_of(s + 1))
+                quantise_half(last[0], last[1], rows_of(s))
+                multiply(SPLINE_PASSES - 1, [(s, n) for n in range(N_TILES)])
+                leave(s, 0, nc.scalar.copy)
+                if s < 2:
+                    leave(s, 1, nc.scalar.copy)
+            for s in range(2, B_TILES):
+                leave(s, 1, nc.vector.tensor_copy)

@@ -31,14 +31,14 @@ N_TILES = N_OUT // N_TILE
 FLOPS = 2 * BATCH * N_OUT * (N_IN + N_IN * N_BASIS)
 
 
-LOOKAHEAD = 2
-COMBINE_LAG = 2
+LOOKAHEAD = 3
+COMBINE_LAG = 3
 PREFETCH = 4
 HALF_O = O_TILES // 2
 CHUNKS = F_TILES * O_TILES
 FIRST_CHUNK_STEP = 3
 EARLY_TILES = 4
-SWITCH = EARLY_TILES * N_KNOTS - 2
+SWITCH = EARLY_TILES * N_KNOTS - 1
 STEPS = F_TILES * N_KNOTS
 
 
@@ -173,7 +173,7 @@ def tile_bsplinekanlayer_kernel(
         silu_codes = keep.tile([P, BASE_PASSES, BATCH], U32, align_bytes=64)
         silu_scales = keep.tile([P, BASE_PASSES, BATCH], U8, align_bytes=64)
         ssw_codes = keep.tile([P, SPLINE_PASSES, N_OUT], U32, align_bytes=64)
-        ssw_scales = keep.tile([P, SPLINE_PASSES, N_OUT], U8, align_bytes=64)
+        ssw_scales = keep.tile([P, SPLINE_PASSES // 4, N_OUT], U8, align_bytes=64)
 
         def three_term(c, j):
             return c < EARLY_TILES and j < PACK
@@ -190,7 +190,7 @@ def tile_bsplinekanlayer_kernel(
 
         def take_square(n):
             c, m = divmod(n, N_KNOTS)
-            square[n] = pool.tile([P, BATCH], F32, tag="square", bufs=3, name="square")
+            square[n] = pool.tile([P, BATCH], F32, tag="square", bufs=4, name="square")
             nc.scalar.activation(
                 out=square[n][:], in_=x_by_feature[:, c, :], func=ACT.Square,
                 bias=neg_knot[:, c, m : m + 1],
@@ -198,7 +198,7 @@ def tile_bsplinekanlayer_kernel(
 
         def take_cube(n):
             c, m = divmod(n, N_KNOTS)
-            cube[n] = pool.tile([P, BATCH], F32, tag="cube", bufs=4, name="cube")
+            cube[n] = pool.tile([P, BATCH], F32, tag="cube", bufs=5, name="cube")
             nc.vector.scalar_tensor_tensor(
                 out=cube[n][:], in0=x_by_feature[:, c, :], scalar=knot[:, c, m : m + 1],
                 in1=square[n][:], op0=ALU.subtract, op1=ALU.mult,
@@ -207,12 +207,12 @@ def tile_bsplinekanlayer_kernel(
         def take_sides(n):
             c, m = divmod(n, N_KNOTS)
             if m <= N_BASIS:
-                up[n] = pool.tile([P, BATCH], F32, tag="up", bufs=5, name="up")
+                up[n] = pool.tile([P, BATCH], F32, tag="up", bufs=6, name="up")
                 nc.scalar.activation(
                     out=up[n][:], in_=cube[n][:], func=ACT.Relu, scale=up_scale[:, c, m : m + 1]
                 )
             if m >= 3 and not three_term(c, m - 3):
-                down[n] = pool.tile([P, BATCH], F32, tag="down", bufs=4, name="down")
+                down[n] = pool.tile([P, BATCH], F32, tag="down", bufs=5, name="down")
                 nc.scalar.activation(
                     out=down[n][:], in_=cube[n][:], func=ACT.Relu,
                     scale=neg_down_scale[:, c, m - 3 : m - 2],
@@ -227,19 +227,25 @@ def tile_bsplinekanlayer_kernel(
         form_banks = {}
 
         def diagonal(scale):
-            tile = pool.tile([P, P], F32, tag="diagonal", bufs=3, name="diagonal")
-            nc.gpsimd.tensor_scalar(
-                out=tile[:], in0=ident_f32[:], scalar1=scale, scalar2=1.0, op0=ALU.mult, op1=ALU.mult
-            )
+            tile = pool.tile([P, P], F32, tag="diagonal", bufs=8, name="diagonal")
+            nc.scalar.activation(out=tile[:], in_=ident_f32[:], func=ACT.Copy, scale=scale)
             return tile
+
+        diagonals = {}
+
+        def take_diagonals(n):
+            c, m = divmod(n, N_KNOTS)
+            if three_term(c, m):
+                diagonals[(c, m)] = (
+                    diagonal(left_mix[:, c, m : m + 1]), diagonal(third_mix[:, c, m : m + 1])
+                )
 
         def combine_on_tensor(psum, n):
             c, m = divmod(n, N_KNOTS)
             j = m - 2
             if j < 0 or not three_term(c, j):
                 return
-            first = diagonal(left_mix[:, c, j : j + 1])
-            third = diagonal(third_mix[:, c, j : j + 1])
+            first, third = diagonals.pop((c, j))
             bank = psum.tile([P, BATCH], F32, tag="flip", bufs=8, name="form")
             nc.tensor.matmul(out=bank[:], lhsT=first[:], rhs=up[n - 2][:], start=True, stop=False)
             nc.tensor.matmul(out=bank[:], lhsT=minus_ident[:], rhs=up[n - 1][:], start=False, stop=False)
@@ -368,12 +374,15 @@ def tile_bsplinekanlayer_kernel(
                     op=ALU.mult,
                 )
 
+        def ssw_plane(k, cols):
+            return ssw_scales[4 * (k % 4) : P, k // 4, cols]
+
         def quantise_ssw(c, part):
             n_cols = slice(part * N_TILE, (part + 1) * N_TILE)
             for half in range(HALVES):
                 nc.vector.quantize_mx(
                     out=ssw_codes[:, c * HALVES + half, n_cols].bitcast(FP8X4),
-                    scales=ssw_scales[:, c * HALVES + half, n_cols],
+                    scales=ssw_plane(c * HALVES + half, n_cols),
                     in_=ssw_grouped[(c, part)][:, half].rearrange("p o t -> p (o t)"),
                 )
 
@@ -430,6 +439,7 @@ def tile_bsplinekanlayer_kernel(
                     take_grouped_peak(c, half, slice(0, BATCH))
                 elif kind == "regroup":
                     regroup(c, half)
+            take_diagonals(n - 1)
             if 0 <= n - COMBINE_LAG < STEPS:
                 combine(n - COMBINE_LAG)
             for kind, c, half in finish.get(n, []):
@@ -531,7 +541,7 @@ def tile_bsplinekanlayer_kernel(
                         lhsT=k_codes[:, s * P : (s + 1) * P].bitcast(FP8X4),
                         lhsT_scale=k_scales[:, s * P : (s + 1) * P],
                         rhs=ssw_codes[:, k, n * N_TILE : (n + 1) * N_TILE].bitcast(FP8X4),
-                        rhs_scale=ssw_scales[:, k, n * N_TILE : (n + 1) * N_TILE],
+                        rhs_scale=ssw_plane(k, slice(n * N_TILE, (n + 1) * N_TILE)),
                         start=(k == 0),
                         stop=(k == SPLINE_PASSES - 1),
                     )
@@ -557,7 +567,7 @@ def tile_bsplinekanlayer_kernel(
                 if n == 0:
                     result = pool.tile([P, N_TILE], F32, tag="slab", bufs=PREFETCH, align_bytes=64)
                 else:
-                    result = pool.tile([P, N_TILE], F32, tag="cube", bufs=4)
+                    result = pool.tile([P, N_TILE], F32, tag="cube", bufs=5)
                 copy(out=result[:], in_=acc[(s, n)][:])
                 nc.sync.dma_start(out=out[rows_of(s), n * N_TILE : (n + 1) * N_TILE], in_=result[:])
 

@@ -33,12 +33,16 @@ FLOPS = 2 * BATCH * N_OUT * (N_IN + N_IN * N_BASIS)
 
 LOOKAHEAD = 3
 COMBINE_LAG = 3
+FORM_LAG = 3
+TERMS = 3
+FORM_BASES = (0, 3, 4, 7)
+KEPT_KNOTS = (4, 7)
 PREFETCH = 4
 HALF_O = O_TILES // 2
 CHUNKS = F_TILES * O_TILES
 FIRST_CHUNK_STEP = 3
 EARLY_TILES = 4
-SWITCH = EARLY_TILES * N_KNOTS - 1
+SWITCH = EARLY_TILES * N_KNOTS + 5
 STEPS = F_TILES * N_KNOTS
 
 
@@ -84,17 +88,27 @@ def spline_constants(nc, consts, scratch, knot_bf):
     neg_down_scale = constant("neg_down_scale", N_BASIS + 1)
     left_mix = constant("left_mix", N_BASIS)
     right_mix = constant("right_mix", N_BASIS)
-    third_mix = constant("third_mix", PACK)
-    neg_outer = constant("neg_outer", PACK)
+    form_weight = constant("form_weight", N_KNOTS)
+    outer = constant("outer", len(FORM_BASES))
+
+    def third_weight(at, j, second_span, third_span):
+        weight = form_weight[:, :, at : at + 1]
+        other = temporary(1)
+        nc.vector.tensor_mul(out=weight, in0=h4[:, :, j : j + 1], in1=second_span)
+        nc.vector.tensor_mul(out=other, in0=third_span[0], in1=third_span[1])
+        nc.vector.tensor_mul(out=weight, in0=weight, in1=other)
 
     def rest():
         r4 = temporary(N_BASIS)
         nc.vector.reciprocal(out=r4, in_=h4)
         nc.vector.memset(left_mix[:, :, 0:1], 1.0)
         nc.vector.tensor_mul(out=left_mix[:, :, 1:8], in0=h1[:, :, 0:7], in1=r4[:, :, 0:7])
-        nc.vector.tensor_mul(out=third_mix[:], in0=h4[:, :, 0:4], in1=r2[:, :, 0:4])
-        nc.vector.tensor_mul(out=neg_outer[:], in0=h3[:, :, 2:6], in1=r4[:, :, 1:5])
-        nc.vector.tensor_mul(out=third_mix[:], in0=third_mix[:], in1=neg_outer[:])
+        for at, j in ((2, 0), (5, 3)):
+            third_weight(
+                at, j, r2[:, :, j : j + 1], (h3[:, :, j + 2 : j + 3], r4[:, :, j + 1 : j + 2])
+            )
+        nc.vector.tensor_copy(out=form_weight[:, :, 0:4:3], in_=left_mix[:, :, 0:4:3])
+        nc.vector.tensor_copy(out=outer[:, :, 2:4], in_=first_left[:, :, 4:8:3])
         first_right = temporary(N_BASIS + 1)
         nc.vector.tensor_mul(out=first_right, in0=r3, in1=r2[:, :, 1:10])
         down_ratio = temporary(N_BASIS)
@@ -103,11 +117,16 @@ def spline_constants(nc, consts, scratch, knot_bf):
         nc.vector.tensor_scalar_mul(out=first_right, in0=first_right, scalar1=-1.0)
         nc.vector.tensor_mul(out=neg_down_scale[:, :, 0:8], in0=first_right[:, :, 0:8], in1=down_ratio)
         nc.vector.tensor_copy(out=neg_down_scale[:, :, 8:9], in_=first_right[:, :, 8:9])
-        nc.vector.tensor_copy(out=neg_outer[:], in_=first_right[:, :, 1:5])
+        nc.vector.tensor_copy(out=outer[:, :, 0:2], in_=first_right[:, :, 1:5:3])
         nc.vector.memset(right_mix[:, :, 7:8], 1.0)
         nc.vector.tensor_mul(out=right_mix[:, :, 0:7], in0=h1[:, :, 4:11], in1=r4[:, :, 1:8])
+        for at, j in ((6, 4), (9, 7)):
+            third_weight(
+                at, j, r2[:, :, j + 2 : j + 3], (h3[:, :, j - 1 : j], r4[:, :, j - 1 : j])
+            )
+        nc.vector.tensor_copy(out=form_weight[:, :, 8:12:3], in_=right_mix[:, :, 4:8:3])
 
-    return knot, neg_knot, up_scale, neg_down_scale, left_mix, right_mix, third_mix, neg_outer, rest
+    return knot, neg_knot, up_scale, neg_down_scale, left_mix, right_mix, form_weight, outer, rest
 
 def tile_bsplinekanlayer_kernel(
     tc, x, base_weight_words, base_weight_scales, spline_weight, spline_scaler, grid, out
@@ -123,8 +142,8 @@ def tile_bsplinekanlayer_kernel(
         x_in = x.rearrange("(s p) i -> p s i", p=P)
         knot_bf = consts.tile([P, F_TILES, N_KNOTS], BF16)
         nc.scalar.dma_start(out=knot_bf[:], in_=grid.rearrange("(c p) m -> p c m", p=P))
-        for s in range(B_TILES):
-            nc.sync.dma_start(out=x_rows[:, s, :], in_=x_in[:, s, :])
+        for cols in (slice(0, 2 * P), slice(2 * P, N_IN)):
+            nc.sync.dma_start(out=x_rows[:, :, cols], in_=x_in[:, :, cols])
 
         scaler_rows = {}
 
@@ -137,6 +156,7 @@ def tile_bsplinekanlayer_kernel(
             scaler_rows[c] = rows
 
         slabs = {}
+        waiting_loads = []
 
         def load_slab(c, part):
             slab = pool.tile([P, HALF_O, P * N_BASIS], BF16, tag="slab", bufs=PREFETCH, align_bytes=64)
@@ -165,7 +185,7 @@ def tile_bsplinekanlayer_kernel(
 
         scratch = pool.tile([P, 1024], F32, tag="grouped", bufs=2, align_bytes=64)
         (
-            knot, neg_knot, up_scale, neg_down_scale, left_mix, right_mix, third_mix, neg_outer,
+            knot, neg_knot, up_scale, neg_down_scale, left_mix, right_mix, form_weight, outer,
             remaining_constants,
         ) = spline_constants(nc, consts, scratch, knot_bf)
 
@@ -176,7 +196,7 @@ def tile_bsplinekanlayer_kernel(
         ssw_scales = keep.tile([P, SPLINE_PASSES // 4, N_OUT], U8, align_bytes=64)
 
         def three_term(c, j):
-            return c < EARLY_TILES and j < PACK
+            return 0 <= c < EARLY_TILES and j in FORM_BASES
 
         square = {}
         cube = {}
@@ -198,7 +218,10 @@ def tile_bsplinekanlayer_kernel(
 
         def take_cube(n):
             c, m = divmod(n, N_KNOTS)
-            cube[n] = pool.tile([P, BATCH], F32, tag="cube", bufs=5, name="cube")
+            if c < EARLY_TILES and m in KEPT_KNOTS:
+                cube[n] = pool.tile([P, BATCH], F32, tag="kept", bufs=2, name="cube")
+            else:
+                cube[n] = pool.tile([P, BATCH], F32, tag="cube", bufs=3, name="cube")
             nc.vector.scalar_tensor_tensor(
                 out=cube[n][:], in0=x_by_feature[:, c, :], scalar=knot[:, c, m : m + 1],
                 in1=square[n][:], op0=ALU.subtract, op1=ALU.mult,
@@ -206,12 +229,12 @@ def tile_bsplinekanlayer_kernel(
 
         def take_sides(n):
             c, m = divmod(n, N_KNOTS)
-            if m <= N_BASIS:
+            if m <= N_BASIS - (1 if c < EARLY_TILES else 0):
                 up[n] = pool.tile([P, BATCH], F32, tag="up", bufs=6, name="up")
                 nc.scalar.activation(
                     out=up[n][:], in_=cube[n][:], func=ACT.Relu, scale=up_scale[:, c, m : m + 1]
                 )
-            if m >= 3 and not three_term(c, m - 3):
+            if m >= 3 + (1 if c < EARLY_TILES else 0):
                 down[n] = pool.tile([P, BATCH], F32, tag="down", bufs=5, name="down")
                 nc.scalar.activation(
                     out=down[n][:], in_=cube[n][:], func=ACT.Relu,
@@ -225,32 +248,43 @@ def tile_bsplinekanlayer_kernel(
             return store[key][:, j % PACK, :]
 
         form_banks = {}
-
-        def diagonal(scale):
-            tile = pool.tile([P, P], F32, tag="diagonal", bufs=8, name="diagonal")
-            nc.scalar.activation(out=tile[:], in_=ident_f32[:], func=ACT.Copy, scale=scale)
-            return tile
-
         diagonals = {}
 
-        def take_diagonals(n):
+        def take_diagonal(n):
             c, m = divmod(n, N_KNOTS)
-            if three_term(c, m):
-                diagonals[(c, m)] = (
-                    diagonal(left_mix[:, c, m : m + 1]), diagonal(third_mix[:, c, m : m + 1])
+            if 0 <= c < EARLY_TILES and m % TERMS != 1:
+                tile = pool.tile([P, P], F32, tag="diagonal", bufs=8, name="diagonal")
+                nc.scalar.activation(
+                    out=tile[:], in_=ident_f32[:], func=ACT.Copy, scale=form_weight[:, c, m : m + 1]
                 )
+                diagonals[n] = tile
 
-        def combine_on_tensor(psum, n):
+        def add_term(psum, n):
             c, m = divmod(n, N_KNOTS)
-            j = m - 2
-            if j < 0 or not three_term(c, j):
+            if not 0 <= c < EARLY_TILES:
                 return
-            first, third = diagonals.pop((c, j))
-            bank = psum.tile([P, BATCH], F32, tag="flip", bufs=8, name="form")
-            nc.tensor.matmul(out=bank[:], lhsT=first[:], rhs=up[n - 2][:], start=True, stop=False)
-            nc.tensor.matmul(out=bank[:], lhsT=minus_ident[:], rhs=up[n - 1][:], start=False, stop=False)
-            nc.tensor.matmul(out=bank[:], lhsT=third[:], rhs=up[n][:], start=False, stop=True)
-            form_banks[(c, j)] = bank
+            form, term = divmod(m, TERMS)
+            if term == 0:
+                form_banks[(c, form)] = psum.tile([P, BATCH], F32, tag="flip", bufs=8, name="form")
+            nc.tensor.matmul(
+                out=form_banks[(c, form)][:],
+                lhsT=minus_ident[:] if term == 1 else diagonals[n][:],
+                rhs=(up if form < 2 else down)[n][:],
+                start=(term == 0),
+                stop=(term == TERMS - 1),
+            )
+
+        def take_minimum(n):
+            c, m = divmod(n, N_KNOTS)
+            form, term = divmod(m, TERMS)
+            if not (0 <= c < EARLY_TILES and term == TERMS - 1):
+                return
+            outer_cube = cube[c * N_KNOTS + KEPT_KNOTS[form % 2]]
+            nc.vector.scalar_tensor_tensor(
+                out=half_tile(peak, c, FORM_BASES[form], "peak"), in0=outer_cube[:],
+                scalar=outer[:, c, form : form + 1], in1=form_banks[(c, form)][:],
+                op0=ALU.mult, op1=ALU.min,
+            )
 
         def combine(n):
             c, m = divmod(n, N_KNOTS)
@@ -261,15 +295,7 @@ def tile_bsplinekanlayer_kernel(
                     scalar=left_mix[:, c, j : j + 1], in1=up[n][:],
                     op0=ALU.mult, op1=ALU.subtract,
                 )
-            if m >= 4 and three_term(c, m - 4):
-                j = m - 4
-                if j == 0:
-                    peak[(c, 0)] = pool.tile([P, PACK, BATCH], BF16, tag="peak", bufs=2, name="peak")
-                nc.vector.scalar_tensor_tensor(
-                    out=peak[(c, 0)][:, j, :], in0=cube[n][:], scalar=neg_outer[:, c, j : j + 1],
-                    in1=form_banks[(c, j)][:], op0=ALU.mult, op1=ALU.min,
-                )
-            elif m >= 4:
+            if m >= 4 and not three_term(c, m - 4):
                 j = m - 4
                 nc.vector.scalar_tensor_tensor(
                     out=half_tile(right, c, j, "right"), in0=down[n][:],
@@ -278,9 +304,11 @@ def tile_bsplinekanlayer_kernel(
                 )
 
         def take_peak(c, half):
-            peak[(c, half)] = pool.tile([P, PACK, BATCH], BF16, tag="peak", bufs=2, name="peak")
+            planes = slice(1, 3) if c < EARLY_TILES else slice(0, PACK)
+            half_tile(peak, c, half * PACK, "peak")
             nc.vector.tensor_tensor(
-                out=peak[(c, half)][:], in0=left[(c, half)][:], in1=right[(c, half)][:], op=ALU.max
+                out=peak[(c, half)][:, planes, :], in0=left[(c, half)][:, planes, :],
+                in1=right[(c, half)][:, planes, :], op=ALU.max,
             )
 
         def regroup(c, half):
@@ -289,7 +317,7 @@ def tile_bsplinekanlayer_kernel(
             )
             to = grouped[(c, half)][:].rearrange("p (g i) t -> p g t i", i=4)
             of = peak[(c, half)][:].rearrange("p t (g i) -> p g t i", i=4)
-            if half == 0 and three_term(c, 0):
+            if c < EARLY_TILES:
                 nc.scalar.activation(out=to, in_=of, func=ACT.Relu)
             else:
                 nc.scalar.copy(out=to, in_=of)
@@ -309,8 +337,8 @@ def tile_bsplinekanlayer_kernel(
         def quantise_half(c, half, cols=slice(0, BATCH)):
             k = c * HALVES + half
             if k not in codes:
-                k_codes = pool.tile([P, BATCH], U32, tag="k_codes", bufs=6, align_bytes=64, name="k_codes")
-                k_scales = pool.tile([P, BATCH], U8, tag="k_scales", bufs=6, align_bytes=64, name="k_scales")
+                k_codes = pool.tile([P, BATCH], U32, tag="k_codes", bufs=7, align_bytes=64, name="k_codes")
+                k_scales = pool.tile([P, BATCH], U8, tag="k_scales", bufs=7, align_bytes=64, name="k_scales")
                 codes[k] = (k_codes, k_scales)
             nc.vector.quantize_mx(
                 out=codes[k][0][:, cols].bitcast(FP8X4), scales=codes[k][1][:, cols],
@@ -347,7 +375,9 @@ def tile_bsplinekanlayer_kernel(
             chunk_words[k] = words
             if r == HALF_O - 1:
                 following = 2 * c + part + PREFETCH
-                if following < 2 * F_TILES:
+                if following < 2 * F_TILES and (1, 1) not in slabs:
+                    waiting_loads.append(following)
+                elif following < 2 * F_TILES:
                     load_slab(following // 2, following % 2)
                 elif following == 2 * F_TILES + 1:
                     load_w()
@@ -408,14 +438,14 @@ def tile_bsplinekanlayer_kernel(
             w_tiles["scales"] = w_scales
 
         def chunks_done(n):
-            return max(0, min(CHUNKS, (n + 1 - FIRST_CHUNK_STEP) * CHUNKS // (SWITCH - 3 - FIRST_CHUNK_STEP)))
+            return max(0, min(CHUNKS, (n + 1 - FIRST_CHUNK_STEP) * CHUNKS // (SWITCH - 4 - FIRST_CHUNK_STEP)))
 
         finish = {}
         for c in range(F_TILES):
             for half in range(HALVES):
                 ready = c * N_KNOTS + (7 if half == 0 else 11) + COMBINE_LAG
-                if half == 0 and three_term(c, 0):
-                    steps = (("regroup", 1), ("quantise", 3))
+                if c < EARLY_TILES and half == 1:
+                    steps = (("peak", 0), ("regroup", 3), ("quantise", 5))
                 elif c < EARLY_TILES or (half == 0 and c < F_TILES - 1):
                     steps = (("peak", 1), ("regroup", 2), ("quantise", 4))
                 elif half == 0 or c < F_TILES - 1:
@@ -439,7 +469,8 @@ def tile_bsplinekanlayer_kernel(
                     take_grouped_peak(c, half, slice(0, BATCH))
                 elif kind == "regroup":
                     regroup(c, half)
-            take_diagonals(n - 1)
+            take_minimum(n - FORM_LAG - 2)
+            take_diagonal(n - 1)
             if 0 <= n - COMBINE_LAG < STEPS:
                 combine(n - COMBINE_LAG)
             for kind, c, half in finish.get(n, []):
@@ -456,20 +487,30 @@ def tile_bsplinekanlayer_kernel(
                             x_rows[:, s, (2 * pair + c) * P : (2 * pair + c + 1) * P],
                             ident_bf[:],
                         )
-                if pair in (1, 2):
+                if pair == 0:
+                    nc.scalar.copy(out=x_by_feature[:, 0, :], in_=flipped[:, 0, :])
+                    for n in range(LOOKAHEAD):
+                        take_square(n)
+                    nc.vector.tensor_copy(out=x_by_feature[:, 1, :], in_=flipped[:, 1, :])
+                elif pair < 3:
                     nc.vector.tensor_copy(out=x_by_feature[:, 2 * pair : 2 * pair + 2, :], in_=flipped[:])
                 else:
                     nc.scalar.copy(out=x_by_feature[:, 2 * pair : 2 * pair + 2, :], in_=flipped[:])
-                if pair == 0:
-                    for n in range(LOOKAHEAD):
-                        take_square(n)
             flip_scaler(psum_flip, 0)
 
-            silu_grouped = pool.tile(
-                [P, HALVES, N_TILE, PACK], BF16, tag="ssw_grouped", bufs=2, align_bytes=64
-            )
+            silu_grouped = {}
+
+            def quantise_silu(g):
+                nc.vector.quantize_mx(
+                    out=silu_codes[:, g, :].bitcast(FP8X4), scales=silu_scales[:, g, :],
+                    in_=silu_grouped[g][:].rearrange("p b t -> p (b t)"),
+                )
 
             def silu_piece(g, pair):
+                if pair == 0:
+                    silu_grouped[g] = pool.tile(
+                        [P, BATCH, PACK], BF16, tag="grouped", bufs=2, align_bytes=64, name="silu_grouped"
+                    )
                 words = psum_flip.tile([P, 2, 2, P], F32, tag="flip", bufs=8)
                 for u in range(2):
                     for s in range(2):
@@ -479,7 +520,7 @@ def tile_bsplinekanlayer_kernel(
                             ident_f32[:],
                         )
                 nc.scalar.activation(
-                    out=silu_grouped[:, g, 2 * pair * P : 2 * (pair + 1) * P, :].rearrange(
+                    out=silu_grouped[g][:, 2 * pair * P : 2 * (pair + 1) * P, :].rearrange(
                         "p b (u e) -> p b u e", e=2
                     ),
                     in_=words[:].bitcast(BF16).rearrange("p u s (b e) -> p (s b) u e", e=2),
@@ -487,32 +528,31 @@ def tile_bsplinekanlayer_kernel(
                 )
 
             for n in range(SWITCH):
-                for k in range(chunks_done(n), chunks_done(n + 1)):
+                if n % 2 == 1 and n < 8:
+                    silu_piece(n // 4, n // 2 % 2)
+                    if n == 7:
+                        load_slab(1, 1)
+                        for half in waiting_loads:
+                            load_slab(half // 2, half % 2)
+                for k in range(chunks_done(n + 1), chunks_done(n + 2)):
                     flip_chunk(psum_flip, k)
                     c, s = divmod(k, O_TILES)
                     if s == HALF_O + 2 and c + 1 < F_TILES:
                         flip_scaler(psum_flip, c + 1)
                         if c + 2 < F_TILES:
                             load_scaler(c + 2)
-                combine_on_tensor(psum_flip, n - COMBINE_LAG)
-                if n < 4:
-                    silu_piece(n // 2, n % 2)
-                    if n == 3:
-                        load_slab(1, 1)
-                if n == 6:
-                    nc.vector.quantize_mx(
-                        out=silu_codes[:].rearrange("p g b -> p (g b)").bitcast(FP8X4),
-                        scales=silu_scales[:].rearrange("p g b -> p (g b)"),
-                        in_=silu_grouped[:].rearrange("p g b t -> p (g b t)"),
-                    )
+                add_term(psum_flip, n - FORM_LAG)
                 run_step(n)
+                if n in (5, 9):
+                    quantise_silu((n - 5) // 4)
                 if n == 0:
                     remaining_constants()
                 for k in range(chunks_done(n - 1), chunks_done(n)):
                     scale_chunk(k)
                     if k % HALF_O == 0 and k > 0:
                         quantise_ssw((k - 1) // O_TILES, (k - 1) // HALF_O % 2)
-            quantise_ssw(F_TILES - 1, 1)
+                if chunks_done(n - 2) < CHUNKS == chunks_done(n - 1):
+                    quantise_ssw(F_TILES - 1, 1)
 
         with tc.psum_pool(name="psum_acc", bufs=1) as psum_acc:
             groups = [(s, n) for s in range(B_TILES) for n in range(N_TILES)]
@@ -554,10 +594,6 @@ def tile_bsplinekanlayer_kernel(
                 if n == SWITCH:
                     multiply_base()
                 run_step(n)
-            while multiplied in codes:
-                multiply(multiplied)
-                multiplied += 1
-
             last = (F_TILES - 1, HALVES - 1)
 
             def rows_of(s):
@@ -567,7 +603,7 @@ def tile_bsplinekanlayer_kernel(
                 if n == 0:
                     result = pool.tile([P, N_TILE], F32, tag="slab", bufs=PREFETCH, align_bytes=64)
                 else:
-                    result = pool.tile([P, N_TILE], F32, tag="cube", bufs=5)
+                    result = pool.tile([P, N_TILE], F32, tag="cube", bufs=3)
                 copy(out=result[:], in_=acc[(s, n)][:])
                 nc.sync.dma_start(out=out[rows_of(s), n * N_TILE : (n + 1) * N_TILE], in_=result[:])
 
@@ -576,7 +612,8 @@ def tile_bsplinekanlayer_kernel(
                 if s + 1 < B_TILES:
                     take_grouped_peak(last[0], last[1], rows_of(s + 1))
                 quantise_half(last[0], last[1], rows_of(s))
-                multiply(SPLINE_PASSES - 1, [(s, n) for n in range(N_TILES)])
+                for k in range(multiplied, SPLINE_PASSES):
+                    multiply(k, [(s, n) for n in range(N_TILES)])
                 leave(s, 0, nc.scalar.copy)
                 if s < 2:
                     leave(s, 1, nc.scalar.copy)

@@ -35,8 +35,8 @@ LOOKAHEAD = 3
 COMBINE_LAG = 3
 FORM_LAG = 3
 TERMS = 3
-FORM_BASES = (0, 3, 4, 7)
-KEPT_KNOTS = (4, 7)
+FORMS = ((0, 0, 4), (3, 3, 7), (4, 6, 4), (7, 9, 7), (1, 1, 5))
+COPIED = (0, 1)
 PREFETCH = 4
 HALF_O = O_TILES // 2
 CHUNKS = F_TILES * O_TILES
@@ -88,43 +88,45 @@ def spline_constants(nc, consts, scratch, knot_bf):
     neg_down_scale = constant("neg_down_scale", N_BASIS + 1)
     left_mix = constant("left_mix", N_BASIS)
     right_mix = constant("right_mix", N_BASIS)
-    form_weight = constant("form_weight", N_KNOTS)
-    outer = constant("outer", len(FORM_BASES))
+    form_weight = constant("form_weight", TERMS * len(FORMS))
+    outer = constant("outer", len(FORMS))
 
     def third_weight(at, j, second_span, third_span):
         weight = form_weight[:, :, at : at + 1]
         other = temporary(1)
-        nc.vector.tensor_mul(out=weight, in0=h4[:, :, j : j + 1], in1=second_span)
-        nc.vector.tensor_mul(out=other, in0=third_span[0], in1=third_span[1])
-        nc.vector.tensor_mul(out=weight, in0=weight, in1=other)
+        nc.gpsimd.tensor_mul(out=weight, in0=h4[:, :, j : j + 1], in1=second_span)
+        nc.gpsimd.tensor_mul(out=other, in0=third_span[0], in1=third_span[1])
+        nc.gpsimd.tensor_mul(out=weight, in0=weight, in1=other)
 
     def rest():
         r4 = temporary(N_BASIS)
         nc.vector.reciprocal(out=r4, in_=h4)
-        nc.vector.memset(left_mix[:, :, 0:1], 1.0)
-        nc.vector.tensor_mul(out=left_mix[:, :, 1:8], in0=h1[:, :, 0:7], in1=r4[:, :, 0:7])
-        for at, j in ((2, 0), (5, 3)):
+        nc.gpsimd.memset(left_mix[:, :, 0:1], 1.0)
+        nc.gpsimd.tensor_mul(out=left_mix[:, :, 1:8], in0=h1[:, :, 0:7], in1=r4[:, :, 0:7])
+        nc.gpsimd.tensor_copy(out=form_weight[:, :, 0:4:3], in_=left_mix[:, :, 0:4:3])
+        nc.gpsimd.tensor_copy(out=form_weight[:, :, 12:13], in_=left_mix[:, :, 1:2])
+        for at, j in ((2, 0), (5, 3), (14, 1)):
             third_weight(
                 at, j, r2[:, :, j : j + 1], (h3[:, :, j + 2 : j + 3], r4[:, :, j + 1 : j + 2])
             )
-        nc.vector.tensor_copy(out=form_weight[:, :, 0:4:3], in_=left_mix[:, :, 0:4:3])
-        nc.vector.tensor_copy(out=outer[:, :, 2:4], in_=first_left[:, :, 4:8:3])
+        nc.gpsimd.tensor_copy(out=outer[:, :, 2:4], in_=first_left[:, :, 4:8:3])
         first_right = temporary(N_BASIS + 1)
-        nc.vector.tensor_mul(out=first_right, in0=r3, in1=r2[:, :, 1:10])
+        nc.gpsimd.tensor_mul(out=first_right, in0=r3, in1=r2[:, :, 1:10])
         down_ratio = temporary(N_BASIS)
-        nc.vector.tensor_mul(out=down_ratio, in0=h4, in1=r1[:, :, 3:11])
-        nc.vector.tensor_mul(out=first_right, in0=first_right, in1=r1[:, :, 2:11])
-        nc.vector.tensor_scalar_mul(out=first_right, in0=first_right, scalar1=-1.0)
-        nc.vector.tensor_mul(out=neg_down_scale[:, :, 0:8], in0=first_right[:, :, 0:8], in1=down_ratio)
-        nc.vector.tensor_copy(out=neg_down_scale[:, :, 8:9], in_=first_right[:, :, 8:9])
-        nc.vector.tensor_copy(out=outer[:, :, 0:2], in_=first_right[:, :, 1:5:3])
-        nc.vector.memset(right_mix[:, :, 7:8], 1.0)
-        nc.vector.tensor_mul(out=right_mix[:, :, 0:7], in0=h1[:, :, 4:11], in1=r4[:, :, 1:8])
+        nc.gpsimd.tensor_mul(out=down_ratio, in0=h4, in1=r1[:, :, 3:11])
+        nc.gpsimd.tensor_mul(out=first_right, in0=first_right, in1=r1[:, :, 2:11])
+        nc.gpsimd.tensor_scalar_mul(out=first_right, in0=first_right, scalar1=-1.0)
+        nc.gpsimd.tensor_mul(out=neg_down_scale[:, :, 0:8], in0=first_right[:, :, 0:8], in1=down_ratio)
+        nc.gpsimd.tensor_copy(out=neg_down_scale[:, :, 8:9], in_=first_right[:, :, 8:9])
+        nc.gpsimd.tensor_copy(out=outer[:, :, 0:2], in_=first_right[:, :, 1:5:3])
+        nc.gpsimd.tensor_copy(out=outer[:, :, 4:5], in_=first_right[:, :, 2:3])
+        nc.gpsimd.memset(right_mix[:, :, 7:8], 1.0)
+        nc.gpsimd.tensor_mul(out=right_mix[:, :, 0:7], in0=h1[:, :, 4:11], in1=r4[:, :, 1:8])
         for at, j in ((6, 4), (9, 7)):
             third_weight(
                 at, j, r2[:, :, j + 2 : j + 3], (h3[:, :, j - 1 : j], r4[:, :, j - 1 : j])
             )
-        nc.vector.tensor_copy(out=form_weight[:, :, 8:12:3], in_=right_mix[:, :, 4:8:3])
+        nc.gpsimd.tensor_copy(out=form_weight[:, :, 8:12:3], in_=right_mix[:, :, 4:8:3])
 
     return knot, neg_knot, up_scale, neg_down_scale, left_mix, right_mix, form_weight, outer, rest
 
@@ -195,8 +197,25 @@ def tile_bsplinekanlayer_kernel(
         ssw_codes = keep.tile([P, SPLINE_PASSES, N_OUT], U32, align_bytes=64)
         ssw_scales = keep.tile([P, SPLINE_PASSES // 4, N_OUT], U8, align_bytes=64)
 
+        def forms_of(c):
+            if not 0 <= c < EARLY_TILES:
+                return ()
+            return range(len(FORMS) if c < EARLY_TILES - 1 else len(FORMS) - 1)
+
         def three_term(c, j):
-            return 0 <= c < EARLY_TILES and j in FORM_BASES
+            return any(FORMS[form][0] == j for form in forms_of(c))
+
+        def terms_of(n):
+            c, m = divmod(n, N_KNOTS)
+            return [(form, m - FORMS[form][1]) for form in forms_of(c) if 0 <= m - FORMS[form][1] < TERMS]
+
+        def kept(c, m):
+            return any(FORMS[form][2] == m for form in forms_of(c))
+
+        def needs_down(c, m):
+            if c >= EARLY_TILES:
+                return m >= 3
+            return m >= 6 or any(m >= 4 and not three_term(c, j) for j in (m - 4, m - 3) if j >= 0)
 
         square = {}
         cube = {}
@@ -218,8 +237,8 @@ def tile_bsplinekanlayer_kernel(
 
         def take_cube(n):
             c, m = divmod(n, N_KNOTS)
-            if c < EARLY_TILES and m in KEPT_KNOTS:
-                cube[n] = pool.tile([P, BATCH], F32, tag="kept", bufs=2, name="cube")
+            if kept(c, m):
+                cube[n] = pool.tile([P, BATCH], F32, tag="kept", bufs=3, name="cube")
             else:
                 cube[n] = pool.tile([P, BATCH], F32, tag="cube", bufs=3, name="cube")
             nc.vector.scalar_tensor_tensor(
@@ -230,11 +249,11 @@ def tile_bsplinekanlayer_kernel(
         def take_sides(n):
             c, m = divmod(n, N_KNOTS)
             if m <= N_BASIS - (1 if c < EARLY_TILES else 0):
-                up[n] = pool.tile([P, BATCH], F32, tag="up", bufs=6, name="up")
+                up[n] = pool.tile([P, BATCH], F32, tag="up", bufs=5, name="up")
                 nc.scalar.activation(
                     out=up[n][:], in_=cube[n][:], func=ACT.Relu, scale=up_scale[:, c, m : m + 1]
                 )
-            if m >= 3 + (1 if c < EARLY_TILES else 0):
+            if needs_down(c, m):
                 down[n] = pool.tile([P, BATCH], F32, tag="down", bufs=5, name="down")
                 nc.scalar.activation(
                     out=down[n][:], in_=cube[n][:], func=ACT.Relu,
@@ -251,40 +270,56 @@ def tile_bsplinekanlayer_kernel(
         diagonals = {}
 
         def take_diagonal(n):
-            c, m = divmod(n, N_KNOTS)
-            if 0 <= c < EARLY_TILES and m % TERMS != 1:
-                tile = pool.tile([P, P], F32, tag="diagonal", bufs=8, name="diagonal")
-                nc.scalar.activation(
-                    out=tile[:], in_=ident_f32[:], func=ACT.Copy, scale=form_weight[:, c, m : m + 1]
-                )
-                diagonals[n] = tile
+            for form, term in terms_of(n):
+                if term != 1:
+                    w = TERMS * form + term
+                    tile = pool.tile([P, P], F32, tag="diagonal", bufs=8, name="diagonal")
+                    nc.scalar.activation(
+                        out=tile[:], in_=ident_f32[:], func=ACT.Copy,
+                        scale=form_weight[:, n // N_KNOTS, w : w + 1],
+                    )
+                    diagonals[(n, form)] = tile
 
         def add_term(psum, n):
+            c = n // N_KNOTS
+            for form, term in terms_of(n):
+                if term == 0:
+                    form_banks[(c, form)] = psum.tile([P, BATCH], F32, tag="flip", bufs=8, name="form")
+                nc.tensor.matmul(
+                    out=form_banks[(c, form)][:],
+                    lhsT=minus_ident[:] if term == 1 else diagonals[(n, form)][:],
+                    rhs=(down if FORMS[form][1] >= 6 else up)[n][:],
+                    start=(term == 0),
+                    stop=(term == TERMS - 1),
+                )
+
+        def copy_form(n):
+            c = n // N_KNOTS
+            for form, term in terms_of(n):
+                if term == TERMS - 1 and form in COPIED:
+                    nc.scalar.copy(
+                        out=half_tile(left, c, FORMS[form][0], "left"), in_=form_banks[(c, form)][:]
+                    )
+
+        def copy_outer(n):
             c, m = divmod(n, N_KNOTS)
-            if not 0 <= c < EARLY_TILES:
-                return
-            form, term = divmod(m, TERMS)
-            if term == 0:
-                form_banks[(c, form)] = psum.tile([P, BATCH], F32, tag="flip", bufs=8, name="form")
-            nc.tensor.matmul(
-                out=form_banks[(c, form)][:],
-                lhsT=minus_ident[:] if term == 1 else diagonals[n][:],
-                rhs=(up if form < 2 else down)[n][:],
-                start=(term == 0),
-                stop=(term == TERMS - 1),
-            )
+            for form in forms_of(c):
+                if form in COPIED and FORMS[form][2] == m:
+                    nc.scalar.activation(
+                        out=half_tile(right, c, FORMS[form][0], "right"), in_=cube[n][:],
+                        func=ACT.Relu, scale=outer[:, c, form : form + 1],
+                    )
 
         def take_minimum(n):
-            c, m = divmod(n, N_KNOTS)
-            form, term = divmod(m, TERMS)
-            if not (0 <= c < EARLY_TILES and term == TERMS - 1):
-                return
-            outer_cube = cube[c * N_KNOTS + KEPT_KNOTS[form % 2]]
-            nc.vector.scalar_tensor_tensor(
-                out=half_tile(peak, c, FORM_BASES[form], "peak"), in0=outer_cube[:],
-                scalar=outer[:, c, form : form + 1], in1=form_banks[(c, form)][:],
-                op0=ALU.mult, op1=ALU.min,
-            )
+            c = n // N_KNOTS
+            for form, term in terms_of(n):
+                if term == TERMS - 1 and form not in COPIED:
+                    j, first_knot, outer_knot = FORMS[form]
+                    nc.vector.scalar_tensor_tensor(
+                        out=half_tile(peak, c, j, "peak"), in0=cube[c * N_KNOTS + outer_knot][:],
+                        scalar=outer[:, c, form : form + 1], in1=form_banks[(c, form)][:],
+                        op0=ALU.mult, op1=ALU.min,
+                    )
 
         def combine(n):
             c, m = divmod(n, N_KNOTS)
@@ -304,12 +339,16 @@ def tile_bsplinekanlayer_kernel(
                 )
 
         def take_peak(c, half):
-            planes = slice(1, 3) if c < EARLY_TILES else slice(0, PACK)
+            rest = [t for t in range(PACK) if not three_term(c, half * PACK + t)]
             half_tile(peak, c, half * PACK, "peak")
-            nc.vector.tensor_tensor(
-                out=peak[(c, half)][:, planes, :], in0=left[(c, half)][:, planes, :],
-                in1=right[(c, half)][:, planes, :], op=ALU.max,
-            )
+            parts = [(slice(rest[0], rest[-1] + 1), ALU.max)]
+            if c < EARLY_TILES and half == 0:
+                parts.append((slice(0, PACK, PACK - 1), ALU.min))
+            for planes, op in parts:
+                nc.vector.tensor_tensor(
+                    out=peak[(c, half)][:, planes, :], in0=left[(c, half)][:, planes, :],
+                    in1=right[(c, half)][:, planes, :], op=op,
+                )
 
         def regroup(c, half):
             grouped[(c, half)] = pool.tile(
@@ -349,16 +388,22 @@ def tile_bsplinekanlayer_kernel(
         chunk_words = {}
         ssw_grouped = {}
 
+        scaler_banks = {}
+
         def flip_scaler(psum_flip, c):
             bank = psum_flip.tile([P, N_OUT], BF16, tag="flip", bufs=8, name="bank")
             for s in range(O_TILES):
                 nc.tensor.transpose(
                     bank[:, s * P : (s + 1) * P], scaler_rows[c][:, s, :], ident_bf[:]
                 )
+            scaler_banks[c] = bank
+
+        def copy_pairs(c, copy):
+            bank = scaler_banks.pop(c)
             for part in range(2):
                 cols = slice(part * N_TILE, (part + 1) * N_TILE)
                 pairs[(c, part)] = pool.tile([P, N_TILE, 2], BF16, tag="pairs", bufs=3, name="pairs")
-                nc.scalar.copy(
+                copy(
                     out=pairs[(c, part)][:],
                     in_=bank[:, cols].unsqueeze(2).to_broadcast([P, N_TILE, 2]),
                 )
@@ -391,18 +436,12 @@ def tile_bsplinekanlayer_kernel(
                     name="ssw_grouped",
                 )
             o_cols = slice(r * P, (r + 1) * P)
-            by_half = chunk_words[k][:].bitcast(BF16).rearrange(
-                "p (h u) (o e) -> p h o u e", u=2, e=2
+            nc.vector.tensor_tensor(
+                out=ssw_grouped[(c, part)][:, :, o_cols, :].rearrange("p h o t -> p o h t"),
+                in0=chunk_words[k][:].bitcast(BF16).rearrange("p w (o e) -> p o w e", e=2),
+                in1=pairs[(c, part)][:, o_cols, :].unsqueeze(2).to_broadcast([P, P, PACK, 2]),
+                op=ALU.mult,
             )
-            for half in range(HALVES):
-                nc.vector.tensor_tensor(
-                    out=ssw_grouped[(c, part)][:, half, o_cols, :].rearrange(
-                        "p o (u e) -> p o u e", e=2
-                    ),
-                    in0=by_half[:, half],
-                    in1=pairs[(c, part)][:, o_cols, :].unsqueeze(2).to_broadcast([P, P, 2, 2]),
-                    op=ALU.mult,
-                )
 
         def ssw_plane(k, cols):
             return ssw_scales[4 * (k % 4) : P, k // 4, cols]
@@ -470,6 +509,8 @@ def tile_bsplinekanlayer_kernel(
                 elif kind == "regroup":
                     regroup(c, half)
             take_minimum(n - FORM_LAG - 2)
+            copy_outer(n - 1)
+            copy_form(n - FORM_LAG - 2)
             take_diagonal(n - 1)
             if 0 <= n - COMBINE_LAG < STEPS:
                 combine(n - COMBINE_LAG)
@@ -478,6 +519,8 @@ def tile_bsplinekanlayer_kernel(
                     quantise_half(c, half)
 
         with tc.psum_pool(name="psum_flip", bufs=8) as psum_flip:
+            late_copies = []
+            scalers_flipped = []
             for pair in range(F_TILES // 2):
                 flipped = psum_flip.tile([P, 2, BATCH], BF16, tag="flip", bufs=8)
                 for c in range(2):
@@ -492,10 +535,11 @@ def tile_bsplinekanlayer_kernel(
                     for n in range(LOOKAHEAD):
                         take_square(n)
                     nc.vector.tensor_copy(out=x_by_feature[:, 1, :], in_=flipped[:, 1, :])
-                elif pair < 3:
+                elif pair == 1:
                     nc.vector.tensor_copy(out=x_by_feature[:, 2 * pair : 2 * pair + 2, :], in_=flipped[:])
                 else:
-                    nc.scalar.copy(out=x_by_feature[:, 2 * pair : 2 * pair + 2, :], in_=flipped[:])
+                    late_copies.append((pair, flipped))
+            remaining_constants()
             flip_scaler(psum_flip, 0)
 
             silu_grouped = {}
@@ -539,14 +583,20 @@ def tile_bsplinekanlayer_kernel(
                     c, s = divmod(k, O_TILES)
                     if s == HALF_O + 2 and c + 1 < F_TILES:
                         flip_scaler(psum_flip, c + 1)
+                        scalers_flipped.append(c + 1)
                         if c + 2 < F_TILES:
                             load_scaler(c + 2)
                 add_term(psum_flip, n - FORM_LAG)
                 run_step(n)
+                if n == 1:
+                    copy_pairs(0, nc.scalar.copy)
+                while scalers_flipped:
+                    copy_pairs(scalers_flipped.pop(0), nc.scalar.copy)
+                if n in (2, 4):
+                    pair, flipped = late_copies.pop(0)
+                    nc.scalar.copy(out=x_by_feature[:, 2 * pair : 2 * pair + 2, :], in_=flipped[:])
                 if n in (5, 9):
                     quantise_silu((n - 5) // 4)
-                if n == 0:
-                    remaining_constants()
                 for k in range(chunks_done(n - 1), chunks_done(n)):
                     scale_chunk(k)
                     if k % HALF_O == 0 and k > 0:

@@ -35,8 +35,9 @@ LOOKAHEAD = 3
 COMBINE_LAG = 3
 FORM_LAG = 3
 TERMS = 3
-FORMS = ((0, 0, 4), (3, 3, 7), (4, 6, 4), (7, 9, 7), (1, 1, 5))
 COPIED = (0, 1)
+UNIT_TERMS = ((0, 0), (0, 1), (1, 1), (2, 1), (3, 1), (3, 2), (4, 1))
+FORMS = ((0, 0, 4), (3, 3, 7), (4, 6, 4), (7, 9, 7), (1, 1, 5))
 PREFETCH = 4
 HALF_O = O_TILES // 2
 CHUNKS = F_TILES * O_TILES
@@ -140,13 +141,8 @@ def tile_bsplinekanlayer_kernel(
         keep = ctx.enter_context(tc.tile_pool(name="keep", bufs=1))
         pool = ctx.enter_context(tc.tile_pool(name="work", bufs=1))
 
-        x_rows = pool.tile([P, B_TILES, N_IN], BF16, tag="slab", bufs=PREFETCH, align_bytes=64)
-        x_in = x.rearrange("(s p) i -> p s i", p=P)
         knot_bf = consts.tile([P, F_TILES, N_KNOTS], BF16)
         nc.scalar.dma_start(out=knot_bf[:], in_=grid.rearrange("(c p) m -> p c m", p=P))
-        for cols in (slice(0, 2 * P), slice(2 * P, N_IN)):
-            nc.sync.dma_start(out=x_rows[:, :, cols], in_=x_in[:, :, cols])
-
         scaler_rows = {}
 
         def load_scaler(c):
@@ -168,6 +164,10 @@ def tile_bsplinekanlayer_kernel(
 
         load_scaler(0)
         load_slab(0, 0)
+        x_rows = pool.tile([P, B_TILES, N_IN], BF16, tag="slab", bufs=PREFETCH, align_bytes=64)
+        x_in = x.rearrange("(s p) i -> p s i", p=P)
+        for cols in (slice(0, 2 * P), slice(2 * P, N_IN)):
+            nc.sync.dma_start(out=x_rows[:, :, cols], in_=x_in[:, :, cols])
         load_slab(0, 1)
         load_slab(1, 0)
         load_scaler(1)
@@ -268,10 +268,11 @@ def tile_bsplinekanlayer_kernel(
 
         form_banks = {}
         diagonals = {}
+        units = {unit: minus_ident if unit[1] == 1 else ident_f32 for unit in UNIT_TERMS}
 
         def take_diagonal(n):
             for form, term in terms_of(n):
-                if term != 1:
+                if (form, term) not in UNIT_TERMS:
                     w = TERMS * form + term
                     tile = pool.tile([P, P], F32, tag="diagonal", bufs=8, name="diagonal")
                     nc.scalar.activation(
@@ -287,16 +288,19 @@ def tile_bsplinekanlayer_kernel(
                     form_banks[(c, form)] = psum.tile([P, BATCH], F32, tag="flip", bufs=8, name="form")
                 nc.tensor.matmul(
                     out=form_banks[(c, form)][:],
-                    lhsT=minus_ident[:] if term == 1 else diagonals[(n, form)][:],
+                    lhsT=diagonals.get((n, form), units.get((form, term)))[:],
                     rhs=(down if FORMS[form][1] >= 6 else up)[n][:],
                     start=(term == 0),
                     stop=(term == TERMS - 1),
                 )
 
+        def copied(c, form):
+            return c >= 1 and form in COPIED
+
         def copy_form(n):
             c = n // N_KNOTS
             for form, term in terms_of(n):
-                if term == TERMS - 1 and form in COPIED:
+                if term == TERMS - 1 and copied(c, form):
                     nc.scalar.copy(
                         out=half_tile(left, c, FORMS[form][0], "left"), in_=form_banks[(c, form)][:]
                     )
@@ -304,7 +308,7 @@ def tile_bsplinekanlayer_kernel(
         def copy_outer(n):
             c, m = divmod(n, N_KNOTS)
             for form in forms_of(c):
-                if form in COPIED and FORMS[form][2] == m:
+                if copied(c, form) and FORMS[form][2] == m:
                     nc.scalar.activation(
                         out=half_tile(right, c, FORMS[form][0], "right"), in_=cube[n][:],
                         func=ACT.Relu, scale=outer[:, c, form : form + 1],
@@ -313,7 +317,7 @@ def tile_bsplinekanlayer_kernel(
         def take_minimum(n):
             c = n // N_KNOTS
             for form, term in terms_of(n):
-                if term == TERMS - 1 and form not in COPIED:
+                if term == TERMS - 1 and not copied(c, form):
                     j, first_knot, outer_knot = FORMS[form]
                     nc.vector.scalar_tensor_tensor(
                         out=half_tile(peak, c, j, "peak"), in0=cube[c * N_KNOTS + outer_knot][:],
@@ -342,7 +346,7 @@ def tile_bsplinekanlayer_kernel(
             rest = [t for t in range(PACK) if not three_term(c, half * PACK + t)]
             half_tile(peak, c, half * PACK, "peak")
             parts = [(slice(rest[0], rest[-1] + 1), ALU.max)]
-            if c < EARLY_TILES and half == 0:
+            if 1 <= c < EARLY_TILES and half == 0:
                 parts.append((slice(0, PACK, PACK - 1), ALU.min))
             for planes, op in parts:
                 nc.vector.tensor_tensor(
@@ -419,8 +423,9 @@ def tile_bsplinekanlayer_kernel(
                 )
             chunk_words[k] = words
             if r == HALF_O - 1:
-                following = 2 * c + part + PREFETCH
-                if following < 2 * F_TILES and (1, 1) not in slabs:
+                half_tile_index = 2 * c + part
+                following = half_tile_index + (PREFETCH if half_tile_index > 0 else PREFETCH - 1)
+                if PREFETCH < following < 2 * F_TILES and (2, 0) not in slabs:
                     waiting_loads.append(following)
                 elif following < 2 * F_TILES:
                     load_slab(following // 2, following % 2)
@@ -477,7 +482,8 @@ def tile_bsplinekanlayer_kernel(
             w_tiles["scales"] = w_scales
 
         def chunks_done(n):
-            return max(0, min(CHUNKS, (n + 1 - FIRST_CHUNK_STEP) * CHUNKS // (SWITCH - 4 - FIRST_CHUNK_STEP)))
+            behind = max(0, n - 2) * (CHUNKS - HALF_O) // (SWITCH - 4 - FIRST_CHUNK_STEP)
+            return min(CHUNKS, HALF_O + behind)
 
         finish = {}
         for c in range(F_TILES):
@@ -485,9 +491,9 @@ def tile_bsplinekanlayer_kernel(
                 ready = c * N_KNOTS + (7 if half == 0 else 11) + COMBINE_LAG
                 if c < EARLY_TILES and half == 1:
                     steps = (("peak", 0), ("regroup", 3), ("quantise", 5))
-                elif c < EARLY_TILES or (half == 0 and c < F_TILES - 1):
+                elif c < EARLY_TILES or half == 0 or c == 5:
                     steps = (("peak", 1), ("regroup", 2), ("quantise", 4))
-                elif half == 0 or c < F_TILES - 1:
+                elif c < F_TILES - 1:
                     steps = (("grouped_peak", 1), ("quantise", 2))
                 else:
                     steps = (("last", 1),)
@@ -521,7 +527,16 @@ def tile_bsplinekanlayer_kernel(
         with tc.psum_pool(name="psum_flip", bufs=8) as psum_flip:
             late_copies = []
             scalers_flipped = []
+            flip_scaler(psum_flip, 0)
+            copy_pairs(0, nc.scalar.copy)
+            for k in range(HALF_O // 2):
+                flip_chunk(psum_flip, k)
+                scale_chunk(k)
             for pair in range(F_TILES // 2):
+                if pair == 1:
+                    for k in range(HALF_O // 2, HALF_O):
+                        flip_chunk(psum_flip, k)
+                        scale_chunk(k)
                 flipped = psum_flip.tile([P, 2, BATCH], BF16, tag="flip", bufs=8)
                 for c in range(2):
                     for s in range(B_TILES):
@@ -540,7 +555,6 @@ def tile_bsplinekanlayer_kernel(
                 else:
                     late_copies.append((pair, flipped))
             remaining_constants()
-            flip_scaler(psum_flip, 0)
 
             silu_grouped = {}
 
@@ -575,7 +589,7 @@ def tile_bsplinekanlayer_kernel(
                 if n % 2 == 1 and n < 8:
                     silu_piece(n // 4, n // 2 % 2)
                     if n == 7:
-                        load_slab(1, 1)
+                        load_slab(2, 0)
                         for half in waiting_loads:
                             load_slab(half // 2, half % 2)
                 for k in range(chunks_done(n + 1), chunks_done(n + 2)):
@@ -588,8 +602,8 @@ def tile_bsplinekanlayer_kernel(
                             load_scaler(c + 2)
                 add_term(psum_flip, n - FORM_LAG)
                 run_step(n)
-                if n == 1:
-                    copy_pairs(0, nc.scalar.copy)
+                if n == 0:
+                    quantise_ssw(0, 0)
                 while scalers_flipped:
                     copy_pairs(scalers_flipped.pop(0), nc.scalar.copy)
                 if n in (2, 4):
@@ -599,7 +613,7 @@ def tile_bsplinekanlayer_kernel(
                     quantise_silu((n - 5) // 4)
                 for k in range(chunks_done(n - 1), chunks_done(n)):
                     scale_chunk(k)
-                    if k % HALF_O == 0 and k > 0:
+                    if k % HALF_O == 0 and k > HALF_O:
                         quantise_ssw((k - 1) // O_TILES, (k - 1) // HALF_O % 2)
                 if chunks_done(n - 2) < CHUNKS == chunks_done(n - 1):
                     quantise_ssw(F_TILES - 1, 1)

@@ -32,7 +32,7 @@ FLOPS = 2 * BATCH * N_OUT * (N_IN + N_IN * N_BASIS)
 
 
 LOOKAHEAD = 3
-COMBINE_LAG = 3
+COMBINE_LAG = 4
 FORM_LAG = 3
 TERMS = 3
 COPIED = (0, 1)
@@ -249,12 +249,12 @@ def tile_bsplinekanlayer_kernel(
         def take_sides(n):
             c, m = divmod(n, N_KNOTS)
             if m <= N_BASIS - (1 if c < EARLY_TILES else 0):
-                up[n] = pool.tile([P, BATCH], F32, tag="up", bufs=5, name="up")
+                up[n] = pool.tile([P, BATCH], F32, tag="up", bufs=6, name="up")
                 nc.scalar.activation(
                     out=up[n][:], in_=cube[n][:], func=ACT.Relu, scale=up_scale[:, c, m : m + 1]
                 )
             if needs_down(c, m):
-                down[n] = pool.tile([P, BATCH], F32, tag="down", bufs=5, name="down")
+                down[n] = pool.tile([P, BATCH], F32, tag="down", bufs=6, name="down")
                 nc.scalar.activation(
                     out=down[n][:], in_=cube[n][:], func=ACT.Relu,
                     scale=neg_down_scale[:, c, m - 3 : m - 2],
@@ -274,7 +274,7 @@ def tile_bsplinekanlayer_kernel(
             for form, term in terms_of(n):
                 if (form, term) not in UNIT_TERMS:
                     w = TERMS * form + term
-                    tile = pool.tile([P, P], F32, tag="diagonal", bufs=8, name="diagonal")
+                    tile = pool.tile([P, P], F32, tag="diagonal", bufs=6, name="diagonal")
                     nc.scalar.activation(
                         out=tile[:], in_=ident_f32[:], func=ACT.Copy,
                         scale=form_weight[:, n // N_KNOTS, w : w + 1],

@@ -35,8 +35,9 @@ LOOKAHEAD = 3
 COMBINE_LAG = 4
 FORM_LAG = 3
 TERMS = 3
+END_KNOTS = (0, N_KNOTS - 1)
 COPIED = (0, 1)
-UNIT_TERMS = ((0, 0), (0, 1), (1, 1), (2, 1), (3, 1), (3, 2), (4, 1))
+UNIT_TERMS = ((0, 1), (1, 1), (2, 1), (3, 1), (4, 1))
 FORMS = ((0, 0, 4), (3, 3, 7), (4, 6, 4), (7, 9, 7), (1, 1, 5))
 PREFETCH = 4
 HALF_O = O_TILES // 2
@@ -104,7 +105,8 @@ def spline_constants(nc, consts, scratch, knot_bf):
         nc.vector.reciprocal(out=r4, in_=h4)
         nc.gpsimd.memset(left_mix[:, :, 0:1], 1.0)
         nc.gpsimd.tensor_mul(out=left_mix[:, :, 1:8], in0=h1[:, :, 0:7], in1=r4[:, :, 0:7])
-        nc.gpsimd.tensor_copy(out=form_weight[:, :, 0:4:3], in_=left_mix[:, :, 0:4:3])
+        nc.gpsimd.tensor_copy(out=form_weight[:, :, 0:1], in_=first_left[:, :, 0:1])
+        nc.gpsimd.tensor_copy(out=form_weight[:, :, 3:4], in_=left_mix[:, :, 3:4])
         nc.gpsimd.tensor_copy(out=form_weight[:, :, 12:13], in_=left_mix[:, :, 1:2])
         for at, j in ((2, 0), (5, 3), (14, 1)):
             third_weight(
@@ -127,7 +129,8 @@ def spline_constants(nc, consts, scratch, knot_bf):
             third_weight(
                 at, j, r2[:, :, j + 2 : j + 3], (h3[:, :, j - 1 : j], r4[:, :, j - 1 : j])
             )
-        nc.gpsimd.tensor_copy(out=form_weight[:, :, 8:12:3], in_=right_mix[:, :, 4:8:3])
+        nc.gpsimd.tensor_copy(out=form_weight[:, :, 8:9], in_=right_mix[:, :, 4:5])
+        nc.gpsimd.tensor_copy(out=form_weight[:, :, 11:12], in_=neg_down_scale[:, :, 8:9])
 
     return knot, neg_knot, up_scale, neg_down_scale, left_mix, right_mix, form_weight, outer, rest
 
@@ -213,6 +216,8 @@ def tile_bsplinekanlayer_kernel(
             return any(FORMS[form][2] == m for form in forms_of(c))
 
         def needs_down(c, m):
+            if m in END_KNOTS:
+                return False
             if c >= EARLY_TILES:
                 return m >= 3
             return m >= 6 or any(m >= 4 and not three_term(c, j) for j in (m - 4, m - 3) if j >= 0)
@@ -223,7 +228,6 @@ def tile_bsplinekanlayer_kernel(
         down = {}
         left = {}
         right = {}
-        peak = {}
         grouped = {}
         codes = {}
 
@@ -237,7 +241,9 @@ def tile_bsplinekanlayer_kernel(
 
         def take_cube(n):
             c, m = divmod(n, N_KNOTS)
-            if kept(c, m):
+            if m in END_KNOTS:
+                cube[n] = pool.tile([P, BATCH], F32, tag="end_cube", bufs=2, name="cube")
+            elif kept(c, m):
                 cube[n] = pool.tile([P, BATCH], F32, tag="kept", bufs=3, name="cube")
             else:
                 cube[n] = pool.tile([P, BATCH], F32, tag="cube", bufs=3, name="cube")
@@ -248,7 +254,7 @@ def tile_bsplinekanlayer_kernel(
 
         def take_sides(n):
             c, m = divmod(n, N_KNOTS)
-            if m <= N_BASIS - (1 if c < EARLY_TILES else 0):
+            if 1 <= m <= N_BASIS - (1 if c < EARLY_TILES else 0):
                 up[n] = pool.tile([P, BATCH], F32, tag="up", bufs=6, name="up")
                 nc.scalar.activation(
                     out=up[n][:], in_=cube[n][:], func=ACT.Relu, scale=up_scale[:, c, m : m + 1]
@@ -263,12 +269,11 @@ def tile_bsplinekanlayer_kernel(
         def half_tile(store, c, j, tag):
             key = (c, j // PACK)
             if key not in store:
-                store[key] = pool.tile([P, PACK, BATCH], BF16, tag=tag, bufs=2, name=tag)
+                store[key] = pool.tile([P, PACK, BATCH], BF16, tag=tag, bufs=3 if tag == "left" else 2, name=tag)
             return store[key][:, j % PACK, :]
 
         form_banks = {}
         diagonals = {}
-        units = {unit: minus_ident if unit[1] == 1 else ident_f32 for unit in UNIT_TERMS}
 
         def take_diagonal(n):
             for form, term in terms_of(n):
@@ -281,6 +286,12 @@ def tile_bsplinekanlayer_kernel(
                     )
                     diagonals[(n, form)] = tile
 
+        def side_of(n):
+            m = n % N_KNOTS
+            if m in END_KNOTS:
+                return cube[n]
+            return (up if m < N_KNOTS // 2 else down)[n]
+
         def add_term(psum, n):
             c = n // N_KNOTS
             for form, term in terms_of(n):
@@ -288,8 +299,8 @@ def tile_bsplinekanlayer_kernel(
                     form_banks[(c, form)] = psum.tile([P, BATCH], F32, tag="flip", bufs=8, name="form")
                 nc.tensor.matmul(
                     out=form_banks[(c, form)][:],
-                    lhsT=diagonals.get((n, form), units.get((form, term)))[:],
-                    rhs=(down if FORMS[form][1] >= 6 else up)[n][:],
+                    lhsT=diagonals.get((n, form), minus_ident)[:],
+                    rhs=side_of(n)[:],
                     start=(term == 0),
                     stop=(term == TERMS - 1),
                 )
@@ -320,7 +331,7 @@ def tile_bsplinekanlayer_kernel(
                 if term == TERMS - 1 and not copied(c, form):
                     j, first_knot, outer_knot = FORMS[form]
                     nc.vector.scalar_tensor_tensor(
-                        out=half_tile(peak, c, j, "peak"), in0=cube[c * N_KNOTS + outer_knot][:],
+                        out=half_tile(left, c, j, "left"), in0=cube[c * N_KNOTS + outer_knot][:],
                         scalar=outer[:, c, form : form + 1], in1=form_banks[(c, form)][:],
                         op0=ALU.mult, op1=ALU.min,
                     )
@@ -330,27 +341,29 @@ def tile_bsplinekanlayer_kernel(
             if 1 <= m <= N_BASIS and not three_term(c, m - 1):
                 j = m - 1
                 nc.vector.scalar_tensor_tensor(
-                    out=half_tile(left, c, j, "left"), in0=up[n - 1][:],
-                    scalar=left_mix[:, c, j : j + 1], in1=up[n][:],
+                    out=half_tile(left, c, j, "left"),
+                    in0=(up[n - 1] if j > 0 else cube[n - 1])[:],
+                    scalar=(left_mix if j > 0 else up_scale)[:, c, j : j + 1], in1=up[n][:],
                     op0=ALU.mult, op1=ALU.subtract,
                 )
             if m >= 4 and not three_term(c, m - 4):
                 j = m - 4
                 nc.vector.scalar_tensor_tensor(
-                    out=half_tile(right, c, j, "right"), in0=down[n][:],
-                    scalar=right_mix[:, c, j : j + 1], in1=down[n - 1][:],
+                    out=half_tile(right, c, j, "right"),
+                    in0=(down[n] if j < N_BASIS - 1 else cube[n])[:],
+                    scalar=(right_mix[:, c, j : j + 1] if j < N_BASIS - 1 else neg_down_scale[:, c, j + 1 : j + 2]),
+                    in1=down[n - 1][:],
                     op0=ALU.mult, op1=ALU.subtract,
                 )
 
         def take_peak(c, half):
             rest = [t for t in range(PACK) if not three_term(c, half * PACK + t)]
-            half_tile(peak, c, half * PACK, "peak")
             parts = [(slice(rest[0], rest[-1] + 1), ALU.max)]
             if 1 <= c < EARLY_TILES and half == 0:
                 parts.append((slice(0, PACK, PACK - 1), ALU.min))
             for planes, op in parts:
                 nc.vector.tensor_tensor(
-                    out=peak[(c, half)][:, planes, :], in0=left[(c, half)][:, planes, :],
+                    out=left[(c, half)][:, planes, :], in0=left[(c, half)][:, planes, :],
                     in1=right[(c, half)][:, planes, :], op=op,
                 )
 
@@ -359,22 +372,21 @@ def tile_bsplinekanlayer_kernel(
                 [P, BATCH, PACK], BF16, tag="grouped", bufs=2, align_bytes=64, name="grouped"
             )
             to = grouped[(c, half)][:].rearrange("p (g i) t -> p g t i", i=4)
-            of = peak[(c, half)][:].rearrange("p t (g i) -> p g t i", i=4)
-            if c < EARLY_TILES:
-                nc.scalar.activation(out=to, in_=of, func=ACT.Relu)
-            else:
-                nc.scalar.copy(out=to, in_=of)
+            of = left[(c, half)][:].rearrange("p t (g i) -> p g t i", i=4)
+            nc.scalar.activation(out=to, in_=of, func=ACT.Relu)
 
         def take_grouped_peak(c, half, cols):
             if (c, half) not in grouped:
                 grouped[(c, half)] = pool.tile(
                     [P, BATCH, PACK], BF16, tag="grouped", bufs=2, align_bytes=64, name="grouped"
                 )
-            nc.vector.tensor_tensor(
+            nc.vector.scalar_tensor_tensor(
                 out=grouped[(c, half)][:, cols, :],
                 in0=left[(c, half)][:, :, cols].rearrange("p t b -> p b t"),
+                scalar=0.0,
                 in1=right[(c, half)][:, :, cols].rearrange("p t b -> p b t"),
-                op=ALU.max,
+                op0=ALU.max,
+                op1=ALU.max,
             )
 
         def quantise_half(c, half, cols=slice(0, BATCH)):
@@ -394,23 +406,20 @@ def tile_bsplinekanlayer_kernel(
 
         scaler_banks = {}
 
-        def flip_scaler(psum_flip, c):
-            bank = psum_flip.tile([P, N_OUT], BF16, tag="flip", bufs=8, name="bank")
-            for s in range(O_TILES):
+        def flip_scaler(psum_flip, c, part):
+            bank = psum_flip.tile([P, N_TILE], BF16, tag="flip", bufs=8, name="bank")
+            for s in range(HALF_O):
                 nc.tensor.transpose(
-                    bank[:, s * P : (s + 1) * P], scaler_rows[c][:, s, :], ident_bf[:]
+                    bank[:, s * P : (s + 1) * P], scaler_rows[c][:, part * HALF_O + s, :], ident_bf[:]
                 )
-            scaler_banks[c] = bank
+            scaler_banks[(c, part)] = bank
 
-        def copy_pairs(c, copy):
-            bank = scaler_banks.pop(c)
-            for part in range(2):
-                cols = slice(part * N_TILE, (part + 1) * N_TILE)
-                pairs[(c, part)] = pool.tile([P, N_TILE, 2], BF16, tag="pairs", bufs=3, name="pairs")
-                copy(
-                    out=pairs[(c, part)][:],
-                    in_=bank[:, cols].unsqueeze(2).to_broadcast([P, N_TILE, 2]),
-                )
+        def copy_pairs(c, part):
+            bank = scaler_banks.pop((c, part))
+            pairs[(c, part)] = pool.tile([P, N_TILE, 2], BF16, tag="pairs", bufs=3, name="pairs")
+            nc.scalar.copy(
+                out=pairs[(c, part)][:], in_=bank[:].unsqueeze(2).to_broadcast([P, N_TILE, 2])
+            )
 
         def flip_chunk(psum_flip, k):
             c, s = divmod(k, O_TILES)
@@ -491,10 +500,8 @@ def tile_bsplinekanlayer_kernel(
                 ready = c * N_KNOTS + (7 if half == 0 else 11) + COMBINE_LAG
                 if c < EARLY_TILES and half == 1:
                     steps = (("peak", 0), ("regroup", 3), ("quantise", 5))
-                elif c < EARLY_TILES or half == 0 or c == 5:
+                elif c < F_TILES - 1 or half == 0:
                     steps = (("peak", 1), ("regroup", 2), ("quantise", 4))
-                elif c < F_TILES - 1:
-                    steps = (("grouped_peak", 1), ("quantise", 2))
                 else:
                     steps = (("last", 1),)
                 for kind, delay in steps:
@@ -510,8 +517,6 @@ def tile_bsplinekanlayer_kernel(
             for kind, c, half in finish.get(n, []):
                 if kind == "peak":
                     take_peak(c, half)
-                elif kind == "grouped_peak":
-                    take_grouped_peak(c, half, slice(0, BATCH))
                 elif kind == "regroup":
                     regroup(c, half)
             take_minimum(n - FORM_LAG - 2)
@@ -527,8 +532,9 @@ def tile_bsplinekanlayer_kernel(
         with tc.psum_pool(name="psum_flip", bufs=8) as psum_flip:
             late_copies = []
             scalers_flipped = []
-            flip_scaler(psum_flip, 0)
-            copy_pairs(0, nc.scalar.copy)
+            for part in range(2):
+                flip_scaler(psum_flip, 0, part)
+                copy_pairs(0, part)
             for k in range(HALF_O // 2):
                 flip_chunk(psum_flip, k)
                 scale_chunk(k)
@@ -595,17 +601,20 @@ def tile_bsplinekanlayer_kernel(
                 for k in range(chunks_done(n + 1), chunks_done(n + 2)):
                     flip_chunk(psum_flip, k)
                     c, s = divmod(k, O_TILES)
-                    if s == HALF_O + 2 and c + 1 < F_TILES:
-                        flip_scaler(psum_flip, c + 1)
-                        scalers_flipped.append(c + 1)
-                        if c + 2 < F_TILES:
-                            load_scaler(c + 2)
+                    if s == HALF_O and c + 1 < F_TILES:
+                        flip_scaler(psum_flip, c + 1, 0)
+                        scalers_flipped.append((c + 1, 0))
+                    elif s == 0 and c > 0:
+                        flip_scaler(psum_flip, c, 1)
+                        scalers_flipped.append((c, 1))
+                        if c + 1 < F_TILES:
+                            load_scaler(c + 1)
                 add_term(psum_flip, n - FORM_LAG)
                 run_step(n)
                 if n == 0:
                     quantise_ssw(0, 0)
                 while scalers_flipped:
-                    copy_pairs(scalers_flipped.pop(0), nc.scalar.copy)
+                    copy_pairs(*scalers_flipped.pop(0))
                 if n in (2, 4):
                     pair, flipped = late_copies.pop(0)
                     nc.scalar.copy(out=x_by_feature[:, 2 * pair : 2 * pair + 2, :], in_=flipped[:])

@@ -37,9 +37,8 @@ FORM_LAG = 3
 TERMS = 3
 END_KNOTS = (0, N_KNOTS - 1)
 COPIED = (0, 1)
-UNIT_TERMS = ((0, 1), (1, 1), (2, 1), (3, 1), (4, 1))
 FORMS = ((0, 0, 4), (3, 3, 7), (4, 6, 4), (7, 9, 7), (1, 1, 5))
-PREFETCH = 4
+PREFETCH = 3
 HALF_O = O_TILES // 2
 CHUNKS = F_TILES * O_TILES
 FIRST_CHUNK_STEP = 3
@@ -59,10 +58,10 @@ def spline_constants(nc, consts, scratch, knot_bf):
     def constant(name, count):
         return consts.tile([P, F_TILES, count], F32, name=name)
 
+    half = constant("half", N_BASIS)
+    nc.gpsimd.memset(half[:], 0.5)
     knot = constant("knot", N_KNOTS)
     nc.vector.tensor_copy(out=knot[:], in_=knot_bf[:])
-    neg_knot = constant("neg_knot", N_KNOTS)
-    nc.vector.tensor_scalar_mul(out=neg_knot[:], in0=knot[:], scalar1=-1.0)
 
     spans = temporary(30)
     starts = {1: 0, 2: 11, 3: 21}
@@ -71,30 +70,45 @@ def spline_constants(nc, consts, scratch, knot_bf):
         nc.vector.tensor_sub(
             out=spans[:, :, first : first + count], in0=knot[:, :, w:], in1=knot[:, :, :count]
         )
-    h4 = temporary(N_BASIS)
-    nc.vector.tensor_sub(out=h4, in0=knot[:, :, 4:], in1=knot[:, :, :N_BASIS])
     inverses = temporary(30)
     nc.vector.reciprocal(out=inverses, in_=spans)
-    h1, h3 = spans[:, :, 0:11], spans[:, :, 21:30]
+    h3 = spans[:, :, 21:30]
     r1, r2, r3 = inverses[:, :, 0:11], inverses[:, :, 11:21], inverses[:, :, 21:30]
 
+    kappa = temporary(N_KNOTS)
     first_left = temporary(N_BASIS + 1)
     nc.vector.tensor_mul(out=first_left, in0=r1[:, :, 0:9], in1=r2[:, :, 0:9])
-    ratio = temporary(N_BASIS)
-    nc.vector.tensor_mul(out=ratio, in0=h4, in1=r1[:, :, 0:8])
     nc.vector.tensor_mul(out=first_left, in0=first_left, in1=r3)
-    up_scale = constant("up_scale", N_BASIS + 1)
-    nc.vector.tensor_copy(out=up_scale[:, :, 0:1], in_=first_left[:, :, 0:1])
-    nc.vector.tensor_mul(out=up_scale[:, :, 1:9], in0=first_left[:, :, 1:9], in1=ratio)
+    root = constant("root", N_KNOTS)
+    root_shift = constant("root_shift", N_KNOTS)
+    nc.gpsimd.tensor_tensor(out=root[:, :, 0:8], in0=first_left[:, :, 0:8], in1=half[:], op=ALU.pow)
+    nc.vector.tensor_copy(out=kappa[:, :, 0:8], in_=first_left[:, :, 0:8])
+    first_right = temporary(N_BASIS + 1)
+    nc.vector.tensor_mul(out=first_right, in0=r3, in1=r2[:, :, 1:10])
+    nc.vector.tensor_mul(out=first_right, in0=first_right, in1=r1[:, :, 2:11])
+    nc.vector.tensor_copy(out=kappa[:, :, 8:12], in_=first_right[:, :, 5:9])
+    per_kappa = temporary(N_KNOTS)
+    nc.vector.reciprocal(out=per_kappa, in_=kappa)
+    nc.gpsimd.tensor_tensor(
+        out=root[:, :, 8:12], in0=first_right[:, :, 5:9], in1=half[:, :, 0:4], op=ALU.pow
+    )
+    nc.vector.scalar_tensor_tensor(
+        out=root_shift[:], in0=root[:], scalar=-1.0, in1=knot[:], op0=ALU.mult, op1=ALU.mult
+    )
 
-    neg_down_scale = constant("neg_down_scale", N_BASIS + 1)
-    left_mix = constant("left_mix", N_BASIS)
-    right_mix = constant("right_mix", N_BASIS)
-    form_weight = constant("form_weight", TERMS * len(FORMS))
-    outer = constant("outer", len(FORMS))
+    h4 = temporary(N_BASIS)
+    nc.vector.tensor_sub(out=h4, in0=knot[:, :, 4:], in1=knot[:, :, :N_BASIS])
+    up_ratio = constant("up_ratio", N_BASIS)
+    nc.vector.tensor_mul(out=up_ratio[:], in0=h4, in1=r1[:, :, 0:8])
+    nc.vector.tensor_mul(out=up_ratio[:], in0=up_ratio[:], in1=first_left[:, :, 1:9])
+    nc.vector.tensor_mul(out=up_ratio[:], in0=up_ratio[:], in1=per_kappa[:, :, 1:9])
+
+    down_ratio = constant("down_ratio", N_BASIS)
+    right_mix = constant("right_mix", PACK)
+    third = constant("third", len(FORMS))
 
     def third_weight(at, j, second_span, third_span):
-        weight = form_weight[:, :, at : at + 1]
+        weight = third[:, :, at : at + 1]
         other = temporary(1)
         nc.gpsimd.tensor_mul(out=weight, in0=h4[:, :, j : j + 1], in1=second_span)
         nc.gpsimd.tensor_mul(out=other, in0=third_span[0], in1=third_span[1])
@@ -103,36 +117,27 @@ def spline_constants(nc, consts, scratch, knot_bf):
     def rest():
         r4 = temporary(N_BASIS)
         nc.vector.reciprocal(out=r4, in_=h4)
-        nc.gpsimd.memset(left_mix[:, :, 0:1], 1.0)
-        nc.gpsimd.tensor_mul(out=left_mix[:, :, 1:8], in0=h1[:, :, 0:7], in1=r4[:, :, 0:7])
-        nc.gpsimd.tensor_copy(out=form_weight[:, :, 0:1], in_=first_left[:, :, 0:1])
-        nc.gpsimd.tensor_copy(out=form_weight[:, :, 3:4], in_=left_mix[:, :, 3:4])
-        nc.gpsimd.tensor_copy(out=form_weight[:, :, 12:13], in_=left_mix[:, :, 1:2])
-        for at, j in ((2, 0), (5, 3), (14, 1)):
+        for at, j in ((0, 0), (4, 1), (1, 3)):
             third_weight(
                 at, j, r2[:, :, j : j + 1], (h3[:, :, j + 2 : j + 3], r4[:, :, j + 1 : j + 2])
             )
-        nc.gpsimd.tensor_copy(out=outer[:, :, 2:4], in_=first_left[:, :, 4:8:3])
-        first_right = temporary(N_BASIS + 1)
-        nc.gpsimd.tensor_mul(out=first_right, in0=r3, in1=r2[:, :, 1:10])
-        down_ratio = temporary(N_BASIS)
-        nc.gpsimd.tensor_mul(out=down_ratio, in0=h4, in1=r1[:, :, 3:11])
-        nc.gpsimd.tensor_mul(out=first_right, in0=first_right, in1=r1[:, :, 2:11])
-        nc.gpsimd.tensor_scalar_mul(out=first_right, in0=first_right, scalar1=-1.0)
-        nc.gpsimd.tensor_mul(out=neg_down_scale[:, :, 0:8], in0=first_right[:, :, 0:8], in1=down_ratio)
-        nc.gpsimd.tensor_copy(out=neg_down_scale[:, :, 8:9], in_=first_right[:, :, 8:9])
-        nc.gpsimd.tensor_copy(out=outer[:, :, 0:2], in_=first_right[:, :, 1:5:3])
-        nc.gpsimd.tensor_copy(out=outer[:, :, 4:5], in_=first_right[:, :, 2:3])
-        nc.gpsimd.memset(right_mix[:, :, 7:8], 1.0)
-        nc.gpsimd.tensor_mul(out=right_mix[:, :, 0:7], in0=h1[:, :, 4:11], in1=r4[:, :, 1:8])
-        for at, j in ((6, 4), (9, 7)):
+        nc.gpsimd.tensor_mul(out=down_ratio[:], in0=h4, in1=r1[:, :, 3:11])
+        nc.gpsimd.tensor_mul(out=down_ratio[:], in0=down_ratio[:], in1=first_right[:, :, 0:8])
+        nc.gpsimd.tensor_mul(out=down_ratio[:], in0=down_ratio[:], in1=per_kappa[:, :, 3:11])
+        nc.gpsimd.tensor_scalar(
+            out=down_ratio[:], in0=down_ratio[:], scalar1=-1.0, scalar2=1.0, op0=ALU.mult, op1=ALU.mult
+        )
+        nc.gpsimd.tensor_mul(out=right_mix[:], in0=first_right[:, :, 1:5], in1=per_kappa[:, :, 4:8])
+        nc.gpsimd.tensor_scalar(
+            out=right_mix[:], in0=right_mix[:], scalar1=-1.0, scalar2=1.0, op0=ALU.mult, op1=ALU.mult
+        )
+        for at, j in ((2, 4), (3, 7)):
             third_weight(
                 at, j, r2[:, :, j + 2 : j + 3], (h3[:, :, j - 1 : j], r4[:, :, j - 1 : j])
             )
-        nc.gpsimd.tensor_copy(out=form_weight[:, :, 8:9], in_=right_mix[:, :, 4:5])
-        nc.gpsimd.tensor_copy(out=form_weight[:, :, 11:12], in_=neg_down_scale[:, :, 8:9])
 
-    return knot, neg_knot, up_scale, neg_down_scale, left_mix, right_mix, form_weight, outer, rest
+    return knot, root, root_shift, up_ratio, down_ratio, right_mix, third, rest
+
 
 def tile_bsplinekanlayer_kernel(
     tc, x, base_weight_words, base_weight_scales, spline_weight, spline_scaler, grid, out
@@ -157,13 +162,19 @@ def tile_bsplinekanlayer_kernel(
             scaler_rows[c] = rows
 
         slabs = {}
-        waiting_loads = []
 
         def load_slab(c, part):
             slab = pool.tile([P, HALF_O, P * N_BASIS], BF16, tag="slab", bufs=PREFETCH, align_bytes=64)
             rows = spline_weight[:, c * P : (c + 1) * P, :].rearrange("(s p) i j -> p s (i j)", p=P)
             nc.sync.dma_start(out=slab[:], in_=rows[:, part * HALF_O : (part + 1) * HALF_O, :])
             slabs[(c, part)] = slab
+
+        def load_next():
+            following = len(slabs)
+            if following < 2 * F_TILES:
+                load_slab(following // 2, following % 2)
+            elif not w_tiles:
+                load_w()
 
         load_scaler(0)
         load_slab(0, 0)
@@ -190,8 +201,7 @@ def tile_bsplinekanlayer_kernel(
 
         scratch = pool.tile([P, 1024], F32, tag="grouped", bufs=2, align_bytes=64)
         (
-            knot, neg_knot, up_scale, neg_down_scale, left_mix, right_mix, form_weight, outer,
-            remaining_constants,
+            knot, root, root_shift, up_ratio, down_ratio, right_mix, third, remaining_constants,
         ) = spline_constants(nc, consts, scratch, knot_bf)
 
         x_by_feature = keep.tile([P, F_TILES, BATCH], BF16)
@@ -212,58 +222,61 @@ def tile_bsplinekanlayer_kernel(
             c, m = divmod(n, N_KNOTS)
             return [(form, m - FORMS[form][1]) for form in forms_of(c) if 0 <= m - FORMS[form][1] < TERMS]
 
-        def kept(c, m):
-            return any(FORMS[form][2] == m for form in forms_of(c))
-
         def needs_down(c, m):
-            if m in END_KNOTS:
+            if not 3 <= m <= 10:
                 return False
-            if c >= EARLY_TILES:
-                return m >= 3
-            return m >= 6 or any(m >= 4 and not three_term(c, j) for j in (m - 4, m - 3) if j >= 0)
+            return m >= 6 or any(
+                not three_term(c, j) for j in (m - 4, m - 3) if 0 <= j and (j > 3 or j + 3 == m)
+            )
 
         square = {}
-        cube = {}
-        up = {}
-        down = {}
+        cubes = {}
+        ups = {}
+        downs = {}
         left = {}
         right = {}
         grouped = {}
         codes = {}
+
+        def part_of(store, c, first, m, tag):
+            key = (c, (m - first) // 4)
+            if key not in store:
+                store[key] = pool.tile([P, 4, BATCH], F32, tag=tag, bufs=3, name=tag)
+            return store[key][:, (m - first) % 4, :]
+
+        def cube(c, m):
+            return part_of(cubes, c, 0, m, "cubes")
+
+        def up(c, m):
+            return part_of(ups, c, 1, m, "sides")
+
+        def down(c, m):
+            return part_of(downs, c, 3, m, "sides")
 
         def take_square(n):
             c, m = divmod(n, N_KNOTS)
             square[n] = pool.tile([P, BATCH], F32, tag="square", bufs=4, name="square")
             nc.scalar.activation(
                 out=square[n][:], in_=x_by_feature[:, c, :], func=ACT.Square,
-                bias=neg_knot[:, c, m : m + 1],
+                scale=root[:, c, m : m + 1], bias=root_shift[:, c, m : m + 1],
             )
 
         def take_cube(n):
             c, m = divmod(n, N_KNOTS)
-            if m in END_KNOTS:
-                cube[n] = pool.tile([P, BATCH], F32, tag="end_cube", bufs=2, name="cube")
-            elif kept(c, m):
-                cube[n] = pool.tile([P, BATCH], F32, tag="kept", bufs=3, name="cube")
-            else:
-                cube[n] = pool.tile([P, BATCH], F32, tag="cube", bufs=3, name="cube")
             nc.vector.scalar_tensor_tensor(
-                out=cube[n][:], in0=x_by_feature[:, c, :], scalar=knot[:, c, m : m + 1],
+                out=cube(c, m), in0=x_by_feature[:, c, :], scalar=knot[:, c, m : m + 1],
                 in1=square[n][:], op0=ALU.subtract, op1=ALU.mult,
             )
 
         def take_sides(n):
             c, m = divmod(n, N_KNOTS)
             if 1 <= m <= N_BASIS - (1 if c < EARLY_TILES else 0):
-                up[n] = pool.tile([P, BATCH], F32, tag="up", bufs=6, name="up")
                 nc.scalar.activation(
-                    out=up[n][:], in_=cube[n][:], func=ACT.Relu, scale=up_scale[:, c, m : m + 1]
+                    out=up(c, m), in_=cube(c, m), func=ACT.Relu, scale=up_ratio[:, c, m - 1 : m]
                 )
             if needs_down(c, m):
-                down[n] = pool.tile([P, BATCH], F32, tag="down", bufs=6, name="down")
                 nc.scalar.activation(
-                    out=down[n][:], in_=cube[n][:], func=ACT.Relu,
-                    scale=neg_down_scale[:, c, m - 3 : m - 2],
+                    out=down(c, m), in_=cube(c, m), func=ACT.Relu, scale=down_ratio[:, c, m - 3 : m - 2]
                 )
 
         def half_tile(store, c, j, tag):
@@ -275,34 +288,36 @@ def tile_bsplinekanlayer_kernel(
         form_banks = {}
         diagonals = {}
 
-        def take_diagonal(n):
-            for form, term in terms_of(n):
-                if (form, term) not in UNIT_TERMS:
-                    w = TERMS * form + term
-                    tile = pool.tile([P, P], F32, tag="diagonal", bufs=6, name="diagonal")
-                    nc.scalar.activation(
-                        out=tile[:], in_=ident_f32[:], func=ACT.Copy,
-                        scale=form_weight[:, n // N_KNOTS, w : w + 1],
-                    )
-                    diagonals[(n, form)] = tile
+        def term_of(c, form, term):
+            j, first_knot, outer_knot = FORMS[form]
+            m = first_knot + term
+            if j < PACK:
+                return (
+                    (ident_f32, cube(c, m)), (minus_ident, up(c, m)), (diagonals.get((c, form)), up(c, m))
+                )[term]
+            return (
+                (diagonals.get((c, form)), down(c, m)), (minus_ident, down(c, m)), (minus_ident, cube(c, m))
+            )[term]
 
-        def side_of(n):
-            m = n % N_KNOTS
-            if m in END_KNOTS:
-                return cube[n]
-            return (up if m < N_KNOTS // 2 else down)[n]
+        def take_diagonal(n):
+            c = n // N_KNOTS
+            for form, term in terms_of(n):
+                if term == (TERMS - 1 if FORMS[form][0] < PACK else 0):
+                    tile = pool.tile([P, P], F32, tag="diagonal", bufs=5, name="diagonal")
+                    nc.scalar.activation(
+                        out=tile[:], in_=ident_f32[:], func=ACT.Copy, scale=third[:, c, form : form + 1]
+                    )
+                    diagonals[(c, form)] = tile
 
         def add_term(psum, n):
             c = n // N_KNOTS
             for form, term in terms_of(n):
                 if term == 0:
                     form_banks[(c, form)] = psum.tile([P, BATCH], F32, tag="flip", bufs=8, name="form")
+                weight, values = term_of(c, form, term)
                 nc.tensor.matmul(
-                    out=form_banks[(c, form)][:],
-                    lhsT=diagonals.get((n, form), minus_ident)[:],
-                    rhs=side_of(n)[:],
-                    start=(term == 0),
-                    stop=(term == TERMS - 1),
+                    out=form_banks[(c, form)][:], lhsT=weight[:], rhs=values,
+                    start=(term == 0), stop=(term == TERMS - 1),
                 )
 
         def copied(c, form):
@@ -321,8 +336,8 @@ def tile_bsplinekanlayer_kernel(
             for form in forms_of(c):
                 if copied(c, form) and FORMS[form][2] == m:
                     nc.scalar.activation(
-                        out=half_tile(right, c, FORMS[form][0], "right"), in_=cube[n][:],
-                        func=ACT.Relu, scale=outer[:, c, form : form + 1],
+                        out=half_tile(right, c, FORMS[form][0], "right"), in_=cube(c, m),
+                        func=ACT.Relu, scale=right_mix[:, c, m - 4 : m - 3],
                     )
 
         def take_minimum(n):
@@ -330,35 +345,54 @@ def tile_bsplinekanlayer_kernel(
             for form, term in terms_of(n):
                 if term == TERMS - 1 and not copied(c, form):
                     j, first_knot, outer_knot = FORMS[form]
-                    nc.vector.scalar_tensor_tensor(
-                        out=half_tile(left, c, j, "left"), in0=cube[c * N_KNOTS + outer_knot][:],
-                        scalar=outer[:, c, form : form + 1], in1=form_banks[(c, form)][:],
-                        op0=ALU.mult, op1=ALU.min,
-                    )
+                    to = half_tile(left, c, j, "left")
+                    if j < PACK:
+                        nc.vector.scalar_tensor_tensor(
+                            out=to, in0=cube(c, outer_knot), scalar=right_mix[:, c, j : j + 1],
+                            in1=form_banks[(c, form)][:], op0=ALU.mult, op1=ALU.min,
+                        )
+                    else:
+                        nc.vector.tensor_tensor(
+                            out=to, in0=cube(c, outer_knot), in1=form_banks[(c, form)][:], op=ALU.min
+                        )
+
+        def negative(c, half):
+            return EARLY_TILES <= c < F_TILES - 1 and half == 1
 
         def combine(n):
             c, m = divmod(n, N_KNOTS)
-            if 1 <= m <= N_BASIS and not three_term(c, m - 1):
-                j = m - 1
-                nc.vector.scalar_tensor_tensor(
-                    out=half_tile(left, c, j, "left"),
-                    in0=(up[n - 1] if j > 0 else cube[n - 1])[:],
-                    scalar=(left_mix if j > 0 else up_scale)[:, c, j : j + 1], in1=up[n][:],
-                    op0=ALU.mult, op1=ALU.subtract,
+            if c < EARLY_TILES and 1 <= m <= N_BASIS and not three_term(c, m - 1):
+                nc.vector.tensor_tensor(
+                    out=half_tile(left, c, m - 1, "left"), in0=cube(c, m - 1), in1=up(c, m), op=ALU.subtract
                 )
-            if m >= 4 and not three_term(c, m - 4):
-                j = m - 4
+            j = m - 4
+            if j >= 0 and not three_term(c, j) and not negative(c, j // PACK):
                 nc.vector.scalar_tensor_tensor(
-                    out=half_tile(right, c, j, "right"),
-                    in0=(down[n] if j < N_BASIS - 1 else cube[n])[:],
-                    scalar=(right_mix[:, c, j : j + 1] if j < N_BASIS - 1 else neg_down_scale[:, c, j + 1 : j + 2]),
-                    in1=down[n - 1][:],
-                    op0=ALU.mult, op1=ALU.subtract,
+                    out=half_tile(right, c, j, "right"), in0=cube(c, m),
+                    scalar=right_mix[:, c, j : j + 1] if j < PACK else -1.0,
+                    in1=down(c, m - 1), op0=ALU.mult, op1=ALU.subtract,
+                )
+
+        def combine_four(n):
+            c, m = divmod(n, N_KNOTS)
+            if c < EARLY_TILES:
+                return
+            if m in (4, 8):
+                half = m // 4 - 1
+                half_tile(left, c, half * PACK, "left")
+                a, b = cubes[(c, half)], ups[(c, half)]
+                if negative(c, half):
+                    a, b = b, a
+                nc.vector.tensor_tensor(out=left[(c, half)][:], in0=a[:], in1=b[:], op=ALU.subtract)
+            if m == N_KNOTS - 1 and negative(c, 1):
+                half_tile(right, c, PACK, "right")
+                nc.vector.tensor_tensor(
+                    out=right[(c, 1)][:], in0=cubes[(c, 2)][:], in1=downs[(c, 1)][:], op=ALU.add
                 )
 
         def take_peak(c, half):
             rest = [t for t in range(PACK) if not three_term(c, half * PACK + t)]
-            parts = [(slice(rest[0], rest[-1] + 1), ALU.max)]
+            parts = [(slice(rest[0], rest[-1] + 1), ALU.min if negative(c, half) else ALU.max)]
             if 1 <= c < EARLY_TILES and half == 0:
                 parts.append((slice(0, PACK, PACK - 1), ALU.min))
             for planes, op in parts:
@@ -373,7 +407,7 @@ def tile_bsplinekanlayer_kernel(
             )
             to = grouped[(c, half)][:].rearrange("p (g i) t -> p g t i", i=4)
             of = left[(c, half)][:].rearrange("p t (g i) -> p g t i", i=4)
-            nc.scalar.activation(out=to, in_=of, func=ACT.Relu)
+            nc.scalar.activation(out=to, in_=of, func=ACT.Relu, scale=-1.0 if negative(c, half) else 1.0)
 
         def take_grouped_peak(c, half, cols):
             if (c, half) not in grouped:
@@ -432,14 +466,7 @@ def tile_bsplinekanlayer_kernel(
                 )
             chunk_words[k] = words
             if r == HALF_O - 1:
-                half_tile_index = 2 * c + part
-                following = half_tile_index + (PREFETCH if half_tile_index > 0 else PREFETCH - 1)
-                if PREFETCH < following < 2 * F_TILES and (2, 0) not in slabs:
-                    waiting_loads.append(following)
-                elif following < 2 * F_TILES:
-                    load_slab(following // 2, following % 2)
-                elif following == 2 * F_TILES + 1:
-                    load_w()
+                load_next()
 
         def scale_chunk(k):
             c, s = divmod(k, O_TILES)
@@ -501,7 +528,7 @@ def tile_bsplinekanlayer_kernel(
                 if c < EARLY_TILES and half == 1:
                     steps = (("peak", 0), ("regroup", 3), ("quantise", 5))
                 elif c < F_TILES - 1 or half == 0:
-                    steps = (("peak", 1), ("regroup", 2), ("quantise", 4))
+                    steps = (("peak", 1), ("regroup", 2), ("quantise", 5))
                 else:
                     steps = (("last", 1),)
                 for kind, delay in steps:
@@ -523,6 +550,8 @@ def tile_bsplinekanlayer_kernel(
             copy_outer(n - 1)
             copy_form(n - FORM_LAG - 2)
             take_diagonal(n - 1)
+            if 0 <= n - COMBINE_LAG + 1 < STEPS:
+                combine_four(n - COMBINE_LAG + 1)
             if 0 <= n - COMBINE_LAG < STEPS:
                 combine(n - COMBINE_LAG)
             for kind, c, half in finish.get(n, []):
@@ -535,6 +564,7 @@ def tile_bsplinekanlayer_kernel(
             for part in range(2):
                 flip_scaler(psum_flip, 0, part)
                 copy_pairs(0, part)
+            load_scaler(2)
             for k in range(HALF_O // 2):
                 flip_chunk(psum_flip, k)
                 scale_chunk(k)
@@ -595,9 +625,7 @@ def tile_bsplinekanlayer_kernel(
                 if n % 2 == 1 and n < 8:
                     silu_piece(n // 4, n // 2 % 2)
                     if n == 7:
-                        load_slab(2, 0)
-                        for half in waiting_loads:
-                            load_slab(half // 2, half % 2)
+                        load_next()
                 for k in range(chunks_done(n + 1), chunks_done(n + 2)):
                     flip_chunk(psum_flip, k)
                     c, s = divmod(k, O_TILES)
@@ -607,8 +635,8 @@ def tile_bsplinekanlayer_kernel(
                     elif s == 0 and c > 0:
                         flip_scaler(psum_flip, c, 1)
                         scalers_flipped.append((c, 1))
-                        if c + 1 < F_TILES:
-                            load_scaler(c + 1)
+                        if c + 2 < F_TILES:
+                            load_scaler(c + 2)
                 add_term(psum_flip, n - FORM_LAG)
                 run_step(n)
                 if n == 0:
@@ -617,7 +645,7 @@ def tile_bsplinekanlayer_kernel(
                     copy_pairs(*scalers_flipped.pop(0))
                 if n in (2, 4):
                     pair, flipped = late_copies.pop(0)
-                    nc.scalar.copy(out=x_by_feature[:, 2 * pair : 2 * pair + 2, :], in_=flipped[:])
+                    nc.vector.tensor_copy(out=x_by_feature[:, 2 * pair : 2 * pair + 2, :], in_=flipped[:])
                 if n in (5, 9):
                     quantise_silu((n - 5) // 4)
                 for k in range(chunks_done(n - 1), chunks_done(n)):
@@ -676,7 +704,7 @@ def tile_bsplinekanlayer_kernel(
                 if n == 0:
                     result = pool.tile([P, N_TILE], F32, tag="slab", bufs=PREFETCH, align_bytes=64)
                 else:
-                    result = pool.tile([P, N_TILE], F32, tag="cube", bufs=3)
+                    result = pool.tile([P, N_TILE], F32, tag="sides", bufs=3)
                 copy(out=result[:], in_=acc[(s, n)][:])
                 nc.sync.dma_start(out=out[rows_of(s), n * N_TILE : (n + 1) * N_TILE], in_=result[:])
 

@@ -36,7 +36,7 @@ COMBINE_LAG = 4
 FORM_LAG = 3
 TERMS = 3
 END_KNOTS = (0, N_KNOTS - 1)
-COPIED = (0, 1)
+COPIED = (0, 1, 2, 3)
 FORMS = ((0, 0, 4), (3, 3, 7), (4, 6, 4), (7, 9, 7), (1, 1, 5))
 PREFETCH = 3
 HALF_O = O_TILES // 2
@@ -58,8 +58,6 @@ def spline_constants(nc, consts, scratch, knot_bf):
     def constant(name, count):
         return consts.tile([P, F_TILES, count], F32, name=name)
 
-    half = constant("half", N_BASIS)
-    nc.gpsimd.memset(half[:], 0.5)
     knot = constant("knot", N_KNOTS)
     nc.vector.tensor_copy(out=knot[:], in_=knot_bf[:])
 
@@ -76,32 +74,38 @@ def spline_constants(nc, consts, scratch, knot_bf):
     r1, r2, r3 = inverses[:, :, 0:11], inverses[:, :, 11:21], inverses[:, :, 21:30]
 
     kappa = temporary(N_KNOTS)
-    first_left = temporary(N_BASIS + 1)
-    nc.vector.tensor_mul(out=first_left, in0=r1[:, :, 0:9], in1=r2[:, :, 0:9])
-    nc.vector.tensor_mul(out=first_left, in0=first_left, in1=r3)
+    starting, ending = kappa[:, :, 0:8], kappa[:, :, 8:12]
+    nc.vector.tensor_mul(out=starting, in0=r1[:, :, 0:8], in1=r2[:, :, 0:8])
+    nc.vector.tensor_mul(out=ending, in0=r1[:, :, 7:11], in1=r2[:, :, 6:10])
+    nc.vector.tensor_mul(out=starting, in0=starting, in1=r3[:, :, 0:8])
+    nc.vector.tensor_mul(out=ending, in0=ending, in1=r3[:, :, 5:9])
     root = constant("root", N_KNOTS)
     root_shift = constant("root_shift", N_KNOTS)
-    nc.gpsimd.tensor_tensor(out=root[:, :, 0:8], in0=first_left[:, :, 0:8], in1=half[:], op=ALU.pow)
-    nc.vector.tensor_copy(out=kappa[:, :, 0:8], in_=first_left[:, :, 0:8])
-    first_right = temporary(N_BASIS + 1)
-    nc.vector.tensor_mul(out=first_right, in0=r3, in1=r2[:, :, 1:10])
-    nc.vector.tensor_mul(out=first_right, in0=first_right, in1=r1[:, :, 2:11])
-    nc.vector.tensor_copy(out=kappa[:, :, 8:12], in_=first_right[:, :, 5:9])
-    per_kappa = temporary(N_KNOTS)
-    nc.vector.reciprocal(out=per_kappa, in_=kappa)
-    nc.gpsimd.tensor_tensor(
-        out=root[:, :, 8:12], in0=first_right[:, :, 5:9], in1=half[:, :, 0:4], op=ALU.pow
-    )
-    nc.vector.scalar_tensor_tensor(
-        out=root_shift[:], in0=root[:], scalar=-1.0, in1=knot[:], op0=ALU.mult, op1=ALU.mult
-    )
-
+    rough = temporary(N_KNOTS)
     h4 = temporary(N_BASIS)
-    nc.vector.tensor_sub(out=h4, in0=knot[:, :, 4:], in1=knot[:, :, :N_BASIS])
     up_ratio = constant("up_ratio", N_BASIS)
-    nc.vector.tensor_mul(out=up_ratio[:], in0=h4, in1=r1[:, :, 0:8])
-    nc.vector.tensor_mul(out=up_ratio[:], in0=up_ratio[:], in1=first_left[:, :, 1:9])
-    nc.vector.tensor_mul(out=up_ratio[:], in0=up_ratio[:], in1=per_kappa[:, :, 1:9])
+    per_kappa = temporary(N_KNOTS)
+
+    def take_roots():
+        nc.scalar.activation(out=rough, in_=kappa, func=ACT.Sqrt)
+        first_left = temporary(N_BASIS)
+        nc.gpsimd.tensor_mul(out=first_left, in0=r1[:, :, 1:9], in1=r2[:, :, 1:9])
+        nc.gpsimd.tensor_mul(out=first_left, in0=first_left, in1=r3[:, :, 1:9])
+        nc.gpsimd.tensor_sub(out=h4, in0=knot[:, :, 4:], in1=knot[:, :, :N_BASIS])
+        nc.vector.reciprocal(out=per_kappa, in_=kappa)
+        nc.vector.reciprocal(out=root[:], in_=rough)
+        nc.vector.scalar_tensor_tensor(
+            out=root[:], in0=root[:], scalar=0.5, in1=kappa, op0=ALU.mult, op1=ALU.mult
+        )
+        nc.vector.scalar_tensor_tensor(
+            out=root[:], in0=rough, scalar=0.5, in1=root[:], op0=ALU.mult, op1=ALU.add
+        )
+        nc.vector.scalar_tensor_tensor(
+            out=root_shift[:], in0=root[:], scalar=-1.0, in1=knot[:], op0=ALU.mult, op1=ALU.mult
+        )
+        nc.gpsimd.tensor_mul(out=up_ratio[:], in0=h4, in1=r1[:, :, 0:8])
+        nc.gpsimd.tensor_mul(out=up_ratio[:], in0=up_ratio[:], in1=first_left)
+        nc.gpsimd.tensor_mul(out=up_ratio[:], in0=up_ratio[:], in1=per_kappa[:, :, 1:9])
 
     down_ratio = constant("down_ratio", N_BASIS)
     right_mix = constant("right_mix", PACK)
@@ -121,8 +125,11 @@ def spline_constants(nc, consts, scratch, knot_bf):
             third_weight(
                 at, j, r2[:, :, j : j + 1], (h3[:, :, j + 2 : j + 3], r4[:, :, j + 1 : j + 2])
             )
+        first_right = rough[:, :, 0:N_BASIS]
+        nc.gpsimd.tensor_mul(out=first_right, in0=r3[:, :, 0:8], in1=r2[:, :, 1:9])
+        nc.gpsimd.tensor_mul(out=first_right, in0=first_right, in1=r1[:, :, 2:10])
         nc.gpsimd.tensor_mul(out=down_ratio[:], in0=h4, in1=r1[:, :, 3:11])
-        nc.gpsimd.tensor_mul(out=down_ratio[:], in0=down_ratio[:], in1=first_right[:, :, 0:8])
+        nc.gpsimd.tensor_mul(out=down_ratio[:], in0=down_ratio[:], in1=first_right)
         nc.gpsimd.tensor_mul(out=down_ratio[:], in0=down_ratio[:], in1=per_kappa[:, :, 3:11])
         nc.gpsimd.tensor_scalar(
             out=down_ratio[:], in0=down_ratio[:], scalar1=-1.0, scalar2=1.0, op0=ALU.mult, op1=ALU.mult
@@ -136,7 +143,7 @@ def spline_constants(nc, consts, scratch, knot_bf):
                 at, j, r2[:, :, j + 2 : j + 3], (h3[:, :, j - 1 : j], r4[:, :, j - 1 : j])
             )
 
-    return knot, root, root_shift, up_ratio, down_ratio, right_mix, third, rest
+    return knot, root, root_shift, up_ratio, down_ratio, right_mix, third, take_roots, rest
 
 
 def tile_bsplinekanlayer_kernel(
@@ -176,19 +183,19 @@ def tile_bsplinekanlayer_kernel(
             elif not w_tiles:
                 load_w()
 
-        load_scaler(0)
-        load_slab(0, 0)
         x_rows = pool.tile([P, B_TILES, N_IN], BF16, tag="slab", bufs=PREFETCH, align_bytes=64)
         x_in = x.rearrange("(s p) i -> p s i", p=P)
-        for cols in (slice(0, 2 * P), slice(2 * P, N_IN)):
-            nc.sync.dma_start(out=x_rows[:, :, cols], in_=x_in[:, :, cols])
+        load_scaler(0)
+        nc.sync.dma_start(out=x_rows[:, :, : 2 * P], in_=x_in[:, :, : 2 * P])
+        load_slab(0, 0)
+        nc.sync.dma_start(out=x_rows[:, :, 2 * P :], in_=x_in[:, :, 2 * P :])
         load_slab(0, 1)
         load_slab(1, 0)
         load_scaler(1)
 
         warm = consts.tile([P, 1], F32)
         nc.vector.memset(warm[:], 0.0)
-        nc.scalar.activation(out=warm[:], in_=warm[:], func=ACT.Silu)
+        nc.scalar.activation(out=warm[:], in_=warm[:], func=ACT.Sqrt)
         ident_bf = consts.tile([P, P], BF16)
         make_identity(nc, ident_bf[:])
         ident_f32 = consts.tile([P, P], F32)
@@ -201,8 +208,10 @@ def tile_bsplinekanlayer_kernel(
 
         scratch = pool.tile([P, 1024], F32, tag="grouped", bufs=2, align_bytes=64)
         (
-            knot, root, root_shift, up_ratio, down_ratio, right_mix, third, remaining_constants,
+            knot, root, root_shift, up_ratio, down_ratio, right_mix, third, take_roots,
+            remaining_constants,
         ) = spline_constants(nc, consts, scratch, knot_bf)
+
 
         x_by_feature = keep.tile([P, F_TILES, BATCH], BF16)
         silu_codes = keep.tile([P, BASE_PASSES, BATCH], U32, align_bytes=64)
@@ -271,13 +280,19 @@ def tile_bsplinekanlayer_kernel(
         def take_sides(n):
             c, m = divmod(n, N_KNOTS)
             if 1 <= m <= N_BASIS - (1 if c < EARLY_TILES else 0):
-                nc.scalar.activation(
-                    out=up(c, m), in_=cube(c, m), func=ACT.Relu, scale=up_ratio[:, c, m - 1 : m]
-                )
+                if c >= EARLY_TILES and m in (3,):
+                    nc.vector.tensor_scalar(out=up(c, m), in0=cube(c, m), scalar1=up_ratio[:, c, m - 1 : m], scalar2=0.0, op0=ALU.mult, op1=ALU.max)
+                else:
+                    nc.scalar.activation(
+                        out=up(c, m), in_=cube(c, m), func=ACT.Relu, scale=up_ratio[:, c, m - 1 : m]
+                    )
             if needs_down(c, m):
-                nc.scalar.activation(
-                    out=down(c, m), in_=cube(c, m), func=ACT.Relu, scale=down_ratio[:, c, m - 3 : m - 2]
-                )
+                if c >= EARLY_TILES and m in (10,):
+                    nc.vector.tensor_scalar(out=down(c, m), in0=cube(c, m), scalar1=down_ratio[:, c, m - 3 : m - 2], scalar2=0.0, op0=ALU.mult, op1=ALU.max)
+                else:
+                    nc.scalar.activation(
+                        out=down(c, m), in_=cube(c, m), func=ACT.Relu, scale=down_ratio[:, c, m - 3 : m - 2]
+                    )
 
         def half_tile(store, c, j, tag):
             key = (c, j // PACK)
@@ -337,7 +352,7 @@ def tile_bsplinekanlayer_kernel(
                 if copied(c, form) and FORMS[form][2] == m:
                     nc.scalar.activation(
                         out=half_tile(right, c, FORMS[form][0], "right"), in_=cube(c, m),
-                        func=ACT.Relu, scale=right_mix[:, c, m - 4 : m - 3],
+                        func=ACT.Relu, scale=right_mix[:, c, m - 4 : m - 3] if FORMS[form][0] < PACK else 1.0,
                     )
 
         def take_minimum(n):
@@ -359,41 +374,56 @@ def tile_bsplinekanlayer_kernel(
         def negative(c, half):
             return EARLY_TILES <= c < F_TILES - 1 and half == 1
 
-        def combine(n):
-            c, m = divmod(n, N_KNOTS)
-            if c < EARLY_TILES and 1 <= m <= N_BASIS and not three_term(c, m - 1):
-                nc.vector.tensor_tensor(
-                    out=half_tile(left, c, m - 1, "left"), in0=cube(c, m - 1), in1=up(c, m), op=ALU.subtract
-                )
-            j = m - 4
-            if j >= 0 and not three_term(c, j) and not negative(c, j // PACK):
-                nc.vector.scalar_tensor_tensor(
-                    out=half_tile(right, c, j, "right"), in0=cube(c, m),
-                    scalar=right_mix[:, c, j : j + 1] if j < PACK else -1.0,
-                    in1=down(c, m - 1), op0=ALU.mult, op1=ALU.subtract,
-                )
+        def runs_of(c, half):
+            runs = []
+            for j in range(half * PACK, (half + 1) * PACK):
+                if three_term(c, j):
+                    continue
+                if runs and runs[-1][1] == j:
+                    runs[-1] = (runs[-1][0], j + 1)
+                else:
+                    runs.append((j, j + 1))
+            return runs
 
-        def combine_four(n):
+        def combine(n, fours):
             c, m = divmod(n, N_KNOTS)
-            if c < EARLY_TILES:
-                return
-            if m in (4, 8):
-                half = m // 4 - 1
-                half_tile(left, c, half * PACK, "left")
-                a, b = cubes[(c, half)], ups[(c, half)]
-                if negative(c, half):
-                    a, b = b, a
-                nc.vector.tensor_tensor(out=left[(c, half)][:], in0=a[:], in1=b[:], op=ALU.subtract)
-            if m == N_KNOTS - 1 and negative(c, 1):
-                half_tile(right, c, PACK, "right")
-                nc.vector.tensor_tensor(
-                    out=right[(c, 1)][:], in0=cubes[(c, 2)][:], in1=downs[(c, 1)][:], op=ALU.add
+            for half in range(HALVES):
+                for first, end in runs_of(c, half):
+                    if (end - first == PACK) != fours:
+                        continue
+                    planes = slice(first - half * PACK, end - half * PACK)
+                    if m == end:
+                        half_tile(left, c, first, "left")
+                        a, b = cubes[(c, half)], ups[(c, half)]
+                        if negative(c, half):
+                            a, b = b, a
+                        nc.vector.tensor_tensor(
+                            out=left[(c, half)][:, planes, :], in0=a[:, planes, :], in1=b[:, planes, :],
+                            op=ALU.subtract,
+                        )
+                    if half == 1 and m == end + 3:
+                        half_tile(right, c, first, "right")
+                        to, a, b = (t[:, planes, :] for t in (right[(c, 1)], cubes[(c, 2)], downs[(c, 1)]))
+                        if negative(c, half):
+                            nc.vector.tensor_tensor(out=to, in0=a, in1=b, op=ALU.add)
+                        else:
+                            nc.vector.scalar_tensor_tensor(
+                                out=to, in0=a, scalar=-1.0, in1=b, op0=ALU.mult, op1=ALU.subtract
+                            )
+
+        def combine_right(n):
+            c, m = divmod(n, N_KNOTS)
+            j = m - 4
+            if 0 <= j < PACK and not three_term(c, j):
+                nc.vector.scalar_tensor_tensor(
+                    out=half_tile(right, c, j, "right"), in0=cube(c, m), scalar=right_mix[:, c, j : j + 1],
+                    in1=down(c, m - 1), op0=ALU.mult, op1=ALU.subtract,
                 )
 
         def take_peak(c, half):
             rest = [t for t in range(PACK) if not three_term(c, half * PACK + t)]
             parts = [(slice(rest[0], rest[-1] + 1), ALU.min if negative(c, half) else ALU.max)]
-            if 1 <= c < EARLY_TILES and half == 0:
+            if 1 <= c < EARLY_TILES:
                 parts.append((slice(0, PACK, PACK - 1), ALU.min))
             for planes, op in parts:
                 nc.vector.tensor_tensor(
@@ -526,7 +556,7 @@ def tile_bsplinekanlayer_kernel(
             for half in range(HALVES):
                 ready = c * N_KNOTS + (7 if half == 0 else 11) + COMBINE_LAG
                 if c < EARLY_TILES and half == 1:
-                    steps = (("peak", 0), ("regroup", 3), ("quantise", 5))
+                    steps = (("peak", 0 if c == 0 else 2), ("regroup", 3), ("quantise", 5))
                 elif c < F_TILES - 1 or half == 0:
                     steps = (("peak", 1), ("regroup", 2), ("quantise", 5))
                 else:
@@ -551,9 +581,10 @@ def tile_bsplinekanlayer_kernel(
             copy_form(n - FORM_LAG - 2)
             take_diagonal(n - 1)
             if 0 <= n - COMBINE_LAG + 1 < STEPS:
-                combine_four(n - COMBINE_LAG + 1)
+                combine(n - COMBINE_LAG + 1, True)
             if 0 <= n - COMBINE_LAG < STEPS:
-                combine(n - COMBINE_LAG)
+                combine(n - COMBINE_LAG, False)
+                combine_right(n - COMBINE_LAG)
             for kind, c, half in finish.get(n, []):
                 if kind == "quantise":
                     quantise_half(c, half)
@@ -563,14 +594,14 @@ def tile_bsplinekanlayer_kernel(
             scalers_flipped = []
             for part in range(2):
                 flip_scaler(psum_flip, 0, part)
-                copy_pairs(0, part)
+            copy_pairs(0, 0)
+            take_roots()
+            nc.scalar.activation(out=warm[:], in_=warm[:], func=ACT.Silu)
             load_scaler(2)
-            for k in range(HALF_O // 2):
-                flip_chunk(psum_flip, k)
-                scale_chunk(k)
             for pair in range(F_TILES // 2):
                 if pair == 1:
-                    for k in range(HALF_O // 2, HALF_O):
+                    copy_pairs(0, 1)
+                    for k in range(HALF_O):
                         flip_chunk(psum_flip, k)
                         scale_chunk(k)
                 flipped = psum_flip.tile([P, 2, BATCH], BF16, tag="flip", bufs=8)
@@ -582,7 +613,7 @@ def tile_bsplinekanlayer_kernel(
                             ident_bf[:],
                         )
                 if pair == 0:
-                    nc.scalar.copy(out=x_by_feature[:, 0, :], in_=flipped[:, 0, :])
+                    nc.vector.tensor_copy(out=x_by_feature[:, 0, :], in_=flipped[:, 0, :])
                     for n in range(LOOKAHEAD):
                         take_square(n)
                     nc.vector.tensor_copy(out=x_by_feature[:, 1, :], in_=flipped[:, 1, :])

@@ -36,14 +36,18 @@ COMBINE_LAG = 4
 FORM_LAG = 3
 TERMS = 3
 END_KNOTS = (0, N_KNOTS - 1)
-COPIED = (0, 1, 2, 3)
-FORMS = ((0, 0, 4), (3, 3, 7), (4, 6, 4), (7, 9, 7), (1, 1, 5))
+COPIED = (0, 2)
+FORMS = ((0, 0, 4), (1, 1, 5), (3, 3, 7))
+SUM_STEP = 10
 PREFETCH = 3
 HALF_O = O_TILES // 2
 CHUNKS = F_TILES * O_TILES
 FIRST_CHUNK_STEP = 3
 EARLY_TILES = 4
-SWITCH = EARLY_TILES * N_KNOTS + 5
+FORM_TILES = 4
+CHUNK_STEPS = 46
+RING = 7
+SWITCH = EARLY_TILES * N_KNOTS + 7
 STEPS = F_TILES * N_KNOTS
 
 
@@ -118,10 +122,17 @@ def spline_constants(nc, consts, scratch, knot_bf):
         nc.gpsimd.tensor_mul(out=other, in0=third_span[0], in1=third_span[1])
         nc.gpsimd.tensor_mul(out=weight, in0=weight, in1=other)
 
+    neg_knot = consts.tile([P, EARLY_TILES, PACK], F32, name="neg_knot")
+
+    def flip_sign(values):
+        nc.gpsimd.tensor_scalar(
+            out=values, in0=values, scalar1=-1.0, scalar2=1.0, op0=ALU.mult, op1=ALU.mult
+        )
+
     def rest():
         r4 = temporary(N_BASIS)
         nc.vector.reciprocal(out=r4, in_=h4)
-        for at, j in ((0, 0), (4, 1), (1, 3)):
+        for at, j in ((0, 0), (1, 1), (2, 3)):
             third_weight(
                 at, j, r2[:, :, j : j + 1], (h3[:, :, j + 2 : j + 3], r4[:, :, j + 1 : j + 2])
             )
@@ -131,19 +142,16 @@ def spline_constants(nc, consts, scratch, knot_bf):
         nc.gpsimd.tensor_mul(out=down_ratio[:], in0=h4, in1=r1[:, :, 3:11])
         nc.gpsimd.tensor_mul(out=down_ratio[:], in0=down_ratio[:], in1=first_right)
         nc.gpsimd.tensor_mul(out=down_ratio[:], in0=down_ratio[:], in1=per_kappa[:, :, 3:11])
-        nc.gpsimd.tensor_scalar(
-            out=down_ratio[:], in0=down_ratio[:], scalar1=-1.0, scalar2=1.0, op0=ALU.mult, op1=ALU.mult
-        )
         nc.gpsimd.tensor_mul(out=right_mix[:], in0=first_right[:, :, 1:5], in1=per_kappa[:, :, 4:8])
-        nc.gpsimd.tensor_scalar(
-            out=right_mix[:], in0=right_mix[:], scalar1=-1.0, scalar2=1.0, op0=ALU.mult, op1=ALU.mult
-        )
-        for at, j in ((2, 4), (3, 7)):
-            third_weight(
-                at, j, r2[:, :, j + 2 : j + 3], (h3[:, :, j - 1 : j], r4[:, :, j - 1 : j])
-            )
+        flip_sign(up_ratio[:, 0:EARLY_TILES, 3:7])
+        flip_sign(down_ratio[:, 0:EARLY_TILES, 0:1])
+        flip_sign(down_ratio[:, 0:EARLY_TILES, 5:8])
+        flip_sign(down_ratio[:, EARLY_TILES:, :])
+        flip_sign(right_mix[:, EARLY_TILES:, :])
+        nc.gpsimd.tensor_copy(out=neg_knot[:], in_=knot[:, 0:EARLY_TILES, 4:8])
+        flip_sign(neg_knot[:])
 
-    return knot, root, root_shift, up_ratio, down_ratio, right_mix, third, take_roots, rest
+    return knot, neg_knot, root, root_shift, up_ratio, down_ratio, right_mix, third, take_roots, rest
 
 
 def tile_bsplinekanlayer_kernel(
@@ -208,21 +216,29 @@ def tile_bsplinekanlayer_kernel(
 
         scratch = pool.tile([P, 1024], F32, tag="grouped", bufs=2, align_bytes=64)
         (
-            knot, root, root_shift, up_ratio, down_ratio, right_mix, third, take_roots,
+            knot, neg_knot, root, root_shift, up_ratio, down_ratio, right_mix, third, take_roots,
             remaining_constants,
         ) = spline_constants(nc, consts, scratch, knot_bf)
 
 
-        x_by_feature = keep.tile([P, F_TILES, BATCH], BF16)
+        x_pairs = []
+        for q in range(F_TILES // 2):
+            x_pair = pool.tile([P, 2, BATCH], BF16, tag="x_pair", bufs=4, align_bytes=64)
+            x_pairs.append(x_pair)
+
+        def x_of(c):
+            return x_pairs[c // 2][:, c % 2, :]
+
         silu_codes = keep.tile([P, BASE_PASSES, BATCH], U32, align_bytes=64)
         silu_scales = keep.tile([P, BASE_PASSES, BATCH], U8, align_bytes=64)
         ssw_codes = keep.tile([P, SPLINE_PASSES, N_OUT], U32, align_bytes=64)
         ssw_scales = keep.tile([P, SPLINE_PASSES // 4, N_OUT], U8, align_bytes=64)
 
         def forms_of(c):
-            if not 0 <= c < EARLY_TILES:
-                return ()
-            return range(len(FORMS) if c < EARLY_TILES - 1 else len(FORMS) - 1)
+            return range(len(FORMS)) if 0 <= c < FORM_TILES else ()
+
+        def summed(c, half):
+            return 0 <= c < EARLY_TILES and half == 1
 
         def three_term(c, j):
             return any(FORMS[form][0] == j for form in forms_of(c))
@@ -231,13 +247,15 @@ def tile_bsplinekanlayer_kernel(
             c, m = divmod(n, N_KNOTS)
             return [(form, m - FORMS[form][1]) for form in forms_of(c) if 0 <= m - FORMS[form][1] < TERMS]
 
-        def needs_down(c, m):
-            if not 3 <= m <= 10:
-                return False
-            return m >= 6 or any(
-                not three_term(c, j) for j in (m - 4, m - 3) if 0 <= j and (j > 3 or j + 3 == m)
-            )
+        def needs_up(c, m):
+            if 1 <= m <= N_BASIS and not three_term(c, m - 1):
+                return True
+            return any(m - FORMS[form][1] in (1, 2) for form in forms_of(c))
 
+        def needs_down(c, m):
+            return 0 <= m - 3 < N_BASIS and not three_term(c, m - 3)
+
+        neg_x = {}
         square = {}
         cubes = {}
         ups = {}
@@ -266,28 +284,34 @@ def tile_bsplinekanlayer_kernel(
             c, m = divmod(n, N_KNOTS)
             square[n] = pool.tile([P, BATCH], F32, tag="square", bufs=4, name="square")
             nc.scalar.activation(
-                out=square[n][:], in_=x_by_feature[:, c, :], func=ACT.Square,
+                out=square[n][:], in_=x_of(c), func=ACT.Square,
                 scale=root[:, c, m : m + 1], bias=root_shift[:, c, m : m + 1],
             )
 
         def take_cube(n):
             c, m = divmod(n, N_KNOTS)
+            if c < EARLY_TILES and m // PACK == 1:
+                if m == PACK:
+                    neg_x[c] = pool.tile([P, BATCH], BF16, tag="neg_x", bufs=1, name="neg_x")
+                    nc.vector.tensor_scalar_mul(out=neg_x[c][:], in0=x_of(c), scalar1=-1.0)
+                values, at = neg_x[c][:], neg_knot[:, c, m - PACK : m - PACK + 1]
+            else:
+                values, at = x_of(c), knot[:, c, m : m + 1]
             nc.vector.scalar_tensor_tensor(
-                out=cube(c, m), in0=x_by_feature[:, c, :], scalar=knot[:, c, m : m + 1],
-                in1=square[n][:], op0=ALU.subtract, op1=ALU.mult,
+                out=cube(c, m), in0=values, scalar=at, in1=square[n][:], op0=ALU.subtract, op1=ALU.mult
             )
 
         def take_sides(n):
             c, m = divmod(n, N_KNOTS)
-            if 1 <= m <= N_BASIS - (1 if c < EARLY_TILES else 0):
-                if c >= EARLY_TILES and m in (3,):
+            if needs_up(c, m):
+                if c >= EARLY_TILES and m == 3:
                     nc.vector.tensor_scalar(out=up(c, m), in0=cube(c, m), scalar1=up_ratio[:, c, m - 1 : m], scalar2=0.0, op0=ALU.mult, op1=ALU.max)
                 else:
                     nc.scalar.activation(
                         out=up(c, m), in_=cube(c, m), func=ACT.Relu, scale=up_ratio[:, c, m - 1 : m]
                     )
             if needs_down(c, m):
-                if c >= EARLY_TILES and m in (10,):
+                if False:
                     nc.vector.tensor_scalar(out=down(c, m), in0=cube(c, m), scalar1=down_ratio[:, c, m - 3 : m - 2], scalar2=0.0, op0=ALU.mult, op1=ALU.max)
                 else:
                     nc.scalar.activation(
@@ -303,37 +327,73 @@ def tile_bsplinekanlayer_kernel(
         form_banks = {}
         diagonals = {}
 
-        def term_of(c, form, term):
-            j, first_knot, outer_knot = FORMS[form]
-            m = first_knot + term
-            if j < PACK:
-                return (
-                    (ident_f32, cube(c, m)), (minus_ident, up(c, m)), (diagonals.get((c, form)), up(c, m))
-                )[term]
-            return (
-                (diagonals.get((c, form)), down(c, m)), (minus_ident, down(c, m)), (minus_ident, cube(c, m))
-            )[term]
-
         def take_diagonal(n):
             c = n // N_KNOTS
             for form, term in terms_of(n):
-                if term == (TERMS - 1 if FORMS[form][0] < PACK else 0):
-                    tile = pool.tile([P, P], F32, tag="diagonal", bufs=5, name="diagonal")
+                if term == TERMS - 1:
+                    tile = pool.tile([P, P], F32, tag="diagonal", bufs=4, name="diagonal")
                     nc.scalar.activation(
                         out=tile[:], in_=ident_f32[:], func=ACT.Copy, scale=third[:, c, form : form + 1]
                     )
                     diagonals[(c, form)] = tile
 
         def add_term(psum, n):
-            c = n // N_KNOTS
+            c, m = divmod(n, N_KNOTS)
             for form, term in terms_of(n):
                 if term == 0:
                     form_banks[(c, form)] = psum.tile([P, BATCH], F32, tag="flip", bufs=8, name="form")
-                weight, values = term_of(c, form, term)
+                weight = (ident_f32, minus_ident, diagonals.get((c, form)))[term]
                 nc.tensor.matmul(
-                    out=form_banks[(c, form)][:], lhsT=weight[:], rhs=values,
+                    out=form_banks[(c, form)][:], lhsT=weight[:], rhs=cube(c, m) if term == 0 else up(c, m),
                     start=(term == 0), stop=(term == TERMS - 1),
                 )
+
+        sum_banks = {}
+        back_banks = {}
+
+        def sum_of(n):
+            c, t = divmod(n - SUM_STEP, N_KNOTS)
+            return (c, PACK + t) if summed(c, 1) and t < PACK else None
+
+        def add_sums(psum, n):
+            if sum_of(n) is None:
+                return
+            c, j = sum_of(n)
+            for side, pair in (("left", (cube(c, j), up(c, j + 1))), ("right", (cube(c, j + 4), down(c, j + 3)))):
+                bank = psum.tile([P, BATCH], F32, tag="flip", bufs=8, name="sum")
+                for s in range(B_TILES):
+                    rows = slice(s * P, (s + 1) * P)
+                    for i, values in enumerate(pair):
+                        nc.tensor.matmul(
+                            out=bank[:, rows], lhsT=values[:, rows], rhs=ident_f32[:],
+                            start=(i == 0), stop=(i == 1), is_transpose=True,
+                        )
+                sum_banks[(c, j, side)] = bank
+
+        def copy_sum(n):
+            if sum_of(n) is not None:
+                c, j = sum_of(n)
+                nc.scalar.copy(out=half_tile(left, c, j, "left"), in_=sum_banks[(c, j, "left")][:])
+
+        def bound_sum(n):
+            if sum_of(n) is not None:
+                c, j = sum_of(n)
+                to = half_tile(left, c, j, "left")
+                nc.vector.tensor_tensor(out=to, in0=sum_banks[(c, j, "right")][:], in1=to, op=ALU.min)
+
+        def turn_back(psum, n):
+            for kind, c, half in finish.get(n, []):
+                if kind == "back":
+                    for part in range(2):
+                        bank = psum.tile([P, PACK, BATCH // 2], BF16, tag="flip", bufs=8, name="back")
+                        for t in range(PACK):
+                            for s in range(2):
+                                nc.tensor.transpose(
+                                    bank[:, t, s * P : (s + 1) * P],
+                                    left[(c, half)][:, t, (2 * part + s) * P : (2 * part + s + 1) * P],
+                                    ident_bf[:],
+                                )
+                        back_banks[(c, part)] = bank
 
         def copied(c, form):
             return c >= 1 and form in COPIED
@@ -352,7 +412,7 @@ def tile_bsplinekanlayer_kernel(
                 if copied(c, form) and FORMS[form][2] == m:
                     nc.scalar.activation(
                         out=half_tile(right, c, FORMS[form][0], "right"), in_=cube(c, m),
-                        func=ACT.Relu, scale=right_mix[:, c, m - 4 : m - 3] if FORMS[form][0] < PACK else 1.0,
+                        func=ACT.Relu, scale=right_mix[:, c, m - 4 : m - 3],
                     )
 
         def take_minimum(n):
@@ -360,24 +420,19 @@ def tile_bsplinekanlayer_kernel(
             for form, term in terms_of(n):
                 if term == TERMS - 1 and not copied(c, form):
                     j, first_knot, outer_knot = FORMS[form]
-                    to = half_tile(left, c, j, "left")
-                    if j < PACK:
-                        nc.vector.scalar_tensor_tensor(
-                            out=to, in0=cube(c, outer_knot), scalar=right_mix[:, c, j : j + 1],
-                            in1=form_banks[(c, form)][:], op0=ALU.mult, op1=ALU.min,
-                        )
-                    else:
-                        nc.vector.tensor_tensor(
-                            out=to, in0=cube(c, outer_knot), in1=form_banks[(c, form)][:], op=ALU.min
-                        )
+                    nc.vector.scalar_tensor_tensor(
+                        out=half_tile(left, c, j, "left"), in0=cube(c, outer_knot),
+                        scalar=right_mix[:, c, j : j + 1], in1=form_banks[(c, form)][:],
+                        op0=ALU.mult, op1=ALU.min,
+                    )
 
         def negative(c, half):
-            return EARLY_TILES <= c < F_TILES - 1 and half == 1
+            return c < F_TILES - 1 and half == 1
 
         def runs_of(c, half):
             runs = []
             for j in range(half * PACK, (half + 1) * PACK):
-                if three_term(c, j):
+                if three_term(c, j) or summed(c, half):
                     continue
                 if runs and runs[-1][1] == j:
                     runs[-1] = (runs[-1][0], j + 1)
@@ -422,8 +477,8 @@ def tile_bsplinekanlayer_kernel(
 
         def take_peak(c, half):
             rest = [t for t in range(PACK) if not three_term(c, half * PACK + t)]
-            parts = [(slice(rest[0], rest[-1] + 1), ALU.min if negative(c, half) else ALU.max)]
-            if 1 <= c < EARLY_TILES:
+            parts = [(slice(rest[0], rest[-1] + 1), ALU.min if negative(c, half) else ALU.max)] if rest else []
+            if 1 <= c < FORM_TILES and half == 0:
                 parts.append((slice(0, PACK, PACK - 1), ALU.min))
             for planes, op in parts:
                 nc.vector.tensor_tensor(
@@ -439,6 +494,19 @@ def tile_bsplinekanlayer_kernel(
             of = left[(c, half)][:].rearrange("p t (g i) -> p g t i", i=4)
             nc.scalar.activation(out=to, in_=of, func=ACT.Relu, scale=-1.0 if negative(c, half) else 1.0)
 
+        def group_back(c, half):
+            grouped[(c, half)] = pool.tile(
+                [P, BATCH, PACK], BF16, tag="grouped", bufs=2, align_bytes=64, name="grouped"
+            )
+            for part in range(2):
+                nc.scalar.activation(
+                    out=grouped[(c, half)][:, part * BATCH // 2 : (part + 1) * BATCH // 2, :].rearrange(
+                        "p (g i) t -> p g t i", i=4
+                    ),
+                    in_=back_banks[(c, part)][:].rearrange("p t (g i) -> p g t i", i=4),
+                    func=ACT.Relu, scale=-1.0,
+                )
+
         def take_grouped_peak(c, half, cols):
             if (c, half) not in grouped:
                 grouped[(c, half)] = pool.tile(
@@ -453,12 +521,28 @@ def tile_bsplinekanlayer_kernel(
                 op1=ALU.max,
             )
 
+        parked = {}
+
+        def code_tiles(k):
+            if RING + 2 <= k < EARLY_TILES * HALVES:
+                if not parked:
+                    parked["codes"] = pool.tile(
+                        [P, 4, BATCH], U32, tag="slab", bufs=PREFETCH, align_bytes=64, name="parked"
+                    )
+                    parked["scales"] = pool.tile([P, 4, BATCH], U8, tag="pairs", bufs=3, align_bytes=64, name="parked_scales")
+                at = k - RING - 2
+                return parked["codes"][:, at, :], parked["scales"][:, at, :]
+            if RING <= k < RING + 2:
+                k_codes = pool.tile([P, BATCH], U32, tag="x_pair", bufs=4, align_bytes=64, name="k_codes_x")
+            else:
+                k_codes = pool.tile([P, BATCH], U32, tag="k_codes", bufs=RING, align_bytes=64, name="k_codes")
+            k_scales = pool.tile([P, BATCH], U8, tag="k_scales", bufs=RING + 1, align_bytes=64, name="k_scales")
+            return k_codes[:], k_scales[:]
+
         def quantise_half(c, half, cols=slice(0, BATCH)):
             k = c * HALVES + half
             if k not in codes:
-                k_codes = pool.tile([P, BATCH], U32, tag="k_codes", bufs=7, align_bytes=64, name="k_codes")
-                k_scales = pool.tile([P, BATCH], U8, tag="k_scales", bufs=7, align_bytes=64, name="k_scales")
-                codes[k] = (k_codes, k_scales)
+                codes[k] = code_tiles(k)
             nc.vector.quantize_mx(
                 out=codes[k][0][:, cols].bitcast(FP8X4), scales=codes[k][1][:, cols],
                 in_=grouped[(c, half)][:, cols, :].rearrange("p b t -> p (b t)"),
@@ -480,7 +564,7 @@ def tile_bsplinekanlayer_kernel(
 
         def copy_pairs(c, part):
             bank = scaler_banks.pop((c, part))
-            pairs[(c, part)] = pool.tile([P, N_TILE, 2], BF16, tag="pairs", bufs=3, name="pairs")
+            pairs[(c, part)] = pool.tile([P, N_TILE, 2], BF16, tag="pairs", bufs=3, align_bytes=64, name="pairs")
             nc.scalar.copy(
                 out=pairs[(c, part)][:], in_=bank[:].unsqueeze(2).to_broadcast([P, N_TILE, 2])
             )
@@ -548,15 +632,16 @@ def tile_bsplinekanlayer_kernel(
             w_tiles["scales"] = w_scales
 
         def chunks_done(n):
-            behind = max(0, n - 2) * (CHUNKS - HALF_O) // (SWITCH - 4 - FIRST_CHUNK_STEP)
+            behind = max(0, n - 2) * (CHUNKS - HALF_O) // CHUNK_STEPS
             return min(CHUNKS, HALF_O + behind)
 
         finish = {}
         for c in range(F_TILES):
             for half in range(HALVES):
                 ready = c * N_KNOTS + (7 if half == 0 else 11) + COMBINE_LAG
-                if c < EARLY_TILES and half == 1:
-                    steps = (("peak", 0 if c == 0 else 2), ("regroup", 3), ("quantise", 5))
+                if summed(c, half):
+                    ready = c * N_KNOTS + SUM_STEP + PACK - 1
+                    steps = (("back", 4), ("from_back", 5), ("quantise", 7))
                 elif c < F_TILES - 1 or half == 0:
                     steps = (("peak", 1), ("regroup", 2), ("quantise", 5))
                 else:
@@ -576,7 +661,11 @@ def tile_bsplinekanlayer_kernel(
                     take_peak(c, half)
                 elif kind == "regroup":
                     regroup(c, half)
+                elif kind == "from_back":
+                    group_back(c, half)
             take_minimum(n - FORM_LAG - 2)
+            copy_sum(n - 1)
+            bound_sum(n - 3)
             copy_outer(n - 1)
             copy_form(n - FORM_LAG - 2)
             take_diagonal(n - 1)
@@ -613,12 +702,12 @@ def tile_bsplinekanlayer_kernel(
                             ident_bf[:],
                         )
                 if pair == 0:
-                    nc.vector.tensor_copy(out=x_by_feature[:, 0, :], in_=flipped[:, 0, :])
+                    nc.vector.tensor_copy(out=x_of(0), in_=flipped[:, 0, :])
                     for n in range(LOOKAHEAD):
                         take_square(n)
-                    nc.vector.tensor_copy(out=x_by_feature[:, 1, :], in_=flipped[:, 1, :])
+                    nc.vector.tensor_copy(out=x_of(1), in_=flipped[:, 1, :])
                 elif pair == 1:
-                    nc.vector.tensor_copy(out=x_by_feature[:, 2 * pair : 2 * pair + 2, :], in_=flipped[:])
+                    nc.vector.tensor_copy(out=x_pairs[pair][:], in_=flipped[:])
                 else:
                     late_copies.append((pair, flipped))
             remaining_constants()
@@ -669,6 +758,8 @@ def tile_bsplinekanlayer_kernel(
                         if c + 2 < F_TILES:
                             load_scaler(c + 2)
                 add_term(psum_flip, n - FORM_LAG)
+                add_sums(psum_flip, n)
+                turn_back(psum_flip, n)
                 run_step(n)
                 if n == 0:
                     quantise_ssw(0, 0)
@@ -676,7 +767,7 @@ def tile_bsplinekanlayer_kernel(
                     copy_pairs(*scalers_flipped.pop(0))
                 if n in (2, 4):
                     pair, flipped = late_copies.pop(0)
-                    nc.vector.tensor_copy(out=x_by_feature[:, 2 * pair : 2 * pair + 2, :], in_=flipped[:])
+                    nc.vector.tensor_copy(out=x_pairs[pair][:], in_=flipped[:])
                 if n in (5, 9):
                     quantise_silu((n - 5) // 4)
                 for k in range(chunks_done(n - 1), chunks_done(n)):

@@ -36,18 +36,18 @@ COMBINE_LAG = 4
 FORM_LAG = 3
 TERMS = 3
 END_KNOTS = (0, N_KNOTS - 1)
-COPIED = (0, 2)
+COPIED = ()
 FORMS = ((0, 0, 4), (1, 1, 5), (3, 3, 7))
-SUM_STEP = 10
+SUM_STEP = 9
 PREFETCH = 3
 HALF_O = O_TILES // 2
 CHUNKS = F_TILES * O_TILES
 FIRST_CHUNK_STEP = 3
-EARLY_TILES = 4
-FORM_TILES = 4
-CHUNK_STEPS = 46
+EARLY_TILES = 6
+FORM_TILES = 6
+CHUNK_STEPS = 66
 RING = 7
-SWITCH = EARLY_TILES * N_KNOTS + 7
+SWITCH = EARLY_TILES * N_KNOTS + 5
 STEPS = F_TILES * N_KNOTS
 
 
@@ -478,7 +478,7 @@ def tile_bsplinekanlayer_kernel(
         def take_peak(c, half):
             rest = [t for t in range(PACK) if not three_term(c, half * PACK + t)]
             parts = [(slice(rest[0], rest[-1] + 1), ALU.min if negative(c, half) else ALU.max)] if rest else []
-            if 1 <= c < FORM_TILES and half == 0:
+            if False:
                 parts.append((slice(0, PACK, PACK - 1), ALU.min))
             for planes, op in parts:
                 nc.vector.tensor_tensor(
@@ -527,16 +527,18 @@ def tile_bsplinekanlayer_kernel(
             if RING + 2 <= k < EARLY_TILES * HALVES:
                 if not parked:
                     parked["codes"] = pool.tile(
-                        [P, 4, BATCH], U32, tag="slab", bufs=PREFETCH, align_bytes=64, name="parked"
+                        [P, 3, BATCH], U32, tag="slab", bufs=PREFETCH, align_bytes=64, name="parked"
                     )
-                    parked["scales"] = pool.tile([P, 4, BATCH], U8, tag="pairs", bufs=3, align_bytes=64, name="parked_scales")
+                    parked["scales"] = pool.tile(
+                        [P, 3, BATCH], U8, tag="pairs", bufs=2, align_bytes=64, name="parked_scales"
+                    )
                 at = k - RING - 2
                 return parked["codes"][:, at, :], parked["scales"][:, at, :]
             if RING <= k < RING + 2:
                 k_codes = pool.tile([P, BATCH], U32, tag="x_pair", bufs=4, align_bytes=64, name="k_codes_x")
             else:
                 k_codes = pool.tile([P, BATCH], U32, tag="k_codes", bufs=RING, align_bytes=64, name="k_codes")
-            k_scales = pool.tile([P, BATCH], U8, tag="k_scales", bufs=RING + 1, align_bytes=64, name="k_scales")
+            k_scales = pool.tile([P, BATCH], U8, tag="k_scales", bufs=RING + 2, align_bytes=64, name="k_scales")
             return k_codes[:], k_scales[:]
 
         def quantise_half(c, half, cols=slice(0, BATCH)):
@@ -564,7 +566,7 @@ def tile_bsplinekanlayer_kernel(
 
         def copy_pairs(c, part):
             bank = scaler_banks.pop((c, part))
-            pairs[(c, part)] = pool.tile([P, N_TILE, 2], BF16, tag="pairs", bufs=3, align_bytes=64, name="pairs")
+            pairs[(c, part)] = pool.tile([P, N_TILE, 2], BF16, tag="pairs", bufs=2, align_bytes=64, name="pairs")
             nc.scalar.copy(
                 out=pairs[(c, part)][:], in_=bank[:].unsqueeze(2).to_broadcast([P, N_TILE, 2])
             )
@@ -641,7 +643,7 @@ def tile_bsplinekanlayer_kernel(
                 ready = c * N_KNOTS + (7 if half == 0 else 11) + COMBINE_LAG
                 if summed(c, half):
                     ready = c * N_KNOTS + SUM_STEP + PACK - 1
-                    steps = (("back", 4), ("from_back", 5), ("quantise", 7))
+                    steps = (("back", 3), ("from_back", 4), ("quantise", 6))
                 elif c < F_TILES - 1 or half == 0:
                     steps = (("peak", 1), ("regroup", 2), ("quantise", 5))
                 else:
@@ -665,7 +667,7 @@ def tile_bsplinekanlayer_kernel(
                     group_back(c, half)
             take_minimum(n - FORM_LAG - 2)
             copy_sum(n - 1)
-            bound_sum(n - 3)
+            bound_sum(n - 2)
             copy_outer(n - 1)
             copy_form(n - FORM_LAG - 2)
             take_diagonal(n - 1)
@@ -749,10 +751,10 @@ def tile_bsplinekanlayer_kernel(
                 for k in range(chunks_done(n + 1), chunks_done(n + 2)):
                     flip_chunk(psum_flip, k)
                     c, s = divmod(k, O_TILES)
-                    if s == HALF_O and c + 1 < F_TILES:
+                    if s == O_TILES - 1 and c + 1 < F_TILES:
                         flip_scaler(psum_flip, c + 1, 0)
                         scalers_flipped.append((c + 1, 0))
-                    elif s == 0 and c > 0:
+                    elif s == HALF_O - 1 and c > 0:
                         flip_scaler(psum_flip, c, 1)
                         scalers_flipped.append((c, 1))
                         if c + 2 < F_TILES:

@@ -37,7 +37,7 @@ FORM_LAG = 3
 TERMS = 3
 END_KNOTS = (0, N_KNOTS - 1)
 COPIED = ()
-FORMS = ((0, 0, 4), (1, 1, 5), (3, 3, 7))
+FORMS = ((0, 0, 4), (2, 2, 6), (3, 3, 7))
 SUM_STEP = 9
 PREFETCH = 3
 HALF_O = O_TILES // 2
@@ -132,7 +132,7 @@ def spline_constants(nc, consts, scratch, knot_bf):
     def rest():
         r4 = temporary(N_BASIS)
         nc.vector.reciprocal(out=r4, in_=h4)
-        for at, j in ((0, 0), (1, 1), (2, 3)):
+        for at, j in ((0, 0), (1, 2), (2, 3)):
             third_weight(
                 at, j, r2[:, :, j : j + 1], (h3[:, :, j + 2 : j + 3], r4[:, :, j + 1 : j + 2])
             )
@@ -291,15 +291,15 @@ def tile_bsplinekanlayer_kernel(
         def take_cube(n):
             c, m = divmod(n, N_KNOTS)
             if c < EARLY_TILES and m // PACK == 1:
-                if m == PACK:
-                    neg_x[c] = pool.tile([P, BATCH], BF16, tag="neg_x", bufs=1, name="neg_x")
-                    nc.vector.tensor_scalar_mul(out=neg_x[c][:], in0=x_of(c), scalar1=-1.0)
                 values, at = neg_x[c][:], neg_knot[:, c, m - PACK : m - PACK + 1]
             else:
                 values, at = x_of(c), knot[:, c, m : m + 1]
             nc.vector.scalar_tensor_tensor(
                 out=cube(c, m), in0=values, scalar=at, in1=square[n][:], op0=ALU.subtract, op1=ALU.mult
             )
+            if c < EARLY_TILES and m == PACK - 2:
+                neg_x[c] = pool.tile([P, BATCH], BF16, tag="neg_x", bufs=1, name="neg_x")
+                nc.vector.tensor_scalar_mul(out=neg_x[c][:], in0=x_of(c), scalar1=-1.0)
 
         def take_sides(n):
             c, m = divmod(n, N_KNOTS)
@@ -332,8 +332,9 @@ def tile_bsplinekanlayer_kernel(
             for form, term in terms_of(n):
                 if term == TERMS - 1:
                     tile = pool.tile([P, P], F32, tag="diagonal", bufs=4, name="diagonal")
-                    nc.scalar.activation(
-                        out=tile[:], in_=ident_f32[:], func=ACT.Copy, scale=third[:, c, form : form + 1]
+                    nc.gpsimd.tensor_scalar(
+                        out=tile[:], in0=ident_f32[:], scalar1=third[:, c, form : form + 1], scalar2=1.0,
+                        op0=ALU.mult, op1=ALU.mult,
                     )
                     diagonals[(c, form)] = tile
 
@@ -361,12 +362,13 @@ def tile_bsplinekanlayer_kernel(
             c, j = sum_of(n)
             for side, pair in (("left", (cube(c, j), up(c, j + 1))), ("right", (cube(c, j + 4), down(c, j + 3)))):
                 bank = psum.tile([P, BATCH], F32, tag="flip", bufs=8, name="sum")
-                for s in range(B_TILES):
-                    rows = slice(s * P, (s + 1) * P)
-                    for i, values in enumerate(pair):
+                for i, values in enumerate(pair):
+                    for s in range(B_TILES):
+                        rows = slice(s * P, (s + 1) * P)
                         nc.tensor.matmul(
                             out=bank[:, rows], lhsT=values[:, rows], rhs=ident_f32[:],
-                            start=(i == 0), stop=(i == 1), is_transpose=True,
+                            start=(i == 0 and s == 0), stop=(i == 1 and s == B_TILES - 1),
+                            is_transpose=True,
                         )
                 sum_banks[(c, j, side)] = bank
 
@@ -603,14 +605,18 @@ def tile_bsplinekanlayer_kernel(
         def ssw_plane(k, cols):
             return ssw_scales[4 * (k % 4) : P, k // 4, cols]
 
-        def quantise_ssw(c, part):
+        def quantise_ssw(c, part, half):
             n_cols = slice(part * N_TILE, (part + 1) * N_TILE)
-            for half in range(HALVES):
-                nc.vector.quantize_mx(
-                    out=ssw_codes[:, c * HALVES + half, n_cols].bitcast(FP8X4),
-                    scales=ssw_plane(c * HALVES + half, n_cols),
-                    in_=ssw_grouped[(c, part)][:, half].rearrange("p o t -> p (o t)"),
-                )
+            nc.vector.quantize_mx(
+                out=ssw_codes[:, c * HALVES + half, n_cols].bitcast(FP8X4),
+                scales=ssw_plane(c * HALVES + half, n_cols),
+                in_=ssw_grouped[(c, part)][:, half].rearrange("p o t -> p (o t)"),
+            )
+
+        def quantise_behind(k):
+            group, half = k // HALF_O - 1, k % HALF_O
+            if group >= 1 and half < HALVES:
+                quantise_ssw(group // 2, group % 2, half)
 
         w_tiles = {}
 
@@ -652,6 +658,7 @@ def tile_bsplinekanlayer_kernel(
                     finish.setdefault(ready + delay, []).append((kind, c, half))
 
         def run_step(n):
+            copy_sum(n - 1)
             if n >= 1 and n - 1 < STEPS:
                 take_sides(n - 1)
             if n + LOOKAHEAD < STEPS:
@@ -666,7 +673,6 @@ def tile_bsplinekanlayer_kernel(
                 elif kind == "from_back":
                     group_back(c, half)
             take_minimum(n - FORM_LAG - 2)
-            copy_sum(n - 1)
             bound_sum(n - 2)
             copy_outer(n - 1)
             copy_form(n - FORM_LAG - 2)
@@ -763,8 +769,8 @@ def tile_bsplinekanlayer_kernel(
                 add_sums(psum_flip, n)
                 turn_back(psum_flip, n)
                 run_step(n)
-                if n == 0:
-                    quantise_ssw(0, 0)
+                if n < HALVES:
+                    quantise_ssw(0, 0, n)
                 while scalers_flipped:
                     copy_pairs(*scalers_flipped.pop(0))
                 if n in (2, 4):
@@ -774,10 +780,10 @@ def tile_bsplinekanlayer_kernel(
                     quantise_silu((n - 5) // 4)
                 for k in range(chunks_done(n - 1), chunks_done(n)):
                     scale_chunk(k)
-                    if k % HALF_O == 0 and k > HALF_O:
-                        quantise_ssw((k - 1) // O_TILES, (k - 1) // HALF_O % 2)
-                if chunks_done(n - 2) < CHUNKS == chunks_done(n - 1):
-                    quantise_ssw(F_TILES - 1, 1)
+                    quantise_behind(k)
+                for half in range(HALVES):
+                    if chunks_done(n - 2 - half) < CHUNKS == chunks_done(n - 1 - half):
+                        quantise_ssw(F_TILES - 1, 1, half)
 
         with tc.psum_pool(name="psum_acc", bufs=1) as psum_acc:
             groups = [(s, n) for s in range(B_TILES) for n in range(N_TILES)]

@@ -47,7 +47,9 @@ EARLY_TILES = 6
 FORM_TILES = 6
 CHUNK_STEPS = 66
 RING = 7
-SWITCH = EARLY_TILES * N_KNOTS + 5
+EARLY_MULTIPLICATIONS = ((75, 0, 10), (76, 1, 10))
+SWITCH = EARLY_TILES * N_KNOTS + 6
+BASE_STEP = SWITCH
 STEPS = F_TILES * N_KNOTS
 
 
@@ -163,6 +165,7 @@ def tile_bsplinekanlayer_kernel(
         consts = ctx.enter_context(tc.tile_pool(name="consts", bufs=1))
         keep = ctx.enter_context(tc.tile_pool(name="keep", bufs=1))
         pool = ctx.enter_context(tc.tile_pool(name="work", bufs=1))
+        psum_flip = ctx.enter_context(tc.psum_pool(name="psum", bufs=8))
 
         knot_bf = consts.tile([P, F_TILES, N_KNOTS], BF16)
         nc.scalar.dma_start(out=knot_bf[:], in_=grid.rearrange("(c p) m -> p c m", p=P))
@@ -311,7 +314,7 @@ def tile_bsplinekanlayer_kernel(
                         out=up(c, m), in_=cube(c, m), func=ACT.Relu, scale=up_ratio[:, c, m - 1 : m]
                     )
             if needs_down(c, m):
-                if False:
+                if c < EARLY_TILES and m == 4:
                     nc.vector.tensor_scalar(out=down(c, m), in0=cube(c, m), scalar1=down_ratio[:, c, m - 3 : m - 2], scalar2=0.0, op0=ALU.mult, op1=ALU.max)
                 else:
                     nc.scalar.activation(
@@ -332,9 +335,8 @@ def tile_bsplinekanlayer_kernel(
             for form, term in terms_of(n):
                 if term == TERMS - 1:
                     tile = pool.tile([P, P], F32, tag="diagonal", bufs=4, name="diagonal")
-                    nc.gpsimd.tensor_scalar(
-                        out=tile[:], in0=ident_f32[:], scalar1=third[:, c, form : form + 1], scalar2=1.0,
-                        op0=ALU.mult, op1=ALU.mult,
+                    nc.scalar.activation(
+                        out=tile[:], in_=ident_f32[:], func=ACT.Copy, scale=third[:, c, form : form + 1]
                     )
                     diagonals[(c, form)] = tile
 
@@ -643,13 +645,53 @@ def tile_bsplinekanlayer_kernel(
             behind = max(0, n - 2) * (CHUNKS - HALF_O) // CHUNK_STEPS
             return min(CHUNKS, HALF_O + behind)
 
+        groups = [(s, n) for s in range(B_TILES) for n in range(N_TILES)]
+        acc = {}
+        multiplied = {}
+
+        def multiply(group, k):
+            s, n = group
+            if group not in acc:
+                acc[group] = psum_flip.tile([P, N_TILE], F32, tag="flip", bufs=8, name="acc")
+            k_codes, k_scales = codes[k]
+            nc.tensor.matmul_mx(
+                out=acc[group][:],
+                lhsT=k_codes[:, s * P : (s + 1) * P].bitcast(FP8X4),
+                lhsT_scale=k_scales[:, s * P : (s + 1) * P],
+                rhs=ssw_codes[:, k, n * N_TILE : (n + 1) * N_TILE].bitcast(FP8X4),
+                rhs_scale=ssw_plane(k, slice(n * N_TILE, (n + 1) * N_TILE)),
+                start=(k == 0),
+                stop=(k == SPLINE_PASSES - 1),
+            )
+            multiplied[group] = k + 1
+
+        def catch_up(group, most=SPLINE_PASSES):
+            for k in range(multiplied.get(group, 0), SPLINE_PASSES):
+                if k not in codes or most == 0:
+                    return
+                multiply(group, k)
+                most -= 1
+
+        def multiply_base(group):
+            s, n = group
+            for g in range(BASE_PASSES):
+                nc.tensor.matmul_mx(
+                    out=acc[group][:],
+                    lhsT=silu_codes[:, g, s * P : (s + 1) * P].bitcast(FP8X4),
+                    lhsT_scale=silu_scales[:, g, s * P : (s + 1) * P],
+                    rhs=w_tiles["codes"][:, g, n * N_TILE : (n + 1) * N_TILE].bitcast(FP8X4),
+                    rhs_scale=w_tiles["scales"][:, g, n * N_TILE : (n + 1) * N_TILE],
+                    start=False,
+                    stop=False,
+                )
+
         finish = {}
         for c in range(F_TILES):
             for half in range(HALVES):
                 ready = c * N_KNOTS + (7 if half == 0 else 11) + COMBINE_LAG
                 if summed(c, half):
                     ready = c * N_KNOTS + SUM_STEP + PACK - 1
-                    steps = (("back", 3), ("from_back", 4), ("quantise", 6))
+                    steps = (("back", 4), ("from_back", 5), ("quantise", 7))
                 elif c < F_TILES - 1 or half == 0:
                     steps = (("peak", 1), ("regroup", 2), ("quantise", 5))
                 else:
@@ -686,167 +728,138 @@ def tile_bsplinekanlayer_kernel(
                 if kind == "quantise":
                     quantise_half(c, half)
 
-        with tc.psum_pool(name="psum_flip", bufs=8) as psum_flip:
-            late_copies = []
-            scalers_flipped = []
-            for part in range(2):
-                flip_scaler(psum_flip, 0, part)
-            copy_pairs(0, 0)
-            take_roots()
-            nc.scalar.activation(out=warm[:], in_=warm[:], func=ACT.Silu)
-            load_scaler(2)
-            for pair in range(F_TILES // 2):
-                if pair == 1:
-                    copy_pairs(0, 1)
-                    for k in range(HALF_O):
-                        flip_chunk(psum_flip, k)
-                        scale_chunk(k)
-                flipped = psum_flip.tile([P, 2, BATCH], BF16, tag="flip", bufs=8)
-                for c in range(2):
-                    for s in range(B_TILES):
-                        nc.tensor.transpose(
-                            flipped[:, c, s * P : (s + 1) * P],
-                            x_rows[:, s, (2 * pair + c) * P : (2 * pair + c + 1) * P],
-                            ident_bf[:],
-                        )
-                if pair == 0:
-                    nc.vector.tensor_copy(out=x_of(0), in_=flipped[:, 0, :])
-                    for n in range(LOOKAHEAD):
-                        take_square(n)
-                    nc.vector.tensor_copy(out=x_of(1), in_=flipped[:, 1, :])
-                elif pair == 1:
-                    nc.vector.tensor_copy(out=x_pairs[pair][:], in_=flipped[:])
-                else:
-                    late_copies.append((pair, flipped))
-            remaining_constants()
-
-            silu_grouped = {}
-
-            def quantise_silu(g):
-                nc.vector.quantize_mx(
-                    out=silu_codes[:, g, :].bitcast(FP8X4), scales=silu_scales[:, g, :],
-                    in_=silu_grouped[g][:].rearrange("p b t -> p (b t)"),
-                )
-
-            def silu_piece(g, pair):
-                if pair == 0:
-                    silu_grouped[g] = pool.tile(
-                        [P, BATCH, PACK], BF16, tag="grouped", bufs=2, align_bytes=64, name="silu_grouped"
-                    )
-                words = psum_flip.tile([P, 2, 2, P], F32, tag="flip", bufs=8)
-                for u in range(2):
-                    for s in range(2):
-                        nc.tensor.transpose(
-                            words[:, u, s, :],
-                            x_rows[:, 2 * pair + s, :].bitcast(F32)[:, 256 * g + u : 256 * (g + 1) : 2],
-                            ident_f32[:],
-                        )
-                nc.scalar.activation(
-                    out=silu_grouped[g][:, 2 * pair * P : 2 * (pair + 1) * P, :].rearrange(
-                        "p b (u e) -> p b u e", e=2
-                    ),
-                    in_=words[:].bitcast(BF16).rearrange("p u s (b e) -> p (s b) u e", e=2),
-                    func=ACT.Silu,
-                )
-
-            for n in range(SWITCH):
-                if n % 2 == 1 and n < 8:
-                    silu_piece(n // 4, n // 2 % 2)
-                    if n == 7:
-                        load_next()
-                for k in range(chunks_done(n + 1), chunks_done(n + 2)):
+        late_copies = []
+        scalers_flipped = []
+        for part in range(2):
+            flip_scaler(psum_flip, 0, part)
+        copy_pairs(0, 0)
+        take_roots()
+        nc.scalar.activation(out=warm[:], in_=warm[:], func=ACT.Silu)
+        load_scaler(2)
+        for pair in range(F_TILES // 2):
+            if pair == 1:
+                copy_pairs(0, 1)
+                for k in range(HALF_O):
                     flip_chunk(psum_flip, k)
-                    c, s = divmod(k, O_TILES)
-                    if s == O_TILES - 1 and c + 1 < F_TILES:
-                        flip_scaler(psum_flip, c + 1, 0)
-                        scalers_flipped.append((c + 1, 0))
-                    elif s == HALF_O - 1 and c > 0:
-                        flip_scaler(psum_flip, c, 1)
-                        scalers_flipped.append((c, 1))
-                        if c + 2 < F_TILES:
-                            load_scaler(c + 2)
-                add_term(psum_flip, n - FORM_LAG)
-                add_sums(psum_flip, n)
-                turn_back(psum_flip, n)
-                run_step(n)
-                if n < HALVES:
-                    quantise_ssw(0, 0, n)
-                while scalers_flipped:
-                    copy_pairs(*scalers_flipped.pop(0))
-                if n in (2, 4):
-                    pair, flipped = late_copies.pop(0)
-                    nc.vector.tensor_copy(out=x_pairs[pair][:], in_=flipped[:])
-                if n in (5, 9):
-                    quantise_silu((n - 5) // 4)
-                for k in range(chunks_done(n - 1), chunks_done(n)):
                     scale_chunk(k)
-                    quantise_behind(k)
-                for half in range(HALVES):
-                    if chunks_done(n - 2 - half) < CHUNKS == chunks_done(n - 1 - half):
-                        quantise_ssw(F_TILES - 1, 1, half)
-
-        with tc.psum_pool(name="psum_acc", bufs=1) as psum_acc:
-            groups = [(s, n) for s in range(B_TILES) for n in range(N_TILES)]
-            acc = {}
-            for s, n in groups:
-                acc[(s, n)] = psum_acc.tile([P, N_TILE], F32, name="acc_%d_%d" % (s, n))
-
-            def multiply_base():
-                for s, n in groups:
-                    for g in range(BASE_PASSES):
-                        nc.tensor.matmul_mx(
-                            out=acc[(s, n)][:],
-                            lhsT=silu_codes[:, g, s * P : (s + 1) * P].bitcast(FP8X4),
-                            lhsT_scale=silu_scales[:, g, s * P : (s + 1) * P],
-                            rhs=w_tiles["codes"][:, g, n * N_TILE : (n + 1) * N_TILE].bitcast(FP8X4),
-                            rhs_scale=w_tiles["scales"][:, g, n * N_TILE : (n + 1) * N_TILE],
-                            start=False,
-                            stop=False,
-                        )
-
-            def multiply(k, of=groups):
-                k_codes, k_scales = codes[k]
-                for s, n in of:
-                    nc.tensor.matmul_mx(
-                        out=acc[(s, n)][:],
-                        lhsT=k_codes[:, s * P : (s + 1) * P].bitcast(FP8X4),
-                        lhsT_scale=k_scales[:, s * P : (s + 1) * P],
-                        rhs=ssw_codes[:, k, n * N_TILE : (n + 1) * N_TILE].bitcast(FP8X4),
-                        rhs_scale=ssw_plane(k, slice(n * N_TILE, (n + 1) * N_TILE)),
-                        start=(k == 0),
-                        stop=(k == SPLINE_PASSES - 1),
+            flipped = psum_flip.tile([P, 2, BATCH], BF16, tag="flip", bufs=8)
+            for c in range(2):
+                for s in range(B_TILES):
+                    nc.tensor.transpose(
+                        flipped[:, c, s * P : (s + 1) * P],
+                        x_rows[:, s, (2 * pair + c) * P : (2 * pair + c + 1) * P],
+                        ident_bf[:],
                     )
+            if pair == 0:
+                nc.vector.tensor_copy(out=x_of(0), in_=flipped[:, 0, :])
+                for n in range(LOOKAHEAD):
+                    take_square(n)
+                nc.vector.tensor_copy(out=x_of(1), in_=flipped[:, 1, :])
+            elif pair == 1:
+                nc.vector.tensor_copy(out=x_pairs[pair][:], in_=flipped[:])
+            else:
+                late_copies.append((pair, flipped))
+        remaining_constants()
 
-            multiplied = 0
-            for n in range(SWITCH, max(finish) + 1):
-                while multiplied in codes:
-                    multiply(multiplied)
-                    multiplied += 1
-                if n == SWITCH:
-                    multiply_base()
-                run_step(n)
-            last = (F_TILES - 1, HALVES - 1)
+        silu_grouped = {}
 
-            def rows_of(s):
-                return slice(s * P, (s + 1) * P)
+        def quantise_silu(g):
+            nc.vector.quantize_mx(
+                out=silu_codes[:, g, :].bitcast(FP8X4), scales=silu_scales[:, g, :],
+                in_=silu_grouped[g][:].rearrange("p b t -> p (b t)"),
+            )
 
-            def leave(s, n, copy):
-                if n == 0:
-                    result = pool.tile([P, N_TILE], F32, tag="slab", bufs=PREFETCH, align_bytes=64)
-                else:
-                    result = pool.tile([P, N_TILE], F32, tag="sides", bufs=3)
-                copy(out=result[:], in_=acc[(s, n)][:])
-                nc.sync.dma_start(out=out[rows_of(s), n * N_TILE : (n + 1) * N_TILE], in_=result[:])
+        def silu_piece(g, pair):
+            if pair == 0:
+                silu_grouped[g] = pool.tile(
+                    [P, BATCH, PACK], BF16, tag="grouped", bufs=2, align_bytes=64, name="silu_grouped"
+                )
+            words = psum_flip.tile([P, 2, 2, P], F32, tag="flip", bufs=8)
+            for u in range(2):
+                for s in range(2):
+                    nc.tensor.transpose(
+                        words[:, u, s, :],
+                        x_rows[:, 2 * pair + s, :].bitcast(F32)[:, 256 * g + u : 256 * (g + 1) : 2],
+                        ident_f32[:],
+                    )
+            nc.scalar.activation(
+                out=silu_grouped[g][:, 2 * pair * P : 2 * (pair + 1) * P, :].rearrange(
+                    "p b (u e) -> p b u e", e=2
+                ),
+                in_=words[:].bitcast(BF16).rearrange("p u s (b e) -> p (s b) u e", e=2),
+                func=ACT.Silu,
+            )
 
-            take_grouped_peak(last[0], last[1], rows_of(0))
-            for s in range(B_TILES):
-                if s + 1 < B_TILES:
-                    take_grouped_peak(last[0], last[1], rows_of(s + 1))
-                quantise_half(last[0], last[1], rows_of(s))
-                for k in range(multiplied, SPLINE_PASSES):
-                    multiply(k, [(s, n) for n in range(N_TILES)])
-                leave(s, 0, nc.scalar.copy)
-                if s < 2:
-                    leave(s, 1, nc.scalar.copy)
-            for s in range(2, B_TILES):
-                leave(s, 1, nc.vector.tensor_copy)
+        for n in range(SWITCH):
+            if n % 2 == 1 and n < 8:
+                silu_piece(n // 4, n // 2 % 2)
+                if n == 7:
+                    load_next()
+            for k in range(chunks_done(n + 1), chunks_done(n + 2)):
+                flip_chunk(psum_flip, k)
+                c, s = divmod(k, O_TILES)
+                if s == O_TILES - 1 and c + 1 < F_TILES:
+                    flip_scaler(psum_flip, c + 1, 0)
+                    scalers_flipped.append((c + 1, 0))
+                elif s == HALF_O - 1 and c > 0:
+                    flip_scaler(psum_flip, c, 1)
+                    scalers_flipped.append((c, 1))
+                    if c + 2 < F_TILES:
+                        load_scaler(c + 2)
+            add_term(psum_flip, n - FORM_LAG)
+            add_sums(psum_flip, n)
+            turn_back(psum_flip, n)
+            for at, group, most in EARLY_MULTIPLICATIONS:
+                if at == n:
+                    catch_up(groups[group], most)
+            run_step(n)
+            if n < HALVES:
+                quantise_ssw(0, 0, n)
+            while scalers_flipped:
+                copy_pairs(*scalers_flipped.pop(0))
+            if n in (2, 4):
+                pair, flipped = late_copies.pop(0)
+                nc.vector.tensor_copy(out=x_pairs[pair][:], in_=flipped[:])
+            if n in (5, 9):
+                quantise_silu((n - 5) // 4)
+            for k in range(chunks_done(n - 1), chunks_done(n)):
+                scale_chunk(k)
+                quantise_behind(k)
+            for half in range(HALVES):
+                if chunks_done(n - 2 - half) < CHUNKS == chunks_done(n - 1 - half):
+                    quantise_ssw(F_TILES - 1, 1, half)
+
+        for n in range(SWITCH, max(finish) + 1):
+            for group in groups:
+                catch_up(group)
+            if n == BASE_STEP:
+                for group in groups:
+                    multiply_base(group)
+            run_step(n)
+        last = (F_TILES - 1, HALVES - 1)
+
+        def rows_of(s):
+            return slice(s * P, (s + 1) * P)
+
+        def leave(s, n, copy):
+            if s == B_TILES - 1:
+                result = pool.tile([P, N_TILE], F32, tag="cubes", bufs=3)
+            elif n == 0:
+                result = pool.tile([P, N_TILE], F32, tag="slab", bufs=PREFETCH, align_bytes=64)
+            else:
+                result = pool.tile([P, N_TILE], F32, tag="sides", bufs=3)
+            copy(out=result[:], in_=acc[(s, n)][:])
+            nc.sync.dma_start(out=out[rows_of(s), n * N_TILE : (n + 1) * N_TILE], in_=result[:])
+
+        take_grouped_peak(last[0], last[1], rows_of(0))
+        for s in range(B_TILES):
+            if s + 1 < B_TILES:
+                take_grouped_peak(last[0], last[1], rows_of(s + 1))
+            quantise_half(last[0], last[1], rows_of(s))
+            for n in range(N_TILES):
+                catch_up((s, n))
+            leave(s, 0, nc.scalar.copy)
+            if s < 2:
+                leave(s, 1, nc.scalar.copy)
+        for s in range(2, B_TILES):
+            leave(s, 1, nc.vector.tensor_copy)

from contextlib import ExitStack

import concourse.mybir as mybir
from concourse.masks import make_identity

F32 = mybir.dt.float32
BF16 = mybir.dt.bfloat16
U32 = mybir.dt.uint32
U8 = mybir.dt.uint8
I32 = mybir.dt.int32
FP8X4 = mybir.dt.float8_e4m3fn_x4
ALU = mybir.AluOpType
ACT = mybir.ActivationFunctionType

P = 128
PACK = 4
BATCH = 512
N_IN = 1024
N_OUT = 1024
N_BASIS = 8
N_KNOTS = 12
HALVES = N_BASIS // PACK
B_TILES = BATCH // P
F_TILES = N_IN // P
O_TILES = N_OUT // P
BASE_PASSES = N_IN // (P * PACK)
SPLINE_PASSES = F_TILES * HALVES
N_TILE = 512
N_TILES = N_OUT // N_TILE

FLOPS = 2 * BATCH * N_OUT * (N_IN + N_IN * N_BASIS)


LOOKAHEAD = 3
COMBINE_LAG = 4
FORM_LAG = 3
TERMS = 3
END_KNOTS = (0, N_KNOTS - 1)
COPIED = ()
FORMS = ((0, 0, 4), (2, 2, 6), (3, 3, 7))
SUM_STEP = 9
PREFETCH = 3
HALF_O = O_TILES // 2
CHUNKS = F_TILES * O_TILES
FIRST_CHUNK_STEP = 3
EARLY_TILES = 6
FORM_TILES = 6
CHUNK_STEPS = 66
RING = 7
EARLY_MULTIPLICATIONS = ((75, 0, 10), (76, 1, 10))
SWITCH = EARLY_TILES * N_KNOTS + 6
BASE_STEP = SWITCH
STEPS = F_TILES * N_KNOTS


def spline_constants(nc, consts, scratch, knot_bf):
    used = [0]

    def temporary(count):
        first = used[0]
        used[0] = first + F_TILES * count
        return scratch[:, first : used[0]].rearrange("p (c m) -> p c m", c=F_TILES)

    def constant(name, count):
        return consts.tile([P, F_TILES, count], F32, name=name)

    knot = constant("knot", N_KNOTS)
    nc.vector.tensor_copy(out=knot[:], in_=knot_bf[:])

    spans = temporary(30)
    starts = {1: 0, 2: 11, 3: 21}
    for w, first in starts.items():
        count = N_KNOTS - w
        nc.vector.tensor_sub(
            out=spans[:, :, first : first + count], in0=knot[:, :, w:], in1=knot[:, :, :count]
        )
    inverses = temporary(30)
    nc.vector.reciprocal(out=inverses, in_=spans)
    h3 = spans[:, :, 21:30]
    r1, r2, r3 = inverses[:, :, 0:11], inverses[:, :, 11:21], inverses[:, :, 21:30]

    kappa = temporary(N_KNOTS)
    starting, ending = kappa[:, :, 0:8], kappa[:, :, 8:12]
    nc.vector.tensor_mul(out=starting, in0=r1[:, :, 0:8], in1=r2[:, :, 0:8])
    nc.vector.tensor_mul(out=ending, in0=r1[:, :, 7:11], in1=r2[:, :, 6:10])
    nc.vector.tensor_mul(out=starting, in0=starting, in1=r3[:, :, 0:8])
    nc.vector.tensor_mul(out=ending, in0=ending, in1=r3[:, :, 5:9])
    root = constant("root", N_KNOTS)
    root_shift = constant("root_shift", N_KNOTS)
    rough = temporary(N_KNOTS)
    h4 = temporary(N_BASIS)
    up_ratio = constant("up_ratio", N_BASIS)
    per_kappa = temporary(N_KNOTS)

    def take_roots():
        nc.scalar.activation(out=rough, in_=kappa, func=ACT.Sqrt)
        first_left = temporary(N_BASIS)
        nc.gpsimd.tensor_mul(out=first_left, in0=r1[:, :, 1:9], in1=r2[:, :, 1:9])
        nc.gpsimd.tensor_mul(out=first_left, in0=first_left, in1=r3[:, :, 1:9])
        nc.gpsimd.tensor_sub(out=h4, in0=knot[:, :, 4:], in1=knot[:, :, :N_BASIS])
        nc.vector.reciprocal(out=per_kappa, in_=kappa)
        nc.vector.reciprocal(out=root[:], in_=rough)
        nc.vector.scalar_tensor_tensor(
            out=root[:], in0=root[:], scalar=0.5, in1=kappa, op0=ALU.mult, op1=ALU.mult
        )
        nc.vector.scalar_tensor_tensor(
            out=root[:], in0=rough, scalar=0.5, in1=root[:], op0=ALU.mult, op1=ALU.add
        )
        nc.vector.scalar_tensor_tensor(
            out=root_shift[:], in0=root[:], scalar=-1.0, in1=knot[:], op0=ALU.mult, op1=ALU.mult
        )
        nc.gpsimd.tensor_mul(out=up_ratio[:], in0=h4, in1=r1[:, :, 0:8])
        nc.gpsimd.tensor_mul(out=up_ratio[:], in0=up_ratio[:], in1=first_left)
        nc.gpsimd.tensor_mul(out=up_ratio[:], in0=up_ratio[:], in1=per_kappa[:, :, 1:9])

    down_ratio = constant("down_ratio", N_BASIS)
    right_mix = constant("right_mix", PACK)
    third = constant("third", len(FORMS))

    def third_weight(at, j, second_span, third_span):
        weight = third[:, :, at : at + 1]
        other = temporary(1)
        nc.gpsimd.tensor_mul(out=weight, in0=h4[:, :, j : j + 1], in1=second_span)
        nc.gpsimd.tensor_mul(out=other, in0=third_span[0], in1=third_span[1])
        nc.gpsimd.tensor_mul(out=weight, in0=weight, in1=other)

    neg_knot = consts.tile([P, EARLY_TILES, PACK], F32, name="neg_knot")

    def flip_sign(values):
        nc.gpsimd.tensor_scalar(
            out=values, in0=values, scalar1=-1.0, scalar2=1.0, op0=ALU.mult, op1=ALU.mult
        )

    def rest():
        r4 = temporary(N_BASIS)
        nc.vector.reciprocal(out=r4, in_=h4)
        for at, j in ((0, 0), (1, 2), (2, 3)):
            third_weight(
                at, j, r2[:, :, j : j + 1], (h3[:, :, j + 2 : j + 3], r4[:, :, j + 1 : j + 2])
            )
        first_right = rough[:, :, 0:N_BASIS]
        nc.gpsimd.tensor_mul(out=first_right, in0=r3[:, :, 0:8], in1=r2[:, :, 1:9])
        nc.gpsimd.tensor_mul(out=first_right, in0=first_right, in1=r1[:, :, 2:10])
        nc.gpsimd.tensor_mul(out=down_ratio[:], in0=h4, in1=r1[:, :, 3:11])
        nc.gpsimd.tensor_mul(out=down_ratio[:], in0=down_ratio[:], in1=first_right)
        nc.gpsimd.tensor_mul(out=down_ratio[:], in0=down_ratio[:], in1=per_kappa[:, :, 3:11])
        nc.gpsimd.tensor_mul(out=right_mix[:], in0=first_right[:, :, 1:5], in1=per_kappa[:, :, 4:8])
        flip_sign(up_ratio[:, 0:EARLY_TILES, 3:7])
        flip_sign(down_ratio[:, 0:EARLY_TILES, 0:1])
        flip_sign(down_ratio[:, 0:EARLY_TILES, 5:8])
        flip_sign(down_ratio[:, EARLY_TILES:, :])
        flip_sign(right_mix[:, EARLY_TILES:, :])
        nc.gpsimd.tensor_copy(out=neg_knot[:], in_=knot[:, 0:EARLY_TILES, 4:8])
        flip_sign(neg_knot[:])

    return knot, neg_knot, root, root_shift, up_ratio, down_ratio, right_mix, third, take_roots, rest


def tile_bsplinekanlayer_kernel(
    tc, x, base_weight_words, base_weight_scales, spline_weight, spline_scaler, grid, out
):
    nc = tc.nc
    with ExitStack() as ctx:
        ctx.enter_context(tc.manual_schedule())
        consts = ctx.enter_context(tc.tile_pool(name="consts", bufs=1))
        keep = ctx.enter_context(tc.tile_pool(name="keep", bufs=1))
        pool = ctx.enter_context(tc.tile_pool(name="work", bufs=1))
        psum_flip = ctx.enter_context(tc.psum_pool(name="psum", bufs=8))

        knot_bf = consts.tile([P, F_TILES, N_KNOTS], BF16)
        nc.scalar.dma_start(out=knot_bf[:], in_=grid.rearrange("(c p) m -> p c m", p=P))
        scaler_rows = {}

        def load_scaler(c):
            rows = pool.tile([P, O_TILES, P], BF16, tag="scaler_rows", bufs=2, align_bytes=64)
            nc.sync.dma_start(
                out=rows[:],
                in_=spline_scaler[:, c * P : (c + 1) * P].rearrange("(s p) i -> p s i", p=P),
            )
            scaler_rows[c] = rows

        slabs = {}

        def load_slab(c, part):
            slab = pool.tile([P, HALF_O, P * N_BASIS], BF16, tag="slab", bufs=PREFETCH, align_bytes=64)
            rows = spline_weight[:, c * P : (c + 1) * P, :].rearrange("(s p) i j -> p s (i j)", p=P)
            nc.sync.dma_start(out=slab[:], in_=rows[:, part * HALF_O : (part + 1) * HALF_O, :])
            slabs[(c, part)] = slab

        def load_next():
            following = len(slabs)
            if following < 2 * F_TILES:
                load_slab(following // 2, following % 2)
            elif not w_tiles:
                load_w()

        x_rows = pool.tile([P, B_TILES, N_IN], BF16, tag="slab", bufs=PREFETCH, align_bytes=64)
        x_in = x.rearrange("(s p) i -> p s i", p=P)
        load_scaler(0)
        nc.sync.dma_start(out=x_rows[:, :, : 2 * P], in_=x_in[:, :, : 2 * P])
        load_slab(0, 0)
        nc.sync.dma_start(out=x_rows[:, :, 2 * P :], in_=x_in[:, :, 2 * P :])
        load_slab(0, 1)
        load_slab(1, 0)
        load_scaler(1)

        warm = consts.tile([P, 1], F32)
        nc.vector.memset(warm[:], 0.0)
        nc.scalar.activation(out=warm[:], in_=warm[:], func=ACT.Sqrt)
        ident_bf = consts.tile([P, P], BF16)
        make_identity(nc, ident_bf[:])
        ident_f32 = consts.tile([P, P], F32)
        make_identity(nc, ident_f32[:])

        minus_ident = consts.tile([P, P], F32)
        nc.gpsimd.tensor_scalar(
            out=minus_ident[:], in0=ident_f32[:], scalar1=-1.0, scalar2=1.0, op0=ALU.mult, op1=ALU.mult
        )

        scratch = pool.tile([P, 1024], F32, tag="grouped", bufs=2, align_bytes=64)
        (
            knot, neg_knot, root, root_shift, up_ratio, down_ratio, right_mix, third, take_roots,
            remaining_constants,
        ) = spline_constants(nc, consts, scratch, knot_bf)


        x_pairs = []
        for q in range(F_TILES // 2):
            x_pair = pool.tile([P, 2, BATCH], BF16, tag="x_pair", bufs=4, align_bytes=64)
            x_pairs.append(x_pair)

        def x_of(c):
            return x_pairs[c // 2][:, c % 2, :]

        silu_codes = keep.tile([P, BASE_PASSES, BATCH], U32, align_bytes=64)
        silu_scales = keep.tile([P, BASE_PASSES, BATCH], U8, align_bytes=64)
        ssw_codes = keep.tile([P, SPLINE_PASSES, N_OUT], U32, align_bytes=64)
        ssw_scales = keep.tile([P, SPLINE_PASSES // 4, N_OUT], U8, align_bytes=64)

        def forms_of(c):
            return range(len(FORMS)) if 0 <= c < FORM_TILES else ()

        def summed(c, half):
            return 0 <= c < EARLY_TILES and half == 1

        def three_term(c, j):
            return any(FORMS[form][0] == j for form in forms_of(c))

        def terms_of(n):
            c, m = divmod(n, N_KNOTS)
            return [(form, m - FORMS[form][1]) for form in forms_of(c) if 0 <= m - FORMS[form][1] < TERMS]

        def needs_up(c, m):
            if 1 <= m <= N_BASIS and not three_term(c, m - 1):
                return True
            return any(m - FORMS[form][1] in (1, 2) for form in forms_of(c))

        def needs_down(c, m):
            return 0 <= m - 3 < N_BASIS and not three_term(c, m - 3)

        neg_x = {}
        square = {}
        cubes = {}
        ups = {}
        downs = {}
        left = {}
        right = {}
        grouped = {}
        codes = {}

        def part_of(store, c, first, m, tag):
            key = (c, (m - first) // 4)
            if key not in store:
                store[key] = pool.tile([P, 4, BATCH], F32, tag=tag, bufs=3, name=tag)
            return store[key][:, (m - first) % 4, :]

        def cube(c, m):
            return part_of(cubes, c, 0, m, "cubes")

        def up(c, m):
            return part_of(ups, c, 1, m, "sides")

        def down(c, m):
            return part_of(downs, c, 3, m, "sides")

        def take_square(n):
            c, m = divmod(n, N_KNOTS)
            square[n] = pool.tile([P, BATCH], F32, tag="square", bufs=4, name="square")
            nc.scalar.activation(
                out=square[n][:], in_=x_of(c), func=ACT.Square,
                scale=root[:, c, m : m + 1], bias=root_shift[:, c, m : m + 1],
            )

        def take_cube(n):
            c, m = divmod(n, N_KNOTS)
            if c < EARLY_TILES and m // PACK == 1:
                values, at = neg_x[c][:], neg_knot[:, c, m - PACK : m - PACK + 1]
            else:
                values, at = x_of(c), knot[:, c, m : m + 1]
            nc.vector.scalar_tensor_tensor(
                out=cube(c, m), in0=values, scalar=at, in1=square[n][:], op0=ALU.subtract, op1=ALU.mult
            )
            if c < EARLY_TILES and m == PACK - 2:
                neg_x[c] = pool.tile([P, BATCH], BF16, tag="neg_x", bufs=1, name="neg_x")
                nc.vector.tensor_scalar_mul(out=neg_x[c][:], in0=x_of(c), scalar1=-1.0)

        def take_sides(n):
            c, m = divmod(n, N_KNOTS)
            if needs_up(c, m):
                if c >= EARLY_TILES and m == 3:
                    nc.vector.tensor_scalar(out=up(c, m), in0=cube(c, m), scalar1=up_ratio[:, c, m - 1 : m], scalar2=0.0, op0=ALU.mult, op1=ALU.max)
                else:
                    nc.scalar.activation(
                        out=up(c, m), in_=cube(c, m), func=ACT.Relu, scale=up_ratio[:, c, m - 1 : m]
                    )
            if needs_down(c, m):
                if c < EARLY_TILES and m == 4:
                    nc.vector.tensor_scalar(out=down(c, m), in0=cube(c, m), scalar1=down_ratio[:, c, m - 3 : m - 2], scalar2=0.0, op0=ALU.mult, op1=ALU.max)
                else:
                    nc.scalar.activation(
                        out=down(c, m), in_=cube(c, m), func=ACT.Relu, scale=down_ratio[:, c, m - 3 : m - 2]
                    )

        def half_tile(store, c, j, tag):
            key = (c, j // PACK)
            if key not in store:
                store[key] = pool.tile([P, PACK, BATCH], BF16, tag=tag, bufs=3 if tag == "left" else 2, name=tag)
            return store[key][:, j % PACK, :]

        form_banks = {}
        diagonals = {}

        def take_diagonal(n):
            c = n // N_KNOTS
            for form, term in terms_of(n):
                if term == TERMS - 1:
                    tile = pool.tile([P, P], F32, tag="diagonal", bufs=4, name="diagonal")
                    nc.scalar.activation(
                        out=tile[:], in_=ident_f32[:], func=ACT.Copy, scale=third[:, c, form : form + 1]
                    )
                    diagonals[(c, form)] = tile

        def add_term(psum, n):
            c, m = divmod(n, N_KNOTS)
            for form, term in terms_of(n):
                if term == 0:
                    form_banks[(c, form)] = psum.tile([P, BATCH], F32, tag="flip", bufs=8, name="form")
                weight = (ident_f32, minus_ident, diagonals.get((c, form)))[term]
                nc.tensor.matmul(
                    out=form_banks[(c, form)][:], lhsT=weight[:], rhs=cube(c, m) if term == 0 else up(c, m),
                    start=(term == 0), stop=(term == TERMS - 1),
                )

        sum_banks = {}
        back_banks = {}

        def sum_of(n):
            c, t = divmod(n - SUM_STEP, N_KNOTS)
            return (c, PACK + t) if summed(c, 1) and t < PACK else None

        def add_sums(psum, n):
            if sum_of(n) is None:
                return
            c, j = sum_of(n)
            for side, pair in (("left", (cube(c, j), up(c, j + 1))), ("right", (cube(c, j + 4), down(c, j + 3)))):
                bank = psum.tile([P, BATCH], F32, tag="flip", bufs=8, name="sum")
                for i, values in enumerate(pair):
                    for s in range(B_TILES):
                        rows = slice(s * P, (s + 1) * P)
                        nc.tensor.matmul(
                            out=bank[:, rows], lhsT=values[:, rows], rhs=ident_f32[:],
                            start=(i == 0 and s == 0), stop=(i == 1 and s == B_TILES - 1),
                            is_transpose=True,
                        )
                sum_banks[(c, j, side)] = bank

        def copy_sum(n):
            if sum_of(n) is not None:
                c, j = sum_of(n)
                nc.scalar.copy(out=half_tile(left, c, j, "left"), in_=sum_banks[(c, j, "left")][:])

        def bound_sum(n):
            if sum_of(n) is not None:
                c, j = sum_of(n)
                to = half_tile(left, c, j, "left")
                nc.vector.tensor_tensor(out=to, in0=sum_banks[(c, j, "right")][:], in1=to, op=ALU.min)

        def turn_back(psum, n):
            for kind, c, half in finish.get(n, []):
                if kind == "back":
                    for part in range(2):
                        bank = psum.tile([P, PACK, BATCH // 2], BF16, tag="flip", bufs=8, name="back")
                        for t in range(PACK):
                            for s in range(2):
                                nc.tensor.transpose(
                                    bank[:, t, s * P : (s + 1) * P],
                                    left[(c, half)][:, t, (2 * part + s) * P : (2 * part + s + 1) * P],
                                    ident_bf[:],
                                )
                        back_banks[(c, part)] = bank

        def copied(c, form):
            return c >= 1 and form in COPIED

        def copy_form(n):
            c = n // N_KNOTS
            for form, term in terms_of(n):
                if term == TERMS - 1 and copied(c, form):
                    nc.scalar.copy(
                        out=half_tile(left, c, FORMS[form][0], "left"), in_=form_banks[(c, form)][:]
                    )

        def copy_outer(n):
            c, m = divmod(n, N_KNOTS)
            for form in forms_of(c):
                if copied(c, form) and FORMS[form][2] == m:
                    nc.scalar.activation(
                        out=half_tile(right, c, FORMS[form][0], "right"), in_=cube(c, m),
                        func=ACT.Relu, scale=right_mix[:, c, m - 4 : m - 3],
                    )

        def take_minimum(n):
            c = n // N_KNOTS
            for form, term in terms_of(n):
                if term == TERMS - 1 and not copied(c, form):
                    j, first_knot, outer_knot = FORMS[form]
                    nc.vector.scalar_tensor_tensor(
                        out=half_tile(left, c, j, "left"), in0=cube(c, outer_knot),
                        scalar=right_mix[:, c, j : j + 1], in1=form_banks[(c, form)][:],
                        op0=ALU.mult, op1=ALU.min,
                    )

        def negative(c, half):
            return c < F_TILES - 1 and half == 1

        def runs_of(c, half):
            runs = []
            for j in range(half * PACK, (half + 1) * PACK):
                if three_term(c, j) or summed(c, half):
                    continue
                if runs and runs[-1][1] == j:
                    runs[-1] = (runs[-1][0], j + 1)
                else:
                    runs.append((j, j + 1))
            return runs

        def combine(n, fours):
            c, m = divmod(n, N_KNOTS)
            for half in range(HALVES):
                for first, end in runs_of(c, half):
                    if (end - first == PACK) != fours:
                        continue
                    planes = slice(first - half * PACK, end - half * PACK)
                    if m == end:
                        half_tile(left, c, first, "left")
                        a, b = cubes[(c, half)], ups[(c, half)]
                        if negative(c, half):
                            a, b = b, a
                        nc.vector.tensor_tensor(
                            out=left[(c, half)][:, planes, :], in0=a[:, planes, :], in1=b[:, planes, :],
                            op=ALU.subtract,
                        )
                    if half == 1 and m == end + 3:
                        half_tile(right, c, first, "right")
                        to, a, b = (t[:, planes, :] for t in (right[(c, 1)], cubes[(c, 2)], downs[(c, 1)]))
                        if negative(c, half):
                            nc.vector.tensor_tensor(out=to, in0=a, in1=b, op=ALU.add)
                        else:
                            nc.vector.scalar_tensor_tensor(
                                out=to, in0=a, scalar=-1.0, in1=b, op0=ALU.mult, op1=ALU.subtract
                            )

        def combine_right(n):
            c, m = divmod(n, N_KNOTS)
            j = m - 4
            if 0 <= j < PACK and not three_term(c, j):
                nc.vector.scalar_tensor_tensor(
                    out=half_tile(right, c, j, "right"), in0=cube(c, m), scalar=right_mix[:, c, j : j + 1],
                    in1=down(c, m - 1), op0=ALU.mult, op1=ALU.subtract,
                )

        def take_peak(c, half):
            rest = [t for t in range(PACK) if not three_term(c, half * PACK + t)]
            parts = [(slice(rest[0], rest[-1] + 1), ALU.min if negative(c, half) else ALU.max)] if rest else []
            if False:
                parts.append((slice(0, PACK, PACK - 1), ALU.min))
            for planes, op in parts:
                nc.vector.tensor_tensor(
                    out=left[(c, half)][:, planes, :], in0=left[(c, half)][:, planes, :],
                    in1=right[(c, half)][:, planes, :], op=op,
                )

        def regroup(c, half):
            grouped[(c, half)] = pool.tile(
                [P, BATCH, PACK], BF16, tag="grouped", bufs=2, align_bytes=64, name="grouped"
            )
            to = grouped[(c, half)][:].rearrange("p (g i) t -> p g t i", i=4)
            of = left[(c, half)][:].rearrange("p t (g i) -> p g t i", i=4)
            nc.scalar.activation(out=to, in_=of, func=ACT.Relu, scale=-1.0 if negative(c, half) else 1.0)

        def group_back(c, half):
            grouped[(c, half)] = pool.tile(
                [P, BATCH, PACK], BF16, tag="grouped", bufs=2, align_bytes=64, name="grouped"
            )
            for part in range(2):
                nc.scalar.activation(
                    out=grouped[(c, half)][:, part * BATCH // 2 : (part + 1) * BATCH // 2, :].rearrange(
                        "p (g i) t -> p g t i", i=4
                    ),
                    in_=back_banks[(c, part)][:].rearrange("p t (g i) -> p g t i", i=4),
                    func=ACT.Relu, scale=-1.0,
                )

        def take_grouped_peak(c, half, cols):
            if (c, half) not in grouped:
                grouped[(c, half)] = pool.tile(
                    [P, BATCH, PACK], BF16, tag="grouped", bufs=2, align_bytes=64, name="grouped"
                )
            nc.vector.scalar_tensor_tensor(
                out=grouped[(c, half)][:, cols, :],
                in0=left[(c, half)][:, :, cols].rearrange("p t b -> p b t"),
                scalar=0.0,
                in1=right[(c, half)][:, :, cols].rearrange("p t b -> p b t"),
                op0=ALU.max,
                op1=ALU.max,
            )

        parked = {}

        def code_tiles(k):
            if RING + 2 <= k < EARLY_TILES * HALVES:
                if not parked:
                    parked["codes"] = pool.tile(
                        [P, 3, BATCH], U32, tag="slab", bufs=PREFETCH, align_bytes=64, name="parked"
                    )
                    parked["scales"] = pool.tile(
                        [P, 3, BATCH], U8, tag="pairs", bufs=2, align_bytes=64, name="parked_scales"
                    )
                at = k - RING - 2
                return parked["codes"][:, at, :], parked["scales"][:, at, :]
            if RING <= k < RING + 2:
                k_codes = pool.tile([P, BATCH], U32, tag="x_pair", bufs=4, align_bytes=64, name="k_codes_x")
            else:
                k_codes = pool.tile([P, BATCH], U32, tag="k_codes", bufs=RING, align_bytes=64, name="k_codes")
            k_scales = pool.tile([P, BATCH], U8, tag="k_scales", bufs=RING + 2, align_bytes=64, name="k_scales")
            return k_codes[:], k_scales[:]

        def quantise_half(c, half, cols=slice(0, BATCH)):
            k = c * HALVES + half
            if k not in codes:
                codes[k] = code_tiles(k)
            nc.vector.quantize_mx(
                out=codes[k][0][:, cols].bitcast(FP8X4), scales=codes[k][1][:, cols],
                in_=grouped[(c, half)][:, cols, :].rearrange("p b t -> p (b t)"),
            )

        pairs = {}
        chunk_words = {}
        ssw_grouped = {}

        scaler_banks = {}

        def flip_scaler(psum_flip, c, part):
            bank = psum_flip.tile([P, N_TILE], BF16, tag="flip", bufs=8, name="bank")
            for s in range(HALF_O):
                nc.tensor.transpose(
                    bank[:, s * P : (s + 1) * P], scaler_rows[c][:, part * HALF_O + s, :], ident_bf[:]
                )
            scaler_banks[(c, part)] = bank

        def copy_pairs(c, part):
            bank = scaler_banks.pop((c, part))
            pairs[(c, part)] = pool.tile([P, N_TILE, 2], BF16, tag="pairs", bufs=2, align_bytes=64, name="pairs")
            nc.scalar.copy(
                out=pairs[(c, part)][:], in_=bank[:].unsqueeze(2).to_broadcast([P, N_TILE, 2])
            )

        def flip_chunk(psum_flip, k):
            c, s = divmod(k, O_TILES)
            part, r = divmod(s, HALF_O)
            slab_words = slabs[(c, part)][:, r, :].bitcast(F32)
            words = psum_flip.tile([P, PACK, P], F32, tag="flip", bufs=8, name="words")
            for w in range(PACK):
                nc.tensor.transpose(
                    words[:, w, :], slab_words[:, w : PACK * P : PACK], ident_f32[:]
                )
            chunk_words[k] = words
            if r == HALF_O - 1:
                load_next()

        def scale_chunk(k):
            c, s = divmod(k, O_TILES)
            part, r = divmod(s, HALF_O)
            if r == 0:
                ssw_grouped[(c, part)] = pool.tile(
                    [P, HALVES, N_TILE, PACK], BF16, tag="ssw_grouped", bufs=2, align_bytes=64,
                    name="ssw_grouped",
                )
            o_cols = slice(r * P, (r + 1) * P)
            nc.vector.tensor_tensor(
                out=ssw_grouped[(c, part)][:, :, o_cols, :].rearrange("p h o t -> p o h t"),
                in0=chunk_words[k][:].bitcast(BF16).rearrange("p w (o e) -> p o w e", e=2),
                in1=pairs[(c, part)][:, o_cols, :].unsqueeze(2).to_broadcast([P, P, PACK, 2]),
                op=ALU.mult,
            )

        def ssw_plane(k, cols):
            return ssw_scales[4 * (k % 4) : P, k // 4, cols]

        def quantise_ssw(c, part, half):
            n_cols = slice(part * N_TILE, (part + 1) * N_TILE)
            nc.vector.quantize_mx(
                out=ssw_codes[:, c * HALVES + half, n_cols].bitcast(FP8X4),
                scales=ssw_plane(c * HALVES + half, n_cols),
                in_=ssw_grouped[(c, part)][:, half].rearrange("p o t -> p (o t)"),
            )

        def quantise_behind(k):
            group, half = k // HALF_O - 1, k % HALF_O
            if group >= 1 and half < HALVES:
                quantise_ssw(group // 2, group % 2, half)

        w_tiles = {}

        def load_w():
            w_codes = pool.tile([P, BASE_PASSES, N_OUT], U32, tag="slab", bufs=PREFETCH, align_bytes=64)
            w_scales = pool.tile([P, BASE_PASSES, N_OUT], U8, tag="scaler_rows", bufs=2, align_bytes=64)
            nc.gpsimd.memset(w_scales[:].bitcast(I32), 0)
            for quadrant in range(4):
                nc.sync.dma_start(
                    out=w_scales[32 * quadrant : 32 * quadrant + 4, :, :].bitcast(I32),
                    in_=base_weight_scales[:, 4 * quadrant : 4 * quadrant + 4, :]
                    .rearrange("g r n -> r g n")
                    .bitcast(I32),
                )
            for g in range(BASE_PASSES):
                nc.sync.dma_start(
                    out=w_codes[:, g, :].bitcast(I32),
                    in_=base_weight_words[g].rearrange("p n t -> p (n t)").bitcast(I32),
                )
            w_tiles["codes"] = w_codes
            w_tiles["scales"] = w_scales

        def chunks_done(n):
            behind = max(0, n - 2) * (CHUNKS - HALF_O) // CHUNK_STEPS
            return min(CHUNKS, HALF_O + behind)

        groups = [(s, n) for s in range(B_TILES) for n in range(N_TILES)]
        acc = {}
        multiplied = {}

        def multiply(group, k):
            s, n = group
            if group not in acc:
                acc[group] = psum_flip.tile([P, N_TILE], F32, tag="flip", bufs=8, name="acc")
            k_codes, k_scales = codes[k]
            nc.tensor.matmul_mx(
                out=acc[group][:],
                lhsT=k_codes[:, s * P : (s + 1) * P].bitcast(FP8X4),
                lhsT_scale=k_scales[:, s * P : (s + 1) * P],
                rhs=ssw_codes[:, k, n * N_TILE : (n + 1) * N_TILE].bitcast(FP8X4),
                rhs_scale=ssw_plane(k, slice(n * N_TILE, (n + 1) * N_TILE)),
                start=(k == 0),
                stop=(k == SPLINE_PASSES - 1),
            )
            multiplied[group] = k + 1

        def catch_up(group, most=SPLINE_PASSES):
            for k in range(multiplied.get(group, 0), SPLINE_PASSES):
                if k not in codes or most == 0:
                    return
                multiply(group, k)
                most -= 1

        def multiply_base(group):
            s, n = group
            for g in range(BASE_PASSES):
                nc.tensor.matmul_mx(
                    out=acc[group][:],
                    lhsT=silu_codes[:, g, s * P : (s + 1) * P].bitcast(FP8X4),
                    lhsT_scale=silu_scales[:, g, s * P : (s + 1) * P],
                    rhs=w_tiles["codes"][:, g, n * N_TILE : (n + 1) * N_TILE].bitcast(FP8X4),
                    rhs_scale=w_tiles["scales"][:, g, n * N_TILE : (n + 1) * N_TILE],
                    start=False,
                    stop=False,
                )

        finish = {}
        for c in range(F_TILES):
            for half in range(HALVES):
                ready = c * N_KNOTS + (7 if half == 0 else 11) + COMBINE_LAG
                if summed(c, half):
                    ready = c * N_KNOTS + SUM_STEP + PACK - 1
                    steps = (("back", 4), ("from_back", 5), ("quantise", 7))
                elif c < F_TILES - 1 or half == 0:
                    steps = (("peak", 1), ("regroup", 2), ("quantise", 5))
                else:
                    steps = (("last", 1),)
                for kind, delay in steps:
                    finish.setdefault(ready + delay, []).append((kind, c, half))

        def run_step(n):
            copy_sum(n - 1)
            if n >= 1 and n - 1 < STEPS:
                take_sides(n - 1)
            if n + LOOKAHEAD < STEPS:
                take_square(n + LOOKAHEAD)
            if n < STEPS:
                take_cube(n)
            for kind, c, half in finish.get(n, []):
                if kind == "peak":
                    take_peak(c, half)
                elif kind == "regroup":
                    regroup(c, half)
                elif kind == "from_back":
                    group_back(c, half)
            take_minimum(n - FORM_LAG - 2)
            bound_sum(n - 2)
            copy_outer(n - 1)
            copy_form(n - FORM_LAG - 2)
            take_diagonal(n - 1)
            if 0 <= n - COMBINE_LAG + 1 < STEPS:
                combine(n - COMBINE_LAG + 1, True)
            if 0 <= n - COMBINE_LAG < STEPS:
                combine(n - COMBINE_LAG, False)
                combine_right(n - COMBINE_LAG)
            for kind, c, half in finish.get(n, []):
                if kind == "quantise":
                    quantise_half(c, half)

        late_copies = []
        scalers_flipped = []
        for part in range(2):
            flip_scaler(psum_flip, 0, part)
        copy_pairs(0, 0)
        take_roots()
        nc.scalar.activation(out=warm[:], in_=warm[:], func=ACT.Silu)
        load_scaler(2)
        for pair in range(F_TILES // 2):
            if pair == 1:
                copy_pairs(0, 1)
                for k in range(HALF_O):
                    flip_chunk(psum_flip, k)
                    scale_chunk(k)
            flipped = psum_flip.tile([P, 2, BATCH], BF16, tag="flip", bufs=8)
            for c in range(2):
                for s in range(B_TILES):
                    nc.tensor.transpose(
                        flipped[:, c, s * P : (s + 1) * P],
                        x_rows[:, s, (2 * pair + c) * P : (2 * pair + c + 1) * P],
                        ident_bf[:],
                    )
            if pair == 0:
                nc.vector.tensor_copy(out=x_of(0), in_=flipped[:, 0, :])
                for n in range(LOOKAHEAD):
                    take_square(n)
                nc.vector.tensor_copy(out=x_of(1), in_=flipped[:, 1, :])
            elif pair == 1:
                nc.vector.tensor_copy(out=x_pairs[pair][:], in_=flipped[:])
            else:
                late_copies.append((pair, flipped))
        remaining_constants()

        silu_grouped = {}

        def quantise_silu(g):
            nc.vector.quantize_mx(
                out=silu_codes[:, g, :].bitcast(FP8X4), scales=silu_scales[:, g, :],
                in_=silu_grouped[g][:].rearrange("p b t -> p (b t)"),
            )

        def silu_piece(g, pair):
            if pair == 0:
                silu_grouped[g] = pool.tile(
                    [P, BATCH, PACK], BF16, tag="grouped", bufs=2, align_bytes=64, name="silu_grouped"
                )
            words = psum_flip.tile([P, 2, 2, P], F32, tag="flip", bufs=8)
            for u in range(2):
                for s in range(2):
                    nc.tensor.transpose(
                        words[:, u, s, :],
                        x_rows[:, 2 * pair + s, :].bitcast(F32)[:, 256 * g + u : 256 * (g + 1) : 2],
                        ident_f32[:],
                    )
            nc.scalar.activation(
                out=silu_grouped[g][:, 2 * pair * P : 2 * (pair + 1) * P, :].rearrange(
                    "p b (u e) -> p b u e", e=2
                ),
                in_=words[:].bitcast(BF16).rearrange("p u s (b e) -> p (s b) u e", e=2),
                func=ACT.Silu,
            )

        for n in range(SWITCH):
            if n % 2 == 1 and n < 8:
                silu_piece(n // 4, n // 2 % 2)
                if n == 7:
                    load_next()
            for k in range(chunks_done(n + 1), chunks_done(n + 2)):
                flip_chunk(psum_flip, k)
                c, s = divmod(k, O_TILES)
                if s == O_TILES - 1 and c + 1 < F_TILES:
                    flip_scaler(psum_flip, c + 1, 0)
                    scalers_flipped.append((c + 1, 0))
                elif s == HALF_O - 1 and c > 0:
                    flip_scaler(psum_flip, c, 1)
                    scalers_flipped.append((c, 1))
                    if c + 2 < F_TILES:
                        load_scaler(c + 2)
            add_term(psum_flip, n - FORM_LAG)
            add_sums(psum_flip, n)
            turn_back(psum_flip, n)
            for at, group, most in EARLY_MULTIPLICATIONS:
                if at == n:
                    catch_up(groups[group], most)
            run_step(n)
            if n < HALVES:
                quantise_ssw(0, 0, n)
            while scalers_flipped:
                copy_pairs(*scalers_flipped.pop(0))
            if n in (2, 4):
                pair, flipped = late_copies.pop(0)
                nc.vector.tensor_copy(out=x_pairs[pair][:], in_=flipped[:])
            if n in (5, 9):
                quantise_silu((n - 5) // 4)
            for k in range(chunks_done(n - 1), chunks_done(n)):
                scale_chunk(k)
                quantise_behind(k)
            for half in range(HALVES):
                if chunks_done(n - 2 - half) < CHUNKS == chunks_done(n - 1 - half):
                    quantise_ssw(F_TILES - 1, 1, half)

        for n in range(SWITCH, max(finish) + 1):
            for group in groups:
                catch_up(group)
            if n == BASE_STEP:
                for group in groups:
                    multiply_base(group)
            run_step(n)
        last = (F_TILES - 1, HALVES - 1)

        def rows_of(s):
            return slice(s * P, (s + 1) * P)

        def leave(s, n, copy):
            if s == B_TILES - 1:
                result = pool.tile([P, N_TILE], F32, tag="cubes", bufs=3)
            elif n == 0:
                result = pool.tile([P, N_TILE], F32, tag="slab", bufs=PREFETCH, align_bytes=64)
            else:
                result = pool.tile([P, N_TILE], F32, tag="sides", bufs=3)
            copy(out=result[:], in_=acc[(s, n)][:])
            nc.sync.dma_start(out=out[rows_of(s), n * N_TILE : (n + 1) * N_TILE], in_=result[:])

        take_grouped_peak(last[0], last[1], rows_of(0))
        for s in range(B_TILES):
            if s + 1 < B_TILES:
                take_grouped_peak(last[0], last[1], rows_of(s + 1))
            quantise_half(last[0], last[1], rows_of(s))
            for n in range(N_TILES):
                catch_up((s, n))
            leave(s, 0, nc.scalar.copy)
            if s < 2:
                leave(s, 1, nc.scalar.copy)
        for s in range(2, B_TILES):
            leave(s, 1, nc.vector.tensor_copy)
